import numpy as np
import ml_dtypes


def mxq(x, axis, fmt="e4m3"):
    dtype, down = {"e4m3": (ml_dtypes.float8_e4m3fn, 7), "e5m2": (ml_dtypes.float8_e5m2, 14)}[fmt]
    v = np.moveaxis(np.asarray(x, np.float32).astype(ml_dtypes.bfloat16).astype(np.float64), axis, -1)
    blocks = v.reshape(v.shape[:-1] + (-1, 32))
    amax = np.abs(blocks).max(-1, keepdims=True)
    byte = np.maximum(np.where(amax > 0, np.frexp(amax)[1] - 1 + 127, 0) - down, 1)
    scale = np.exp2(byte - 127.0)
    codes = (blocks / scale).astype(np.float32).astype(dtype).astype(np.float64)
    return np.moveaxis((codes * scale).reshape(v.shape), -1, axis)


WIDE = False


def mx_kscale(k):
    if not WIDE:
        return np.ones(k)
    levels = np.array([10, -10, 5, -5, 0])
    if k % 512:
        return np.exp2(np.random.permutation(np.resize(levels, k // 32))).repeat(32)
    a = np.empty((k // 512, 16))
    for p in range(k // 512):
        a[p, :8] = np.random.permutation(np.resize(levels, 8))
        for g in range(8):
            far = levels[np.abs(levels - a[p, g]) >= 10]
            a[p, g + 8] = far[np.random.randint(len(far))]
    return np.exp2(a.ravel()).repeat(32)


BF16 = ml_dtypes.bfloat16


def bf(x):
    return np.asarray(x, np.float32).astype(BF16)


def f64(x):
    return np.asarray(x).astype(np.float64)


B, S, D, E = 2, 1024, 1024, 1024


def draw0():
    s, t = mx_kscale(S), mx_kscale(D)
    return {"q": bf(np.random.standard_normal((B, S, D)) / t),
            "k": bf(np.random.standard_normal((B, S, D)) * s[:, None] * t),
            "v": bf(np.random.standard_normal((B, S, E)) / s[:, None])}


def core(q, k, v):
    scale = 1.0 / np.sqrt(q.shape[1])
    qn = f64(q) * scale
    kn = f64(k) * scale
    kv_mat = mxq(kn, 1, "e4m3").transpose(0, 2, 1) @ mxq(f64(v), 1, "e4m3")
    out = mxq(qn, 2, "e4m3") @ mxq(kv_mat, 1, "e4m3")
    return out


def e4m3fn_bytes(y):
    return np.clip(np.asarray(y, np.float64), -448.0, 448.0).astype(np.float32).astype(ml_dtypes.float8_e4m3fn).view(np.uint8)


def e4m3fn_values(b):
    return np.asarray(b, np.uint8).view(ml_dtypes.float8_e4m3fn).astype(np.float64)


def setup_inputs():
    d = draw0()
    x0 = np.asarray(d['v']).astype(np.float64)
    s = (np.max(np.abs(x0), axis=(0, 2), keepdims=True) / 448.0).astype(np.float32)
    out = {}
    for k, v in d.items():
        if k == 'v':
            out['v_bytes'] = e4m3fn_bytes(x0 / s.astype(np.float64))
            out['v_scale'] = s
        else:
            out[k] = v
    return out


def reference(q, k, v_bytes, v_scale):
    return core(q, k, e4m3fn_values(v_bytes) * v_scale.astype(np.float64))

@@ -1,0 +1,219 @@
+from contextlib import ExitStack
+
+import concourse.mybir as mybir
+from concourse.masks import make_identity
+
+B, S, D, E = 2, 1024, 1024, 1024
+FLOPS = 2 * B * (D * S * E + S * D * E)
+
+F32 = mybir.dt.float32
+BF16 = mybir.dt.bfloat16
+U32 = mybir.dt.uint32
+U8 = mybir.dt.uint8
+FP8 = mybir.dt.float8_e4m3fn
+FP8X4 = mybir.dt.float8_e4m3fn_x4
+COPY = mybir.ActivationFunctionType.Copy
+MULT = mybir.AluOpType.mult
+
+P = 128
+PACK = 4
+HALF = 512
+INV = 1.0 / 32.0
+
+
+def tile_efficientattention_kernel(tc, q, k, v_bytes, v_scale, out):
+    nc = tc.nc
+    with ExitStack() as ctx:
+        keep = ctx.enter_context(tc.tile_pool(name="keep", bufs=1))
+        raw = ctx.enter_context(tc.tile_pool(name="raw", bufs=4))
+        work = ctx.enter_context(tc.tile_pool(name="work", bufs=3))
+        psum = ctx.enter_context(tc.psum_pool(name="psum", bufs=8))
+        ctx.enter_context(tc.manual_schedule())
+
+        scl = keep.tile([P, 2, PACK], F32, name="scl")
+        nc.scalar.dma_start(out=scl[:], in_=v_scale.rearrange("o (g p j) x -> p (o g) (j x)", p=P, j=PACK))
+        ident = keep.tile([P, P], F32, name="ident")
+        make_identity(nc, ident[:])
+        warm = keep.tile([P, 1], F32, name="warm")
+        nc.vector.memset(warm[:], 0.0)
+        nc.scalar.activation(out=warm[:], in_=warm[:], func=COPY, scale=1.0)
+
+        kc = [keep.tile([P, 2, D], U32, name=f"kc{b}", align_bytes=64) for b in range(B)]
+        ks = [keep.tile([P, 2, D], U8, name=f"ks{b}", align_bytes=64) for b in range(B)]
+        vc = [keep.tile([P, 2, E], U32, name=f"vc{b}", align_bytes=64) for b in range(B)]
+        vs = [keep.tile([P, 2, E], U8, name=f"vs{b}", align_bytes=64) for b in range(B)]
+        qc = [keep.tile([P, 2, S], U32, name=f"qc{b}", align_bytes=64) for b in range(B)]
+        qs = [keep.tile([P, 2, S], U8, name=f"qs{b}", align_bytes=64) for b in range(B)]
+        mc = [keep.tile([P, 2, E], U32, name=f"mc{b}", align_bytes=64) for b in range(B)]
+        ms = [keep.tile([P, 2, E], U8, name=f"ms{b}", align_bytes=64) for b in range(B)]
+
+        k_raw, v_raw, q_raw = {}, {}, {}
+        v_wide, k_grp, v_grp, q_grp, m_grp, xt, acc, res = {}, {}, {}, {}, {}, {}, {}, {}
+
+        def load_k(b, g):
+            t = raw.tile([P, PACK, D], BF16, name="k_raw", bufs=3)
+            nc.sync.dma_start(out=t[:], in_=k[b].rearrange("(g p j) d -> g p j d", p=P, j=PACK)[g])
+            k_raw[b, g] = t
+
+        def load_v(b, g):
+            t = raw.tile([P, PACK, E], U8, name="v_raw", bufs=2)
+            nc.sync.dma_start(out=t[:], in_=v_bytes[b].rearrange("(g p j) e -> g p j e", p=P, j=PACK)[g])
+            v_raw[b, g] = t
+
+        def load_q(b, a):
+            t = raw.tile([P, 4, D], BF16, name="q_raw", bufs=3)
+            nc.sync.dma_start(out=t[:], in_=q[b].rearrange("(p r) d -> p r d", r=8)[:, 4 * a:4 * a + 4, :])
+            q_raw[b, a] = t
+
+        def k_interleave(b, G, g):
+            t = work.tile([P, HALF * PACK], BF16, name="k_grp", align_bytes=64)
+            nc.vector.tensor_scalar(
+                out=t[:].rearrange("p (t m j) -> p m j t", t=PACK, j=PACK),
+                in0=k_raw[b, g][:, :, G * HALF:(G + 1) * HALF].rearrange("p j (m t) -> p m j t", t=PACK),
+                scalar1=INV, scalar2=None, op0=MULT)
+            k_grp[b, G, g] = t
+
+        def k_quant(b, G, g):
+            c = slice(G * HALF, (G + 1) * HALF)
+            nc.vector.quantize_mx(out=kc[b][:, g, c].bitcast(FP8X4), scales=ks[b][:, g, c], in_=k_grp[b, G, g][:])
+
+        def v_widen(b, h, g, eng):
+            t = work.tile([P, PACK, HALF], BF16, name="v_wide", bufs=3)
+            for j in range(PACK):
+                src = v_raw[b, g][:, j, h * HALF:(h + 1) * HALF].bitcast(FP8)
+                if eng == "S":
+                    nc.scalar.activation(out=t[:, j, :], in_=src, func=COPY, scale=scl[:, g, j:j + 1])
+                else:
+                    nc.vector.tensor_scalar(out=t[:, j, :], in0=src, scalar1=scl[:, g, j:j + 1], scalar2=None, op0=MULT)
+            v_wide[b, h, g] = t
+
+        def v_interleave(b, h, g):
+            t = work.tile([P, HALF * PACK], BF16, name="v_grp", align_bytes=64)
+            nc.vector.tensor_copy(out=t[:].rearrange("p (c i j) -> p c j i", i=4, j=PACK), in_=v_wide[b, h, g][:].rearrange("p j (c i) -> p c j i", i=4))
+            v_grp[b, h, g] = t
+
+        def v_quant(b, h, g):
+            c = slice(h * HALF, (h + 1) * HALF)
+            nc.vector.quantize_mx(out=vc[b][:, g, c].bitcast(FP8X4), scales=vs[b][:, g, c], in_=v_grp[b, h, g][:])
+
+        def q_transpose(b, G, i):
+            x = psum.tile([P, 2, 2, P], F32, name="bank")
+            for r in range(2):
+                row = 2 * i + r
+                words = q_raw[b, row // 4][:, row % 4, :].bitcast(F32)
+                for u in range(2):
+                    nc.tensor.transpose(x[:, r, u, :], words[:, 256 * G + u:256 * (G + 1):2], ident[:])
+            xt[b, G, i] = x
+
+        def q_copy(b, G, i, eng):
+            if i == 0:
+                q_grp[b, G] = work.tile([P, S * PACK], BF16, name="q_grp", align_bytes=64, bufs=4)
+            dst = q_grp[b, G][:, i * 1024:(i + 1) * 1024].bitcast(F32).rearrange("p (r n u) -> p r n u", r=2, u=2)
+            src = xt[b, G, i][:].rearrange("p r u n -> p r n u")
+            if eng == "S":
+                nc.scalar.copy(out=dst, in_=src)
+            else:
+                nc.vector.tensor_copy(out=dst, in_=src)
+
+        def q_quant(b, G):
+            nc.vector.quantize_mx(out=qc[b][:, G, :].bitcast(FP8X4), scales=qs[b][:, G, :], in_=q_grp[b, G][:])
+
+        def kv_matmul(b, h, G, e4):
+            x = psum.tile([P, PACK, P], F32, name="bank")
+            c = slice(h * HALF + e4 * P, h * HALF + (e4 + 1) * P)
+            for t in range(PACK):
+                m = slice(G * HALF + t * P, G * HALF + (t + 1) * P)
+                for g in range(2):
+                    nc.tensor.matmul_mx(out=x[:, t, :], lhsT=kc[b][:, g, m].bitcast(FP8X4), lhsT_scale=ks[b][:, g, m],
+                                        rhs=vc[b][:, g, c].bitcast(FP8X4), rhs_scale=vs[b][:, g, c], start=(g == 0), stop=(g == 1))
+            acc[b, h, G, e4] = x
+
+        def kv_copy(b, h, G, e4, eng):
+            if e4 == 0:
+                m_grp[b, h, G] = work.tile([P, HALF * PACK], BF16, name="m_grp", align_bytes=64, bufs=5)
+            dst = m_grp[b, h, G][:, e4 * 512:(e4 + 1) * 512].rearrange("p (n t) -> p n t", t=PACK)
+            src = acc[b, h, G, e4][:].rearrange("p t n -> p n t")
+            if eng == "S":
+                nc.scalar.copy(out=dst, in_=src)
+            else:
+                nc.vector.tensor_copy(out=dst, in_=src)
+
+        def kv_quant(b, h, G):
+            c = slice(h * HALF, (h + 1) * HALF)
+            nc.vector.quantize_mx(out=mc[b][:, G, c].bitcast(FP8X4), scales=ms[b][:, G, c], in_=m_grp[b, h, G][:])
+
+        def out_matmul(b, h, r):
+            x = psum.tile([P, HALF], F32, name="bank")
+            m, c = slice(r * P, (r + 1) * P), slice(h * HALF, (h + 1) * HALF)
+            for G in range(2):
+                nc.tensor.matmul_mx(out=x[:], lhsT=qc[b][:, G, m].bitcast(FP8X4), lhsT_scale=qs[b][:, G, m],
+                                    rhs=mc[b][:, G, c].bitcast(FP8X4), rhs_scale=ms[b][:, G, c], start=(G == 0), stop=(G == 1))
+            acc[b, h, r] = x
+
+        def out_copy(b, h, r, eng):
+            t = work.tile([P, HALF], F32, name="res", bufs=6)
+            if eng == "S":
+                nc.scalar.activation(out=t[:], in_=acc[b, h, r][:], func=COPY, scale=INV)
+            else:
+                nc.vector.tensor_scalar(out=t[:], in0=acc[b, h, r][:], scalar1=INV, scalar2=None, op0=MULT)
+            nc.sync.dma_start(out=out[b].rearrange("(p r) e -> p r e", r=8)[:, r, h * HALF:(h + 1) * HALF], in_=t[:])
+
+        steps = (
+            "lv00 lv01 lk00 lq00 lq01 lk01 TR00 W000:V W010:S TR01 lv10 lq10 "
+            "lq11 lk10 W001:S VI000 VI010 W011:S lv11 QC00:S KI000 VQ010 VQ000 VI001 "
+            "KQ000 VI011 QC01:S KI001 W100:S VQ001 KQ001 S1000 VQ011 KI011 S1010 KC000:S "
+            "TR10 KI010 lk11 W110:V VI100 KQ011 KC010:S QC10:S KQ010 KI100 W101:S S1011 "
+            "VQ100 KQ100 KI101 QQ00 VI101 KC011:S KQ101 S1001 TR11 VQ101 MQ011 KC001:S "
+            "QQ01 MQ010 KI110 KI111 S1100 KQ110 KQ111 MQ001 QC11:S MQ000 KC100:S W111:V "
+            "S2010 OC010:S S2011 VI110 VI111 VQ110 VQ111 OC011:S QQ10 S1101 KC101:S S2000 "
+            "OC000:S QQ11 MQ100 MQ101 S2001 OC001:S S1111 S2100 KC111:A S1110 OC100:S S2101 "
+            "OC101:S KC110:V MQ111 MQ110 S2110 S2111 OC110:S OC111:A "
+        )
+        for item in steps.split(" "):
+            if item == "":
+                continue
+            name = item.split(":")[0]
+            eng = item.split(":")[1] if ":" in item else ""
+            op = name[0:2] if name[0] != "W" else "W"
+            a = [int(c) for c in name[len(op):]]
+            es = [eng] * 4 if eng != "A" else ["S", "V", "S", "V"]
+            if eng == "B":
+                es = ["V", "S", "V", "S"]
+            if op == "lk":
+                load_k(*a)
+            elif op == "lv":
+                load_v(*a)
+            elif op == "lq":
+                load_q(*a)
+            elif op == "KI":
+                k_interleave(*a)
+            elif op == "KQ":
+                k_quant(*a)
+            elif op == "W":
+                v_widen(*a, eng)
+            elif op == "VI":
+                v_interleave(*a)
+            elif op == "VQ":
+                v_quant(*a)
+            elif op == "QQ":
+                q_quant(*a)
+            elif op == "MQ":
+                kv_quant(*a)
+            elif op == "TR":
+                for i in range(4):
+                    q_transpose(a[0], a[1], i)
+            elif op == "QC":
+                for i in range(4):
+                    q_copy(a[0], a[1], i, es[i])
+            elif op == "S1":
+                for i in range(4):
+                    kv_matmul(a[0], a[1], a[2], i)
+            elif op == "KC":
+                for i in range(4):
+                    kv_copy(a[0], a[1], a[2], i, es[i])
+            elif op == "S2":
+                for i in range(4):
+                    out_matmul(a[0], a[1], 4 * a[2] + i)
+            elif op == "OC":
+                for i in range(4):
+                    out_copy(a[0], a[1], 4 * a[2] + i, es[i])

@@ -18,6 +18,7 @@ MULT = mybir.AluOpType.mult
 P = 128
 PACK = 4
 HALF = 512
+QUARTER = 256
 INV = 1.0 / 32.0
 
 
@@ -25,8 +26,9 @@ def tile_efficientattention_kernel(tc, q, k, v_bytes, v_scale, out):
     nc = tc.nc
     with ExitStack() as ctx:
         keep = ctx.enter_context(tc.tile_pool(name="keep", bufs=1))
-        raw = ctx.enter_context(tc.tile_pool(name="raw", bufs=4))
+        raw = ctx.enter_context(tc.tile_pool(name="raw", bufs=1))
         work = ctx.enter_context(tc.tile_pool(name="work", bufs=3))
+        mx = ctx.enter_context(tc.tile_pool(name="mx", bufs=8))
         psum = ctx.enter_context(tc.psum_pool(name="psum", bufs=8))
         ctx.enter_context(tc.manual_schedule())
 
@@ -34,186 +36,289 @@ def tile_efficientattention_kernel(tc, q, k, v_bytes, v_scale, out):
         nc.scalar.dma_start(out=scl[:], in_=v_scale.rearrange("o (g p j) x -> p (o g) (j x)", p=P, j=PACK))
         ident = keep.tile([P, P], F32, name="ident")
         make_identity(nc, ident[:])
-        warm = keep.tile([P, 1], F32, name="warm")
-        nc.vector.memset(warm[:], 0.0)
-        nc.scalar.activation(out=warm[:], in_=warm[:], func=COPY, scale=1.0)
-
-        kc = [keep.tile([P, 2, D], U32, name=f"kc{b}", align_bytes=64) for b in range(B)]
-        ks = [keep.tile([P, 2, D], U8, name=f"ks{b}", align_bytes=64) for b in range(B)]
-        vc = [keep.tile([P, 2, E], U32, name=f"vc{b}", align_bytes=64) for b in range(B)]
-        vs = [keep.tile([P, 2, E], U8, name=f"vs{b}", align_bytes=64) for b in range(B)]
-        qc = [keep.tile([P, 2, S], U32, name=f"qc{b}", align_bytes=64) for b in range(B)]
-        qs = [keep.tile([P, 2, S], U8, name=f"qs{b}", align_bytes=64) for b in range(B)]
-        mc = [keep.tile([P, 2, E], U32, name=f"mc{b}", align_bytes=64) for b in range(B)]
-        ms = [keep.tile([P, 2, E], U8, name=f"ms{b}", align_bytes=64) for b in range(B)]
 
         k_raw, v_raw, q_raw = {}, {}, {}
-        v_wide, k_grp, v_grp, q_grp, m_grp, xt, acc, res = {}, {}, {}, {}, {}, {}, {}, {}
+        v_wide, grouped, codes, bank, res = {}, {}, {}, {}, {}
+
+        def load_k_half(b, G, g):
+            t = raw.tile([P, PACK, HALF], BF16, name="k_half", bufs=4)
+            nc.sync.dma_start(out=t[:], in_=k[b].rearrange("(g p j) d -> g p j d", p=P, j=PACK)[g][:, :, G * HALF:(G + 1) * HALF])
+            k_raw[b, G, g] = t[:]
 
         def load_k(b, g):
-            t = raw.tile([P, PACK, D], BF16, name="k_raw", bufs=3)
+            t = raw.tile([P, PACK, D], BF16, name="k_full", bufs=2)
             nc.sync.dma_start(out=t[:], in_=k[b].rearrange("(g p j) d -> g p j d", p=P, j=PACK)[g])
-            k_raw[b, g] = t
+            for G in range(2):
+                k_raw[b, G, g] = t[:, :, G * HALF:(G + 1) * HALF]
 
         def load_v(b, g):
-            t = raw.tile([P, PACK, E], U8, name="v_raw", bufs=2)
+            t = raw.tile([P, PACK, E], U8, name="v_raw", bufs=4)
             nc.sync.dma_start(out=t[:], in_=v_bytes[b].rearrange("(g p j) e -> g p j e", p=P, j=PACK)[g])
             v_raw[b, g] = t
 
-        def load_q(b, a):
-            t = raw.tile([P, 4, D], BF16, name="q_raw", bufs=3)
-            nc.sync.dma_start(out=t[:], in_=q[b].rearrange("(p r) d -> p r d", r=8)[:, 4 * a:4 * a + 4, :])
-            q_raw[b, a] = t
+        def load_q(b, i):
+            t = raw.tile([P, 2, D], BF16, name="q_raw", bufs=6)
+            nc.sync.dma_start(out=t[:], in_=q[b].rearrange("(p r) d -> p r d", r=8)[:, 2 * i:2 * i + 2, :])
+            q_raw[b, i] = t
+
+        live = {"k": 8, "v": 6, "q": 8, "m": 5}
+
+        def quantise(key):
+            c = mx.tile([P, HALF], U32, name="codes_" + key[0], align_bytes=64, bufs=live[key[0]])
+            s = mx.tile([P, HALF], U8, name="scales_" + key[0], align_bytes=64, bufs=live[key[0]])
+            nc.vector.quantize_mx(out=c[:].bitcast(FP8X4), scales=s[:], in_=grouped[key][:])
+            codes[key] = (c, s)
 
         def k_interleave(b, G, g):
-            t = work.tile([P, HALF * PACK], BF16, name="k_grp", align_bytes=64)
+            t = work.tile([P, HALF * PACK], BF16, name="k_grp", align_bytes=64, bufs=2)
             nc.vector.tensor_scalar(
                 out=t[:].rearrange("p (t m j) -> p m j t", t=PACK, j=PACK),
-                in0=k_raw[b, g][:, :, G * HALF:(G + 1) * HALF].rearrange("p j (m t) -> p m j t", t=PACK),
+                in0=k_raw[b, G, g].rearrange("p j (m t) -> p m j t", t=PACK),
                 scalar1=INV, scalar2=None, op0=MULT)
-            k_grp[b, G, g] = t
+            grouped["k", b, G, g] = t
 
-        def k_quant(b, G, g):
-            c = slice(G * HALF, (G + 1) * HALF)
-            nc.vector.quantize_mx(out=kc[b][:, g, c].bitcast(FP8X4), scales=ks[b][:, g, c], in_=k_grp[b, G, g][:])
+        def widen(dst, src, g, j, on_scalar):
+            if on_scalar:
+                nc.scalar.activation(out=dst, in_=src.bitcast(FP8), func=COPY, scale=scl[:, g, j:j + 1])
+            else:
+                nc.vector.tensor_scalar(out=dst, in0=src.bitcast(FP8), scalar1=scl[:, g, j:j + 1], scalar2=None, op0=MULT)
 
-        def v_widen(b, h, g, eng):
-            t = work.tile([P, PACK, HALF], BF16, name="v_wide", bufs=3)
-            for j in range(PACK):
-                src = v_raw[b, g][:, j, h * HALF:(h + 1) * HALF].bitcast(FP8)
-                if eng == "S":
-                    nc.scalar.activation(out=t[:, j, :], in_=src, func=COPY, scale=scl[:, g, j:j + 1])
-                else:
-                    nc.vector.tensor_scalar(out=t[:, j, :], in0=src, scalar1=scl[:, g, j:j + 1], scalar2=None, op0=MULT)
-            v_wide[b, h, g] = t
+        def v_widen(b, h, g, on_scalar, rows=range(PACK)):
+            if (b, h, g) not in v_wide:
+                v_wide[b, h, g] = work.tile([P, PACK, HALF], BF16, name="v_wide", bufs=4)
+            for j in rows:
+                widen(v_wide[b, h, g][:, j, :], v_raw[b, g][:, j, h * HALF:(h + 1) * HALF], g, j, on_scalar)
+
+        def v_widen_quarter(c):
+            t = work.tile([P, 2, PACK, QUARTER], BF16, name="v_wide", bufs=4)
+            for g in range(2):
+                for j in range(PACK):
+                    widen(t[:, g, j, :], v_raw[1, g][:, j, c * QUARTER:(c + 1) * QUARTER], g, j, False)
+            v_wide[1, c] = t
+
+        def v_interleave_quarter(c):
+            t = work.tile([P, HALF * PACK], BF16, name="v_grp", align_bytes=64, bufs=2)
+            nc.vector.tensor_copy(out=t[:].rearrange("p (g c i j) -> p g c j i", g=2, i=4, j=PACK),
+                                  in_=v_wide[1, c][:].rearrange("p g j (c i) -> p g c j i", i=4))
+            grouped["v", 1, c] = t
 
         def v_interleave(b, h, g):
-            t = work.tile([P, HALF * PACK], BF16, name="v_grp", align_bytes=64)
-            nc.vector.tensor_copy(out=t[:].rearrange("p (c i j) -> p c j i", i=4, j=PACK), in_=v_wide[b, h, g][:].rearrange("p j (c i) -> p c j i", i=4))
-            v_grp[b, h, g] = t
+            t = work.tile([P, HALF * PACK], BF16, name="v_grp", align_bytes=64, bufs=2)
+            nc.vector.tensor_copy(out=t[:].rearrange("p (c i j) -> p c j i", i=4, j=PACK),
+                                  in_=v_wide[b, h, g][:].rearrange("p j (c i) -> p c j i", i=4))
+            grouped["v", b, h, g] = t
 
-        def v_quant(b, h, g):
-            c = slice(h * HALF, (h + 1) * HALF)
-            nc.vector.quantize_mx(out=vc[b][:, g, c].bitcast(FP8X4), scales=vs[b][:, g, c], in_=v_grp[b, h, g][:])
-
-        def q_transpose(b, G, i):
-            x = psum.tile([P, 2, 2, P], F32, name="bank")
-            for r in range(2):
-                row = 2 * i + r
-                words = q_raw[b, row // 4][:, row % 4, :].bitcast(F32)
-                for u in range(2):
-                    nc.tensor.transpose(x[:, r, u, :], words[:, 256 * G + u:256 * (G + 1):2], ident[:])
-            xt[b, G, i] = x
-
-        def q_copy(b, G, i, eng):
-            if i == 0:
-                q_grp[b, G] = work.tile([P, S * PACK], BF16, name="q_grp", align_bytes=64, bufs=4)
-            dst = q_grp[b, G][:, i * 1024:(i + 1) * 1024].bitcast(F32).rearrange("p (r n u) -> p r n u", r=2, u=2)
-            src = xt[b, G, i][:].rearrange("p r u n -> p r n u")
-            if eng == "S":
+        def evacuate(dst, src, on_scalar):
+            if on_scalar:
                 nc.scalar.copy(out=dst, in_=src)
             else:
                 nc.vector.tensor_copy(out=dst, in_=src)
 
-        def q_quant(b, G):
-            nc.vector.quantize_mx(out=qc[b][:, G, :].bitcast(FP8X4), scales=qs[b][:, G, :], in_=q_grp[b, G][:])
-
-        def kv_matmul(b, h, G, e4):
-            x = psum.tile([P, PACK, P], F32, name="bank")
-            c = slice(h * HALF + e4 * P, h * HALF + (e4 + 1) * P)
-            for t in range(PACK):
-                m = slice(G * HALF + t * P, G * HALF + (t + 1) * P)
-                for g in range(2):
-                    nc.tensor.matmul_mx(out=x[:, t, :], lhsT=kc[b][:, g, m].bitcast(FP8X4), lhsT_scale=ks[b][:, g, m],
-                                        rhs=vc[b][:, g, c].bitcast(FP8X4), rhs_scale=vs[b][:, g, c], start=(g == 0), stop=(g == 1))
-            acc[b, h, G, e4] = x
-
-        def kv_copy(b, h, G, e4, eng):
-            if e4 == 0:
-                m_grp[b, h, G] = work.tile([P, HALF * PACK], BF16, name="m_grp", align_bytes=64, bufs=5)
-            dst = m_grp[b, h, G][:, e4 * 512:(e4 + 1) * 512].rearrange("p (n t) -> p n t", t=PACK)
-            src = acc[b, h, G, e4][:].rearrange("p t n -> p n t")
-            if eng == "S":
-                nc.scalar.copy(out=dst, in_=src)
-            else:
-                nc.vector.tensor_copy(out=dst, in_=src)
-
-        def kv_quant(b, h, G):
-            c = slice(h * HALF, (h + 1) * HALF)
-            nc.vector.quantize_mx(out=mc[b][:, G, c].bitcast(FP8X4), scales=ms[b][:, G, c], in_=m_grp[b, h, G][:])
-
-        def out_matmul(b, h, r):
-            x = psum.tile([P, HALF], F32, name="bank")
-            m, c = slice(r * P, (r + 1) * P), slice(h * HALF, (h + 1) * HALF)
+        def q_transpose(b, i):
             for G in range(2):
-                nc.tensor.matmul_mx(out=x[:], lhsT=qc[b][:, G, m].bitcast(FP8X4), lhsT_scale=qs[b][:, G, m],
-                                    rhs=mc[b][:, G, c].bitcast(FP8X4), rhs_scale=ms[b][:, G, c], start=(G == 0), stop=(G == 1))
-            acc[b, h, r] = x
+                x = psum.tile([P, 2, 2, P], F32, name="bank")
+                for r in range(2):
+                    words = q_raw[b, i][:, r, :].bitcast(F32)
+                    for u in range(2):
+                        nc.tensor.transpose(x[:, r, u, :], words[:, 256 * G + u:256 * (G + 1):2], ident[:])
+                bank["q", b, i, G] = x
 
-        def out_copy(b, h, r, eng):
-            t = work.tile([P, HALF], F32, name="res", bufs=6)
-            if eng == "S":
-                nc.scalar.activation(out=t[:], in_=acc[b, h, r][:], func=COPY, scale=INV)
+        def q_out(b, i, on_scalar=(True, True)):
+            t = work.tile([P, HALF * PACK], BF16, name="q_grp", align_bytes=64, bufs=4)
+            for G in range(2):
+                dst = t[:, G * 1024:(G + 1) * 1024].bitcast(F32).rearrange("p (r n u) -> p r n u", r=2, u=2)
+                evacuate(dst, bank["q", b, i, G][:].rearrange("p r u n -> p r n u"), on_scalar[G])
+            grouped["q", b, i] = t
+
+        def kv_matmul(b, G, c, passes=(0, 1)):
+            if passes[0] == 0:
+                bank["m", b, G, c] = psum.tile([P, PACK, P], F32, name="bank")
+            x = bank["m", b, G, c]
+            for g in passes:
+                kc, ks = codes["k", b, G, g]
+                (vc, vs), at = (codes["v", 0, c // 4, g], c % 4) if b == 0 else (codes["v", 1, c // 2], 2 * g + c % 2)
+                cols = slice(at * P, (at + 1) * P)
+                for t in range(PACK):
+                    m = slice(t * P, (t + 1) * P)
+                    nc.tensor.matmul_mx(out=x[:, t, :], lhsT=kc[:, m].bitcast(FP8X4), lhsT_scale=ks[:, m],
+                                        rhs=vc[:, cols].bitcast(FP8X4), rhs_scale=vs[:, cols],
+                                        start=(g == 0 and t == 0), stop=(g == 1 and t == PACK - 1))
+
+        def kv_out(b, G, c, on_scalar=True):
+            key, at = (("m", b, G, c // 4), c % 4) if b == 0 else (("m", b, c // 2), 2 * G + c % 2)
+            if key not in grouped:
+                grouped[key] = work.tile([P, HALF * PACK], BF16, name="m_grp", align_bytes=64, bufs=4)
+            dst = grouped[key][:, at * HALF:(at + 1) * HALF].rearrange("p (n t) -> p n t", t=PACK)
+            evacuate(dst, bank["m", b, G, c][:].rearrange("p t n -> p n t"), on_scalar)
+
+        def out_matmul0(h, r):
+            x = psum.tile([P, HALF], F32, name="bank")
+            qc, qs = codes["q", 0, r // 2]
+            for G in range(2):
+                m = slice(G * QUARTER + (r % 2) * P, G * QUARTER + (r % 2 + 1) * P)
+                mc, ms = codes["m", 0, G, h]
+                nc.tensor.matmul_mx(out=x[:], lhsT=qc[:, m].bitcast(FP8X4), lhsT_scale=qs[:, m],
+                                    rhs=mc[:].bitcast(FP8X4), rhs_scale=ms[:], start=(G == 0), stop=(G == 1))
+            bank["o", 0, h, r] = x
+
+        def out_matmul1(c, i):
+            x = psum.tile([P, 2, QUARTER], F32, name="bank")
+            qc, qs = codes["q", 1, i]
+            mc, ms = codes["m", 1, c]
+            for r in range(2):
+                for G in range(2):
+                    m = slice(G * QUARTER + r * P, G * QUARTER + (r + 1) * P)
+                    n = slice(G * QUARTER, (G + 1) * QUARTER)
+                    nc.tensor.matmul_mx(out=x[:, r, :], lhsT=qc[:, m].bitcast(FP8X4), lhsT_scale=qs[:, m],
+                                        rhs=mc[:, n].bitcast(FP8X4), rhs_scale=ms[:, n], start=(G == 0), stop=(G == 1))
+            bank["o", 1, c, i] = x
+
+        def scaled_out(dst, src, on_scalar):
+            if on_scalar:
+                nc.scalar.activation(out=dst, in_=src, func=COPY, scale=INV)
             else:
-                nc.vector.tensor_scalar(out=t[:], in0=acc[b, h, r][:], scalar1=INV, scalar2=None, op0=MULT)
-            nc.sync.dma_start(out=out[b].rearrange("(p r) e -> p r e", r=8)[:, r, h * HALF:(h + 1) * HALF], in_=t[:])
+                nc.vector.tensor_scalar(out=dst, in0=src, scalar1=INV, scalar2=None, op0=MULT)
 
-        steps = (
-            "lv00 lv01 lk00 lq00 lq01 lk01 TR00 W000:V W010:S TR01 lv10 lq10 "
-            "lq11 lk10 W001:S VI000 VI010 W011:S lv11 QC00:S KI000 VQ010 VQ000 VI001 "
-            "KQ000 VI011 QC01:S KI001 W100:S VQ001 KQ001 S1000 VQ011 KI011 S1010 KC000:S "
-            "TR10 KI010 lk11 W110:V VI100 KQ011 KC010:S QC10:S KQ010 KI100 W101:S S1011 "
-            "VQ100 KQ100 KI101 QQ00 VI101 KC011:S KQ101 S1001 TR11 VQ101 MQ011 KC001:S "
-            "QQ01 MQ010 KI110 KI111 S1100 KQ110 KQ111 MQ001 QC11:S MQ000 KC100:S W111:V "
-            "S2010 OC010:S S2011 VI110 VI111 VQ110 VQ111 OC011:S QQ10 S1101 KC101:S S2000 "
-            "OC000:S QQ11 MQ100 MQ101 S2001 OC001:S S1111 S2100 KC111:A S1110 OC100:S S2101 "
-            "OC101:S KC110:V MQ111 MQ110 S2110 S2111 OC110:S OC111:A "
-        )
-        for item in steps.split(" "):
-            if item == "":
-                continue
-            name = item.split(":")[0]
-            eng = item.split(":")[1] if ":" in item else ""
-            op = name[0:2] if name[0] != "W" else "W"
-            a = [int(c) for c in name[len(op):]]
-            es = [eng] * 4 if eng != "A" else ["S", "V", "S", "V"]
-            if eng == "B":
-                es = ["V", "S", "V", "S"]
-            if op == "lk":
-                load_k(*a)
-            elif op == "lv":
-                load_v(*a)
-            elif op == "lq":
-                load_q(*a)
-            elif op == "KI":
-                k_interleave(*a)
-            elif op == "KQ":
-                k_quant(*a)
-            elif op == "W":
-                v_widen(*a, eng)
-            elif op == "VI":
-                v_interleave(*a)
-            elif op == "VQ":
-                v_quant(*a)
-            elif op == "QQ":
-                q_quant(*a)
-            elif op == "MQ":
-                kv_quant(*a)
-            elif op == "TR":
-                for i in range(4):
-                    q_transpose(a[0], a[1], i)
-            elif op == "QC":
-                for i in range(4):
-                    q_copy(a[0], a[1], i, es[i])
-            elif op == "S1":
-                for i in range(4):
-                    kv_matmul(a[0], a[1], a[2], i)
-            elif op == "KC":
-                for i in range(4):
-                    kv_copy(a[0], a[1], a[2], i, es[i])
-            elif op == "S2":
-                for i in range(4):
-                    out_matmul(a[0], a[1], 4 * a[2] + i)
-            elif op == "OC":
-                for i in range(4):
-                    out_copy(a[0], a[1], 4 * a[2] + i, es[i])
+        def out_store0(h, r, on_scalar=True):
+            t = work.tile([P, HALF], F32, name="res", bufs=10)
+            scaled_out(t[:], bank["o", 0, h, r][:], on_scalar)
+            nc.sync.dma_start(out=out[0].rearrange("(p r) e -> p r e", r=8)[:, r, h * HALF:(h + 1) * HALF], in_=t[:])
+
+        def out_store1(c, i, on_scalar=True):
+            t = work.tile([P, HALF], F32, name="res", bufs=10)
+            scaled_out(t[:], bank["o", 1, c, i][:].rearrange("p r n -> p (r n)"), on_scalar)
+            nc.sync.dma_start(out=out[1].rearrange("(p r) e -> p r e", r=8)[:, 2 * i:2 * i + 2, c * QUARTER:(c + 1) * QUARTER],
+                              in_=t[:].rearrange("p (r n) -> p r n", r=2))
+
+        load_v(0, 0)
+        load_k_half(0, 0, 0)
+        load_q(0, 0)
+        load_v(0, 1)
+        load_k_half(0, 0, 1)
+        load_q(0, 1)
+        load_q(0, 2)
+        load_k_half(0, 1, 0)
+        load_k_half(0, 1, 1)
+        load_q(0, 3)
+        load_q(1, 0)
+        load_q(1, 1)
+
+        v_widen(0, 0, 0, False)
+        v_widen(0, 1, 0, True)
+        v_interleave(0, 0, 0)
+        k_interleave(0, 0, 0)
+        quantise(("v", 0, 0, 0))
+        quantise(("k", 0, 0, 0))
+        q_transpose(0, 0)
+        v_widen(0, 0, 1, True)
+        q_out(0, 0)
+        v_widen(0, 1, 1, True, range(3))
+        for c in range(4):
+            kv_matmul(0, 0, c, (0,))
+        k_interleave(0, 0, 1)
+        v_interleave(0, 0, 1)
+        quantise(("k", 0, 0, 1))
+        quantise(("v", 0, 0, 1))
+        q_transpose(0, 1)
+        q_out(0, 1)
+        q_transpose(0, 2)
+        q_out(0, 2)
+        load_k(1, 0)
+        load_k(1, 1)
+        load_q(1, 2)
+        load_q(1, 3)
+        load_v(1, 0)
+        load_v(1, 1)
+        k_interleave(0, 1, 0)
+        v_widen(0, 1, 1, False, range(3, 4))
+        k_interleave(0, 1, 1)
+        quantise(("k", 0, 1, 0))
+        quantise(("k", 0, 1, 1))
+        for c in range(4):
+            kv_matmul(0, 0, c, (1,))
+            kv_out(0, 0, c)
+        q_transpose(0, 3)
+        q_out(0, 3)
+        for c in range(4):
+            kv_matmul(0, 1, c)
+            kv_out(0, 1, c)
+        quantise(("q", 0, 0))
+        v_interleave(0, 1, 0)
+        quantise(("m", 0, 0, 0))
+        quantise(("v", 0, 1, 0))
+        quantise(("q", 0, 1))
+        quantise(("q", 0, 2))
+        quantise(("m", 0, 1, 0))
+        quantise(("q", 0, 3))
+        q_transpose(1, 0)
+        q_out(1, 0)
+        q_transpose(1, 1)
+        q_out(1, 1)
+        v_interleave(0, 1, 1)
+        k_interleave(1, 0, 0)
+        quantise(("v", 0, 1, 1))
+        for r in range(8):
+            out_matmul0(0, r)
+            out_store0(0, r)
+
+        quantise(("k", 1, 0, 0))
+        k_interleave(1, 1, 0)
+        k_interleave(1, 0, 1)
+        quantise(("k", 1, 1, 0))
+        quantise(("k", 1, 0, 1))
+        k_interleave(1, 1, 1)
+        for G in range(2):
+            for c in range(4, 8):
+                kv_matmul(0, G, c)
+                kv_out(0, G, c)
+        quantise(("m", 0, 0, 1))
+        quantise(("k", 1, 1, 1))
+        v_widen_quarter(0)
+        quantise(("m", 0, 1, 1))
+        v_interleave_quarter(0)
+        v_widen_quarter(1)
+        quantise(("v", 1, 0))
+        v_interleave_quarter(1)
+        q_transpose(1, 2)
+        q_out(1, 2)
+        q_transpose(1, 3)
+        q_out(1, 3)
+        quantise(("q", 1, 0))
+        quantise(("v", 1, 1))
+        for r in range(8):
+            out_matmul0(1, r)
+            out_store0(1, r)
+        v_widen_quarter(2)
+        quantise(("q", 1, 1))
+        v_interleave_quarter(2)
+        quantise(("q", 1, 2))
+        quantise(("v", 1, 2))
+
+        def stage1(c, shares):
+            for n in range(4):
+                kv_matmul(1, n // 2, 2 * c + n % 2)
+                kv_out(1, n // 2, 2 * c + n % 2, shares[n])
+
+        def stage2(c, shares):
+            for i in range(4):
+                out_matmul1(c, i)
+                out_store1(c, i, shares[i])
+
+        scalar_only = (True, True, True, True)
+        in_turn = (True, False, True, False)
+        stage1(0, scalar_only)
+        quantise(("q", 1, 3))
+        quantise(("m", 1, 0))
+        v_widen_quarter(3)
+        stage1(1, scalar_only)
+        v_interleave_quarter(3)
+        quantise(("m", 1, 1))
+        quantise(("v", 1, 3))
+        stage2(0, scalar_only)
+        stage1(2, in_turn)
+        quantise(("m", 1, 2))
+        stage2(1, in_turn)
+        stage1(3, in_turn)
+        quantise(("m", 1, 3))
+        stage2(2, in_turn)
+        stage2(3, in_turn)

@@ -29,7 +29,7 @@ def tile_efficientattention_kernel(tc, q, k, v_bytes, v_scale, out):
         raw = ctx.enter_context(tc.tile_pool(name="raw", bufs=1))
         work = ctx.enter_context(tc.tile_pool(name="work", bufs=3))
         mx = ctx.enter_context(tc.tile_pool(name="mx", bufs=8))
-        psum = ctx.enter_context(tc.psum_pool(name="psum", bufs=8))
+        psum = ctx.enter_context(tc.psum_pool(name="psum", bufs=1))
         ctx.enter_context(tc.manual_schedule())
 
         scl = keep.tile([P, 2, PACK], F32, name="scl")
@@ -39,6 +39,16 @@ def tile_efficientattention_kernel(tc, q, k, v_bytes, v_scale, out):
 
         k_raw, v_raw, q_raw = {}, {}, {}
         v_wide, grouped, codes, bank, res = {}, {}, {}, {}, {}
+
+        free_banks, held = list(range(8)), {}
+
+        def take_bank(key, shape):
+            held[key] = free_banks.pop(0)
+            bank[key] = psum.tile(shape, F32, name="bank%d" % held[key])
+            return bank[key]
+
+        def emptied(key):
+            free_banks.append(held[key])
 
         def load_k_half(b, G, g):
             t = raw.tile([P, PACK, HALF], BF16, name="k_half", bufs=4)
@@ -116,23 +126,23 @@ def tile_efficientattention_kernel(tc, q, k, v_bytes, v_scale, out):
 
         def q_transpose(b, i):
             for G in range(2):
-                x = psum.tile([P, 2, 2, P], F32, name="bank")
+                x = take_bank(("q", b, i, G), [P, 2, 2, P])
                 for r in range(2):
                     words = q_raw[b, i][:, r, :].bitcast(F32)
                     for u in range(2):
                         nc.tensor.transpose(x[:, r, u, :], words[:, 256 * G + u:256 * (G + 1):2], ident[:])
-                bank["q", b, i, G] = x
 
         def q_out(b, i, on_scalar=(True, True)):
             t = work.tile([P, HALF * PACK], BF16, name="q_grp", align_bytes=64, bufs=4)
             for G in range(2):
                 dst = t[:, G * 1024:(G + 1) * 1024].bitcast(F32).rearrange("p (r n u) -> p r n u", r=2, u=2)
                 evacuate(dst, bank["q", b, i, G][:].rearrange("p r u n -> p r n u"), on_scalar[G])
+                emptied(("q", b, i, G))
             grouped["q", b, i] = t
 
         def kv_matmul(b, G, c, passes=(0, 1)):
             if passes[0] == 0:
-                bank["m", b, G, c] = psum.tile([P, PACK, P], F32, name="bank")
+                take_bank(("m", b, G, c), [P, PACK, P])
             x = bank["m", b, G, c]
             for g in passes:
                 kc, ks = codes["k", b, G, g]
@@ -150,19 +160,19 @@ def tile_efficientattention_kernel(tc, q, k, v_bytes, v_scale, out):
                 grouped[key] = work.tile([P, HALF * PACK], BF16, name="m_grp", align_bytes=64, bufs=4)
             dst = grouped[key][:, at * HALF:(at + 1) * HALF].rearrange("p (n t) -> p n t", t=PACK)
             evacuate(dst, bank["m", b, G, c][:].rearrange("p t n -> p n t"), on_scalar)
+            emptied(("m", b, G, c))
 
         def out_matmul0(h, r):
-            x = psum.tile([P, HALF], F32, name="bank")
+            x = take_bank(("o", 0, h, r), [P, HALF])
             qc, qs = codes["q", 0, r // 2]
             for G in range(2):
                 m = slice(G * QUARTER + (r % 2) * P, G * QUARTER + (r % 2 + 1) * P)
                 mc, ms = codes["m", 0, G, h]
                 nc.tensor.matmul_mx(out=x[:], lhsT=qc[:, m].bitcast(FP8X4), lhsT_scale=qs[:, m],
                                     rhs=mc[:].bitcast(FP8X4), rhs_scale=ms[:], start=(G == 0), stop=(G == 1))
-            bank["o", 0, h, r] = x
 
         def out_matmul1(c, i):
-            x = psum.tile([P, 2, QUARTER], F32, name="bank")
+            x = take_bank(("o", 1, c, i), [P, 2, QUARTER])
             qc, qs = codes["q", 1, i]
             mc, ms = codes["m", 1, c]
             for r in range(2):
@@ -171,7 +181,16 @@ def tile_efficientattention_kernel(tc, q, k, v_bytes, v_scale, out):
                     n = slice(G * QUARTER, (G + 1) * QUARTER)
                     nc.tensor.matmul_mx(out=x[:, r, :], lhsT=qc[:, m].bitcast(FP8X4), lhsT_scale=qs[:, m],
                                         rhs=mc[:, n].bitcast(FP8X4), rhs_scale=ms[:, n], start=(G == 0), stop=(G == 1))
-            bank["o", 1, c, i] = x
+
+        def out_matmul_row(c, row):
+            x = take_bank(("row", row), [P, QUARTER])
+            qc, qs = codes["q", 1, row // 2]
+            mc, ms = codes["m", 1, c]
+            for G in range(2):
+                m = slice(G * QUARTER + (row % 2) * P, G * QUARTER + (row % 2 + 1) * P)
+                n = slice(G * QUARTER, (G + 1) * QUARTER)
+                nc.tensor.matmul_mx(out=x[:], lhsT=qc[:, m].bitcast(FP8X4), lhsT_scale=qs[:, m],
+                                    rhs=mc[:, n].bitcast(FP8X4), rhs_scale=ms[:, n], start=(G == 0), stop=(G == 1))
 
         def scaled_out(dst, src, on_scalar):
             if on_scalar:
@@ -182,13 +201,20 @@ def tile_efficientattention_kernel(tc, q, k, v_bytes, v_scale, out):
         def out_store0(h, r, on_scalar=True):
             t = work.tile([P, HALF], F32, name="res", bufs=10)
             scaled_out(t[:], bank["o", 0, h, r][:], on_scalar)
+            emptied(("o", 0, h, r))
             nc.sync.dma_start(out=out[0].rearrange("(p r) e -> p r e", r=8)[:, r, h * HALF:(h + 1) * HALF], in_=t[:])
 
         def out_store1(c, i, on_scalar=True):
             t = work.tile([P, HALF], F32, name="res", bufs=10)
             scaled_out(t[:], bank["o", 1, c, i][:].rearrange("p r n -> p (r n)"), on_scalar)
+            emptied(("o", 1, c, i))
             nc.sync.dma_start(out=out[1].rearrange("(p r) e -> p r e", r=8)[:, 2 * i:2 * i + 2, c * QUARTER:(c + 1) * QUARTER],
                               in_=t[:].rearrange("p (r n) -> p r n", r=2))
+
+        def out_store_row(c, row, on_scalar):
+            t = work.tile([P, HALF], F32, name="res", bufs=10)
+            scaled_out(t[:, :QUARTER], bank["row", row][:], on_scalar)
+            nc.sync.dma_start(out=out[1].rearrange("(p r) e -> p r e", r=8)[:, row, c * QUARTER:(c + 1) * QUARTER], in_=t[:, :QUARTER])
 
         load_v(0, 0)
         load_k_half(0, 0, 0)
@@ -292,7 +318,6 @@ def tile_efficientattention_kernel(tc, q, k, v_bytes, v_scale, out):
         quantise(("q", 1, 1))
         v_interleave_quarter(2)
         quantise(("q", 1, 2))
-        quantise(("v", 1, 2))
 
         def stage1(c, shares):
             for n in range(4):
@@ -307,18 +332,24 @@ def tile_efficientattention_kernel(tc, q, k, v_bytes, v_scale, out):
         scalar_only = (True, True, True, True)
         in_turn = (True, False, True, False)
         stage1(0, scalar_only)
-        quantise(("q", 1, 3))
         quantise(("m", 1, 0))
+        quantise(("q", 1, 3))
+        quantise(("v", 1, 2))
         v_widen_quarter(3)
         stage1(1, scalar_only)
-        v_interleave_quarter(3)
         quantise(("m", 1, 1))
-        quantise(("v", 1, 3))
+        v_interleave_quarter(3)
         stage2(0, scalar_only)
-        stage1(2, in_turn)
+        stage1(2, scalar_only)
+        quantise(("v", 1, 3))
         quantise(("m", 1, 2))
-        stage2(1, in_turn)
+        stage2(1, (True, True, False, True))
         stage1(3, in_turn)
         quantise(("m", 1, 3))
-        stage2(2, in_turn)
-        stage2(3, in_turn)
+        stage2(2, (True, True, False, True))
+        for i in range(3):
+            out_matmul1(3, i)
+            out_store1(3, i, i == 1)
+        for row in (6, 7):
+            out_matmul_row(3, row)
+            out_store_row(3, row, row == 6)

@@ -20,6 +20,7 @@ PACK = 4
 HALF = 512
 QUARTER = 256
 INV = 1.0 / 32.0
+PARTS = ((0, 256), (256, 256), (512, 256), (768, 128), (896, 128))
 
 
 def tile_efficientattention_kernel(tc, q, k, v_bytes, v_scale, out):
@@ -36,15 +37,17 @@ def tile_efficientattention_kernel(tc, q, k, v_bytes, v_scale, out):
         nc.scalar.dma_start(out=scl[:], in_=v_scale.rearrange("o (g p j) x -> p (o g) (j x)", p=P, j=PACK))
         ident = keep.tile([P, P], F32, name="ident")
         make_identity(nc, ident[:])
+        ident_k = keep.tile([P, P], BF16, name="ident_k")
+        nc.scalar.activation(out=ident_k[:], in_=ident[:], func=COPY, scale=INV)
 
         k_raw, v_raw, q_raw = {}, {}, {}
-        v_wide, grouped, codes, bank, res = {}, {}, {}, {}, {}
+        v_wide, grouped, codes, bank = {}, {}, {}, {}
 
         free_banks, held = list(range(8)), {}
 
-        def take_bank(key, shape):
+        def take_bank(key, shape, dtype=F32):
             held[key] = free_banks.pop(0)
-            bank[key] = psum.tile(shape, F32, name="bank%d" % held[key])
+            bank[key] = psum.tile(shape, dtype, name="bank%d" % held[key])
             return bank[key]
 
         def emptied(key):
@@ -71,20 +74,36 @@ def tile_efficientattention_kernel(tc, q, k, v_bytes, v_scale, out):
             nc.sync.dma_start(out=t[:], in_=q[b].rearrange("(p r) d -> p r d", r=8)[:, 2 * i:2 * i + 2, :])
             q_raw[b, i] = t
 
-        live = {"k": 8, "v": 6, "q": 8, "m": 5}
+        live = {"k": 8, "v": 7, "q": 8, "m": 6}
 
         def quantise(key):
-            c = mx.tile([P, HALF], U32, name="codes_" + key[0], align_bytes=64, bufs=live[key[0]])
-            s = mx.tile([P, HALF], U8, name="scales_" + key[0], align_bytes=64, bufs=live[key[0]])
+            words = grouped[key].shape[1] // PACK
+            c = mx.tile([P, words], U32, name="codes_" + key[0], align_bytes=64, bufs=live[key[0]])
+            s = mx.tile([P, words], U8, name="scales_" + key[0], align_bytes=64, bufs=live[key[0]])
             nc.vector.quantize_mx(out=c[:].bitcast(FP8X4), scales=s[:], in_=grouped[key][:])
             codes[key] = (c, s)
 
         def k_interleave(b, G, g):
-            t = work.tile([P, HALF * PACK], BF16, name="k_grp", align_bytes=64, bufs=2)
+            t = work.tile([P, HALF * PACK], BF16, name="k_grp", align_bytes=64, bufs=3)
             nc.vector.tensor_scalar(
                 out=t[:].rearrange("p (t m j) -> p m j t", t=PACK, j=PACK),
                 in0=k_raw[b, G, g].rearrange("p j (m t) -> p m j t", t=PACK),
                 scalar1=INV, scalar2=None, op0=MULT)
+            grouped["k", b, G, g] = t
+
+        def k_interleave_tensor(b, G, g):
+            planes = k_raw[b, G, g].rearrange("p j (m t) -> p t m j", t=PACK)
+            for pair in range(2):
+                x = take_bank(("k", b, G, g, pair), [P, 2, P, PACK], BF16)
+                for t in range(2):
+                    nc.tensor.matmul(x[:, t], lhsT=ident_k[:], rhs=planes[:, 2 * pair + t], start=True, stop=True)
+
+        def k_out(b, G, g):
+            t = work.tile([P, HALF * PACK], BF16, name="k_grp", align_bytes=64, bufs=3)
+            for pair in range(2):
+                key = ("k", b, G, g, pair)
+                nc.scalar.copy(out=t[:, pair * 1024:(pair + 1) * 1024], in_=bank[key][:].rearrange("p t m j -> p (t m j)"))
+                emptied(key)
             grouped["k", b, G, g] = t
 
         def widen(dst, src, g, j, on_scalar):
@@ -93,30 +112,31 @@ def tile_efficientattention_kernel(tc, q, k, v_bytes, v_scale, out):
             else:
                 nc.vector.tensor_scalar(out=dst, in0=src.bitcast(FP8), scalar1=scl[:, g, j:j + 1], scalar2=None, op0=MULT)
 
-        def v_widen(b, h, g, on_scalar, rows=range(PACK)):
-            if (b, h, g) not in v_wide:
-                v_wide[b, h, g] = work.tile([P, PACK, HALF], BF16, name="v_wide", bufs=4)
+        def v_widen(h, g, on_scalar, rows=range(PACK)):
+            if (0, h, g) not in v_wide:
+                v_wide[0, h, g] = work.tile([P, PACK, HALF], BF16, name="v_wide", bufs=4)
             for j in rows:
-                widen(v_wide[b, h, g][:, j, :], v_raw[b, g][:, j, h * HALF:(h + 1) * HALF], g, j, on_scalar)
+                widen(v_wide[0, h, g][:, j, :], v_raw[0, g][:, j, h * HALF:(h + 1) * HALF], g, j, on_scalar)
 
-        def v_widen_quarter(c):
-            t = work.tile([P, 2, PACK, QUARTER], BF16, name="v_wide", bufs=4)
-            for g in range(2):
-                for j in range(PACK):
-                    widen(t[:, g, j, :], v_raw[1, g][:, j, c * QUARTER:(c + 1) * QUARTER], g, j, False)
-            v_wide[1, c] = t
-
-        def v_interleave_quarter(c):
-            t = work.tile([P, HALF * PACK], BF16, name="v_grp", align_bytes=64, bufs=2)
-            nc.vector.tensor_copy(out=t[:].rearrange("p (g c i j) -> p g c j i", g=2, i=4, j=PACK),
-                                  in_=v_wide[1, c][:].rearrange("p g j (c i) -> p g c j i", i=4))
-            grouped["v", 1, c] = t
-
-        def v_interleave(b, h, g):
+        def v_interleave(h, g):
             t = work.tile([P, HALF * PACK], BF16, name="v_grp", align_bytes=64, bufs=2)
             nc.vector.tensor_copy(out=t[:].rearrange("p (c i j) -> p c j i", i=4, j=PACK),
-                                  in_=v_wide[b, h, g][:].rearrange("p j (c i) -> p c j i", i=4))
-            grouped["v", b, h, g] = t
+                                  in_=v_wide[0, h, g][:].rearrange("p j (c i) -> p c j i", i=4))
+            grouped["v", 0, h, g] = t
+
+        def v_widen_part(n, passes=(0, 1), on_scalar=False):
+            first, width = PARTS[n]
+            if (1, n) not in v_wide:
+                v_wide[1, n] = work.tile([P, 2, PACK, width], BF16, name="v_wide", bufs=4)
+            for g in passes:
+                for j in range(PACK):
+                    widen(v_wide[1, n][:, g, j, :], v_raw[1, g][:, j, first:first + width], g, j, on_scalar)
+
+        def v_interleave_part(n):
+            t = work.tile([P, 2 * PACK * PARTS[n][1]], BF16, name="v_grp", align_bytes=64, bufs=2)
+            nc.vector.tensor_copy(out=t[:].rearrange("p (g c i j) -> p g c j i", g=2, i=4, j=PACK),
+                                  in_=v_wide[1, n][:].rearrange("p g j (c i) -> p g c j i", i=4))
+            grouped["v", 1, n] = t
 
         def evacuate(dst, src, on_scalar):
             if on_scalar:
@@ -132,89 +152,88 @@ def tile_efficientattention_kernel(tc, q, k, v_bytes, v_scale, out):
                     for u in range(2):
                         nc.tensor.transpose(x[:, r, u, :], words[:, 256 * G + u:256 * (G + 1):2], ident[:])
 
-        def q_out(b, i, on_scalar=(True, True)):
+        def q_out(b, i):
             t = work.tile([P, HALF * PACK], BF16, name="q_grp", align_bytes=64, bufs=4)
             for G in range(2):
                 dst = t[:, G * 1024:(G + 1) * 1024].bitcast(F32).rearrange("p (r n u) -> p r n u", r=2, u=2)
-                evacuate(dst, bank["q", b, i, G][:].rearrange("p r u n -> p r n u"), on_scalar[G])
+                evacuate(dst, bank["q", b, i, G][:].rearrange("p r u n -> p r n u"), True)
                 emptied(("q", b, i, G))
             grouped["q", b, i] = t
 
-        def kv_matmul(b, G, c, passes=(0, 1)):
-            if passes[0] == 0:
-                take_bank(("m", b, G, c), [P, PACK, P])
-            x = bank["m", b, G, c]
-            for g in passes:
-                kc, ks = codes["k", b, G, g]
-                (vc, vs), at = (codes["v", 0, c // 4, g], c % 4) if b == 0 else (codes["v", 1, c // 2], 2 * g + c % 2)
-                cols = slice(at * P, (at + 1) * P)
-                for t in range(PACK):
-                    m = slice(t * P, (t + 1) * P)
-                    nc.tensor.matmul_mx(out=x[:, t, :], lhsT=kc[:, m].bitcast(FP8X4), lhsT_scale=ks[:, m],
+        def kv_passes(b, G, g, targets):
+            if g == 0:
+                for key, operand, at in targets:
+                    take_bank(key, [P, PACK, P])
+            kc, ks = codes["k", b, G, g]
+            for t in range(PACK):
+                m = slice(t * P, (t + 1) * P)
+                for key, (vc, vs), at in targets:
+                    cols = slice(at * P, (at + 1) * P)
+                    nc.tensor.matmul_mx(out=bank[key][:, t, :], lhsT=kc[:, m].bitcast(FP8X4), lhsT_scale=ks[:, m],
                                         rhs=vc[:, cols].bitcast(FP8X4), rhs_scale=vs[:, cols],
                                         start=(g == 0 and t == 0), stop=(g == 1 and t == PACK - 1))
 
-        def kv_out(b, G, c, on_scalar=True):
-            key, at = (("m", b, G, c // 4), c % 4) if b == 0 else (("m", b, c // 2), 2 * G + c % 2)
-            if key not in grouped:
-                grouped[key] = work.tile([P, HALF * PACK], BF16, name="m_grp", align_bytes=64, bufs=4)
-            dst = grouped[key][:, at * HALF:(at + 1) * HALF].rearrange("p (n t) -> p n t", t=PACK)
-            evacuate(dst, bank["m", b, G, c][:].rearrange("p t n -> p n t"), on_scalar)
-            emptied(("m", b, G, c))
+        def kv_out(key, group, width, at, on_scalar):
+            if group not in grouped:
+                grouped[group] = work.tile([P, width], BF16, name="m_grp", align_bytes=64, bufs=4)
+            dst = grouped[group][:, at * HALF:(at + 1) * HALF].rearrange("p (n t) -> p n t", t=PACK)
+            evacuate(dst, bank[key][:].rearrange("p t n -> p n t"), on_scalar)
+            emptied(key)
 
-        def out_matmul0(h, r):
-            x = take_bank(("o", 0, h, r), [P, HALF])
-            qc, qs = codes["q", 0, r // 2]
-            for G in range(2):
-                m = slice(G * QUARTER + (r % 2) * P, G * QUARTER + (r % 2 + 1) * P)
-                mc, ms = codes["m", 0, G, h]
-                nc.tensor.matmul_mx(out=x[:], lhsT=qc[:, m].bitcast(FP8X4), lhsT_scale=qs[:, m],
-                                    rhs=mc[:].bitcast(FP8X4), rhs_scale=ms[:], start=(G == 0), stop=(G == 1))
+        def stage1_half(G, h, passes=(0, 1), pairs=(0, 1)):
+            for pair in pairs:
+                tiles = (2 * pair, 2 * pair + 1)
+                for g in passes:
+                    kv_passes(0, G, g, [(("m", 0, G, h, c), codes["v", 0, h, g], c) for c in tiles])
+                if passes[-1] == 1:
+                    for c in tiles:
+                        kv_out(("m", 0, G, h, c), ("m", 0, G, h), HALF * PACK, c, True)
 
-        def out_matmul1(c, i):
-            x = take_bank(("o", 1, c, i), [P, 2, QUARTER])
-            qc, qs = codes["q", 1, i]
-            mc, ms = codes["m", 1, c]
-            for r in range(2):
-                for G in range(2):
-                    m = slice(G * QUARTER + r * P, G * QUARTER + (r + 1) * P)
-                    n = slice(G * QUARTER, (G + 1) * QUARTER)
-                    nc.tensor.matmul_mx(out=x[:, r, :], lhsT=qc[:, m].bitcast(FP8X4), lhsT_scale=qs[:, m],
-                                        rhs=mc[:, n].bitcast(FP8X4), rhs_scale=ms[:, n], start=(G == 0), stop=(G == 1))
+        def stage1_part(n, shares, halves=(0, 1)):
+            tiles = PARTS[n][1] // P
+            for G in halves:
+                for g in range(2):
+                    kv_passes(1, G, g, [(("m", 1, n, G * tiles + c), codes["v", 1, n], g * tiles + c) for c in range(tiles)])
+                for at in range(G * tiles, (G + 1) * tiles):
+                    kv_out(("m", 1, n, at), ("m", 1, n), 2 * tiles * HALF, at, shares[at])
 
-        def out_matmul_row(c, row):
-            x = take_bank(("row", row), [P, QUARTER])
-            qc, qs = codes["q", 1, row // 2]
-            mc, ms = codes["m", 1, c]
-            for G in range(2):
+        def out_passes(dst, b, row, operands):
+            qc, qs = codes["q", b, row // 2]
+            for G, (mc, ms), cols in operands:
                 m = slice(G * QUARTER + (row % 2) * P, G * QUARTER + (row % 2 + 1) * P)
-                n = slice(G * QUARTER, (G + 1) * QUARTER)
-                nc.tensor.matmul_mx(out=x[:], lhsT=qc[:, m].bitcast(FP8X4), lhsT_scale=qs[:, m],
-                                    rhs=mc[:, n].bitcast(FP8X4), rhs_scale=ms[:, n], start=(G == 0), stop=(G == 1))
+                nc.tensor.matmul_mx(out=dst, lhsT=qc[:, m].bitcast(FP8X4), lhsT_scale=qs[:, m],
+                                    rhs=mc[:, cols].bitcast(FP8X4), rhs_scale=ms[:, cols], start=(G == 0), stop=(G == 1))
 
-        def scaled_out(dst, src, on_scalar):
+        def out_store(key, b, row, rows, first, width, on_scalar):
+            t = work.tile([P, rows, width], F32, name="res", bufs=10)
             if on_scalar:
-                nc.scalar.activation(out=dst, in_=src, func=COPY, scale=INV)
+                nc.scalar.activation(out=t[:], in_=bank[key][:], func=COPY, scale=INV)
             else:
-                nc.vector.tensor_scalar(out=dst, in0=src, scalar1=INV, scalar2=None, op0=MULT)
+                nc.vector.tensor_scalar(out=t[:], in0=bank[key][:], scalar1=INV, scalar2=None, op0=MULT)
+            emptied(key)
+            nc.sync.dma_start(out=out[b].rearrange("(p r) e -> p r e", r=8)[:, row:row + rows, first:first + width], in_=t[:])
 
-        def out_store0(h, r, on_scalar=True):
-            t = work.tile([P, HALF], F32, name="res", bufs=10)
-            scaled_out(t[:], bank["o", 0, h, r][:], on_scalar)
-            emptied(("o", 0, h, r))
-            nc.sync.dma_start(out=out[0].rearrange("(p r) e -> p r e", r=8)[:, r, h * HALF:(h + 1) * HALF], in_=t[:])
+        def stage2_open(h, rows):
+            for row in rows:
+                out_passes(take_bank(("o", 0, h, row), [P, 1, HALF])[:, 0, :], 0, row, [(0, codes["m", 0, 0, h], slice(0, HALF))])
 
-        def out_store1(c, i, on_scalar=True):
-            t = work.tile([P, HALF], F32, name="res", bufs=10)
-            scaled_out(t[:], bank["o", 1, c, i][:].rearrange("p r n -> p (r n)"), on_scalar)
-            emptied(("o", 1, c, i))
-            nc.sync.dma_start(out=out[1].rearrange("(p r) e -> p r e", r=8)[:, 2 * i:2 * i + 2, c * QUARTER:(c + 1) * QUARTER],
-                              in_=t[:].rearrange("p (r n) -> p r n", r=2))
+        def stage2_half(h, rows, early=0):
+            for n, row in enumerate(rows):
+                key = ("o", 0, h, row)
+                if n >= early:
+                    take_bank(key, [P, 1, HALF])
+                out_passes(bank[key][:, 0, :], 0, row, [(G, codes["m", 0, G, h], slice(0, HALF)) for G in range(1 if n < early else 0, 2)])
+                out_store(key, 0, row, 1, h * HALF, HALF, True)
 
-        def out_store_row(c, row, on_scalar):
-            t = work.tile([P, HALF], F32, name="res", bufs=10)
-            scaled_out(t[:, :QUARTER], bank["row", row][:], on_scalar)
-            nc.sync.dma_start(out=out[1].rearrange("(p r) e -> p r e", r=8)[:, row, c * QUARTER:(c + 1) * QUARTER], in_=t[:, :QUARTER])
+        def stage2_part(n, first_row, rows, shares):
+            first, width = PARTS[n]
+            for i, on_scalar in enumerate(shares):
+                row = first_row + i * rows
+                key = ("o", 1, n, row)
+                x = take_bank(key, [P, rows, width])
+                for r in range(rows):
+                    out_passes(x[:, r, :], 1, row + r, [(G, codes["m", 1, n], slice(G * width, (G + 1) * width)) for G in range(2)])
+                out_store(key, 1, row, rows, first, width, on_scalar)
 
         load_v(0, 0)
         load_k_half(0, 0, 0)
@@ -229,127 +248,108 @@ def tile_efficientattention_kernel(tc, q, k, v_bytes, v_scale, out):
         load_q(1, 0)
         load_q(1, 1)
 
-        v_widen(0, 0, 0, False)
-        v_widen(0, 1, 0, True)
-        v_interleave(0, 0, 0)
-        k_interleave(0, 0, 0)
-        quantise(("v", 0, 0, 0))
-        quantise(("k", 0, 0, 0))
+        v_widen(0, 0, False)
+        v_widen(1, 0, True)
+        k_interleave_tensor(0, 0, 0)
+        k_out(0, 0, 0)
+        v_interleave(0, 0)
         q_transpose(0, 0)
-        v_widen(0, 0, 1, True)
         q_out(0, 0)
-        v_widen(0, 1, 1, True, range(3))
-        for c in range(4):
-            kv_matmul(0, 0, c, (0,))
-        k_interleave(0, 0, 1)
-        v_interleave(0, 0, 1)
-        quantise(("k", 0, 0, 1))
+        quantise(("v", 0, 0, 0))
+        v_widen(0, 1, False)
+        quantise(("k", 0, 0, 0))
+        k_interleave_tensor(0, 0, 1)
+        k_out(0, 0, 1)
+        v_widen(1, 1, True)
+        stage1_half(0, 0, (0,))
+        v_interleave(0, 1)
+        quantise(("q", 0, 0))
         quantise(("v", 0, 0, 1))
+        quantise(("k", 0, 0, 1))
         q_transpose(0, 1)
         q_out(0, 1)
         q_transpose(0, 2)
         q_out(0, 2)
         load_k(1, 0)
         load_k(1, 1)
-        load_q(1, 2)
-        load_q(1, 3)
         load_v(1, 0)
         load_v(1, 1)
+        load_q(1, 2)
+        load_q(1, 3)
         k_interleave(0, 1, 0)
-        v_widen(0, 1, 1, False, range(3, 4))
         k_interleave(0, 1, 1)
         quantise(("k", 0, 1, 0))
         quantise(("k", 0, 1, 1))
-        for c in range(4):
-            kv_matmul(0, 0, c, (1,))
-            kv_out(0, 0, c)
+        stage1_half(0, 0, (1,))
         q_transpose(0, 3)
         q_out(0, 3)
-        for c in range(4):
-            kv_matmul(0, 1, c)
-            kv_out(0, 1, c)
-        quantise(("q", 0, 0))
-        v_interleave(0, 1, 0)
-        quantise(("m", 0, 0, 0))
+        stage1_half(1, 0)
+        v_interleave(1, 0)
+        v_interleave(1, 1)
         quantise(("v", 0, 1, 0))
-        quantise(("q", 0, 1))
-        quantise(("q", 0, 2))
+        quantise(("v", 0, 1, 1))
+        for i in range(1, 4):
+            quantise(("q", 0, i))
+        quantise(("m", 0, 0, 0))
         quantise(("m", 0, 1, 0))
-        quantise(("q", 0, 3))
         q_transpose(1, 0)
         q_out(1, 0)
         q_transpose(1, 1)
         q_out(1, 1)
-        v_interleave(0, 1, 1)
-        k_interleave(1, 0, 0)
-        quantise(("v", 0, 1, 1))
-        for r in range(8):
-            out_matmul0(0, r)
-            out_store0(0, r)
+        stage1_half(0, 1)
+        stage2_half(0, range(8))
 
-        quantise(("k", 1, 0, 0))
-        k_interleave(1, 1, 0)
+        scalar_only = (True, True, True, True)
+        k_interleave(1, 0, 0)
         k_interleave(1, 0, 1)
-        quantise(("k", 1, 1, 0))
+        quantise(("k", 1, 0, 0))
         quantise(("k", 1, 0, 1))
-        k_interleave(1, 1, 1)
-        for G in range(2):
-            for c in range(4, 8):
-                kv_matmul(0, G, c)
-                kv_out(0, G, c)
+        v_widen_part(0)
         quantise(("m", 0, 0, 1))
-        quantise(("k", 1, 1, 1))
-        v_widen_quarter(0)
-        quantise(("m", 0, 1, 1))
-        v_interleave_quarter(0)
-        v_widen_quarter(1)
+        v_interleave_part(0)
+        k_interleave(1, 1, 0)
         quantise(("v", 1, 0))
-        v_interleave_quarter(1)
+        stage1_half(1, 1)
+        v_widen_part(1, (0,), True)
+        k_interleave(1, 1, 1)
+        quantise(("m", 0, 1, 1))
+        quantise(("k", 1, 1, 0))
+        quantise(("k", 1, 1, 1))
         q_transpose(1, 2)
         q_out(1, 2)
         q_transpose(1, 3)
         q_out(1, 3)
+        stage1_part(0, scalar_only, (0,))
+        v_widen_part(1, (1,))
         quantise(("q", 1, 0))
+        v_interleave_part(1)
+        v_widen_part(2)
         quantise(("v", 1, 1))
-        for r in range(8):
-            out_matmul0(1, r)
-            out_store0(1, r)
-        v_widen_quarter(2)
+        v_interleave_part(2)
         quantise(("q", 1, 1))
-        v_interleave_quarter(2)
-        quantise(("q", 1, 2))
-
-        def stage1(c, shares):
-            for n in range(4):
-                kv_matmul(1, n // 2, 2 * c + n % 2)
-                kv_out(1, n // 2, 2 * c + n % 2, shares[n])
-
-        def stage2(c, shares):
-            for i in range(4):
-                out_matmul1(c, i)
-                out_store1(c, i, shares[i])
-
-        scalar_only = (True, True, True, True)
-        in_turn = (True, False, True, False)
-        stage1(0, scalar_only)
-        quantise(("m", 1, 0))
-        quantise(("q", 1, 3))
         quantise(("v", 1, 2))
-        v_widen_quarter(3)
-        stage1(1, scalar_only)
-        quantise(("m", 1, 1))
-        v_interleave_quarter(3)
-        stage2(0, scalar_only)
-        stage1(2, scalar_only)
+        stage2_half(1, range(8))
+        stage1_part(0, scalar_only, (1,))
+        v_widen_part(3)
+        quantise(("q", 1, 2))
+        quantise(("m", 1, 0))
+        v_interleave_part(3)
+        quantise(("q", 1, 3))
         quantise(("v", 1, 3))
+        v_widen_part(4)
+        stage1_part(1, scalar_only)
+        quantise(("m", 1, 1))
+        v_interleave_part(4)
+        stage1_part(2, scalar_only)
         quantise(("m", 1, 2))
-        stage2(1, (True, True, False, True))
-        stage1(3, in_turn)
+        quantise(("v", 1, 4))
+        stage2_part(0, 0, 2, scalar_only)
+        stage1_part(3, (True, False))
         quantise(("m", 1, 3))
-        stage2(2, (True, True, False, True))
-        for i in range(3):
-            out_matmul1(3, i)
-            out_store1(3, i, i == 1)
-        for row in (6, 7):
-            out_matmul_row(3, row)
-            out_store_row(3, row, row == 6)
+        stage2_part(1, 0, 2, (True, False, True, False))
+        stage1_part(4, (True, False))
+        quantise(("m", 1, 4))
+        stage2_part(2, 0, 2, (True, False, True, False))
+        stage2_part(3, 0, 4, (True, False))
+        stage2_part(4, 0, 4, (True,))
+        stage2_part(4, 4, 2, (False, True))

@@ -20,7 +20,7 @@ PACK = 4
 HALF = 512
 QUARTER = 256
 INV = 1.0 / 32.0
-PARTS = ((0, 256), (256, 256), (512, 256), (768, 128), (896, 128))
+PARTS = ((0, 256), (256, 256), (512, 256), (768, 256))
 
 
 def tile_efficientattention_kernel(tc, q, k, v_bytes, v_scale, out):
@@ -37,10 +37,9 @@ def tile_efficientattention_kernel(tc, q, k, v_bytes, v_scale, out):
         nc.scalar.dma_start(out=scl[:], in_=v_scale.rearrange("o (g p j) x -> p (o g) (j x)", p=P, j=PACK))
         ident = keep.tile([P, P], F32, name="ident")
         make_identity(nc, ident[:])
-        ident_k = keep.tile([P, P], BF16, name="ident_k")
-        nc.scalar.activation(out=ident_k[:], in_=ident[:], func=COPY, scale=INV)
 
         k_raw, v_raw, q_raw = {}, {}, {}
+        q_split = {}
         v_wide, grouped, codes, bank = {}, {}, {}, {}
 
         free_banks, held = list(range(8)), {}
@@ -84,26 +83,11 @@ def tile_efficientattention_kernel(tc, q, k, v_bytes, v_scale, out):
             codes[key] = (c, s)
 
         def k_interleave(b, G, g):
-            t = work.tile([P, HALF * PACK], BF16, name="k_grp", align_bytes=64, bufs=3)
+            t = work.tile([P, HALF * PACK], BF16, name="k_grp", align_bytes=64, bufs=2)
             nc.vector.tensor_scalar(
                 out=t[:].rearrange("p (t m j) -> p m j t", t=PACK, j=PACK),
                 in0=k_raw[b, G, g].rearrange("p j (m t) -> p m j t", t=PACK),
                 scalar1=INV, scalar2=None, op0=MULT)
-            grouped["k", b, G, g] = t
-
-        def k_interleave_tensor(b, G, g):
-            planes = k_raw[b, G, g].rearrange("p j (m t) -> p t m j", t=PACK)
-            for pair in range(2):
-                x = take_bank(("k", b, G, g, pair), [P, 2, P, PACK], BF16)
-                for t in range(2):
-                    nc.tensor.matmul(x[:, t], lhsT=ident_k[:], rhs=planes[:, 2 * pair + t], start=True, stop=True)
-
-        def k_out(b, G, g):
-            t = work.tile([P, HALF * PACK], BF16, name="k_grp", align_bytes=64, bufs=3)
-            for pair in range(2):
-                key = ("k", b, G, g, pair)
-                nc.scalar.copy(out=t[:, pair * 1024:(pair + 1) * 1024], in_=bank[key][:].rearrange("p t m j -> p (t m j)"))
-                emptied(key)
             grouped["k", b, G, g] = t
 
         def widen(dst, src, g, j, on_scalar):
@@ -144,13 +128,23 @@ def tile_efficientattention_kernel(tc, q, k, v_bytes, v_scale, out):
             else:
                 nc.vector.tensor_copy(out=dst, in_=src)
 
+        def q_shuffle(b, i):
+            t = work.tile([P, 4, 2, P, 2], BF16, name="q_split", bufs=3)
+            nc.vector.tensor_copy(out=t[:].rearrange("p a u n e -> p a n u e"),
+                                  in_=q_raw[b, i][:].rearrange("p r (G n u e) -> p (r G) n u e", G=2, u=2, e=2))
+            q_split[b, i] = t
+
         def q_transpose(b, i):
             for G in range(2):
                 x = take_bank(("q", b, i, G), [P, 2, 2, P])
                 for r in range(2):
                     words = q_raw[b, i][:, r, :].bitcast(F32)
                     for u in range(2):
-                        nc.tensor.transpose(x[:, r, u, :], words[:, 256 * G + u:256 * (G + 1):2], ident[:])
+                        if (b, i) in q_split:
+                            src = q_split[b, i][:, 2 * r + G, u].rearrange("p n e -> p (n e)").bitcast(F32)
+                        else:
+                            src = words[:, 256 * G + u:256 * (G + 1):2]
+                        nc.tensor.transpose(x[:, r, u, :], src, ident[:])
 
         def q_out(b, i):
             t = work.tile([P, HALF * PACK], BF16, name="q_grp", align_bytes=64, bufs=4)
@@ -181,20 +175,18 @@ def tile_efficientattention_kernel(tc, q, k, v_bytes, v_scale, out):
             emptied(key)
 
         def stage1_half(G, h, passes=(0, 1), pairs=(0, 1)):
-            for pair in pairs:
-                tiles = (2 * pair, 2 * pair + 1)
+            for c in range(2 * pairs[0], 2 * pairs[-1] + 2):
                 for g in passes:
-                    kv_passes(0, G, g, [(("m", 0, G, h, c), codes["v", 0, h, g], c) for c in tiles])
+                    kv_passes(0, G, g, [(("m", 0, G, h, c), codes["v", 0, h, g], c)])
                 if passes[-1] == 1:
-                    for c in tiles:
-                        kv_out(("m", 0, G, h, c), ("m", 0, G, h), HALF * PACK, c, True)
+                    kv_out(("m", 0, G, h, c), ("m", 0, G, h), HALF * PACK, c, True)
 
         def stage1_part(n, shares, halves=(0, 1)):
             tiles = PARTS[n][1] // P
             for G in halves:
-                for g in range(2):
-                    kv_passes(1, G, g, [(("m", 1, n, G * tiles + c), codes["v", 1, n], g * tiles + c) for c in range(tiles)])
                 for at in range(G * tiles, (G + 1) * tiles):
+                    for g in range(2):
+                        kv_passes(1, G, g, [(("m", 1, n, at), codes["v", 1, n], g * tiles + at % tiles)])
                     kv_out(("m", 1, n, at), ("m", 1, n), 2 * tiles * HALF, at, shares[at])
 
         def out_passes(dst, b, row, operands):
@@ -205,7 +197,7 @@ def tile_efficientattention_kernel(tc, q, k, v_bytes, v_scale, out):
                                     rhs=mc[:, cols].bitcast(FP8X4), rhs_scale=ms[:, cols], start=(G == 0), stop=(G == 1))
 
         def out_store(key, b, row, rows, first, width, on_scalar):
-            t = work.tile([P, rows, width], F32, name="res", bufs=10)
+            t = work.tile([P, rows, width], F32, name="res", bufs=8)
             if on_scalar:
                 nc.scalar.activation(out=t[:], in_=bank[key][:], func=COPY, scale=INV)
             else:
@@ -247,109 +239,107 @@ def tile_efficientattention_kernel(tc, q, k, v_bytes, v_scale, out):
         load_q(0, 3)
         load_q(1, 0)
         load_q(1, 1)
-
-        v_widen(0, 0, False)
-        v_widen(1, 0, True)
-        k_interleave_tensor(0, 0, 0)
-        k_out(0, 0, 0)
-        v_interleave(0, 0)
-        q_transpose(0, 0)
-        q_out(0, 0)
-        quantise(("v", 0, 0, 0))
-        v_widen(0, 1, False)
-        quantise(("k", 0, 0, 0))
-        k_interleave_tensor(0, 0, 1)
-        k_out(0, 0, 1)
-        v_widen(1, 1, True)
-        stage1_half(0, 0, (0,))
-        v_interleave(0, 1)
-        quantise(("q", 0, 0))
-        quantise(("v", 0, 0, 1))
-        quantise(("k", 0, 0, 1))
-        q_transpose(0, 1)
-        q_out(0, 1)
-        q_transpose(0, 2)
-        q_out(0, 2)
         load_k(1, 0)
-        load_k(1, 1)
         load_v(1, 0)
-        load_v(1, 1)
+        load_k(1, 1)
+        v_widen(0, 0, False)
+        v_interleave(0, 0)
+        k_interleave(0, 0, 0)
+        quantise(("v", 0, 0, 0))
+        quantise(("k", 0, 0, 0))
+        k_interleave(0, 0, 1)
+        v_widen(1, 0, True)
+        q_transpose(0, 0)
         load_q(1, 2)
-        load_q(1, 3)
+        v_widen(0, 1, True)
+        v_interleave(0, 1)
+        quantise(("k", 0, 0, 1))
+        quantise(("v", 0, 0, 1))
         k_interleave(0, 1, 0)
+        v_widen(1, 1, False, range(3, 4))
         k_interleave(0, 1, 1)
         quantise(("k", 0, 1, 0))
         quantise(("k", 0, 1, 1))
-        stage1_half(0, 0, (1,))
-        q_transpose(0, 3)
-        q_out(0, 3)
-        stage1_half(1, 0)
         v_interleave(1, 0)
+        q_out(0, 0)
+        v_widen(1, 1, True, range(0, 3))
         v_interleave(1, 1)
         quantise(("v", 0, 1, 0))
         quantise(("v", 0, 1, 1))
-        for i in range(1, 4):
-            quantise(("q", 0, i))
+        quantise(("q", 0, 0))
+        stage1_half(0, 0, (0,), (0, 1))
+        q_transpose(0, 1)
+        q_out(0, 1)
+        load_q(1, 3)
+        load_v(1, 1)
+        stage1_half(0, 0, (1,), (0,))
+        q_transpose(0, 2)
+        q_out(0, 2)
+        stage1_half(0, 0, (1,), (1,))
         quantise(("m", 0, 0, 0))
+        q_transpose(0, 3)
+        q_out(0, 3)
+        stage1_half(1, 0, (0, 1), (0, 1))
         quantise(("m", 0, 1, 0))
-        q_transpose(1, 0)
-        q_out(1, 0)
-        q_transpose(1, 1)
-        q_out(1, 1)
-        stage1_half(0, 1)
-        stage2_half(0, range(8))
-
-        scalar_only = (True, True, True, True)
+        quantise(("q", 0, 1))
+        quantise(("q", 0, 2))
+        quantise(("q", 0, 3))
         k_interleave(1, 0, 0)
         k_interleave(1, 0, 1)
         quantise(("k", 1, 0, 0))
         quantise(("k", 1, 0, 1))
-        v_widen_part(0)
+        q_shuffle(1, 1)
+        q_shuffle(1, 2)
+        q_shuffle(1, 3)
+        q_transpose(1, 0)
+        q_out(1, 0)
+        v_widen_part(0, (0,), True)
+        stage1_half(0, 1, (0, 1), (0, 1))
         quantise(("m", 0, 0, 1))
-        v_interleave_part(0)
+        v_widen_part(0, (1,), False)
         k_interleave(1, 1, 0)
-        quantise(("v", 1, 0))
-        stage1_half(1, 1)
-        v_widen_part(1, (0,), True)
-        k_interleave(1, 1, 1)
+        v_widen_part(1, (0,), False)
+        stage2_half(0, range(0, 8))
+        stage1_half(1, 1, (0, 1), (0, 1))
         quantise(("m", 0, 1, 1))
+        v_interleave_part(0)
         quantise(("k", 1, 1, 0))
+        k_interleave(1, 1, 1)
+        v_widen_part(1, (1,), False)
+        quantise(("v", 1, 0))
+        v_interleave_part(1)
         quantise(("k", 1, 1, 1))
+        quantise(("v", 1, 1))
+        quantise(("q", 1, 0))
+        q_transpose(1, 1)
+        q_out(1, 1)
+        quantise(("q", 1, 1))
+        v_widen_part(2, (0,), False)
         q_transpose(1, 2)
         q_out(1, 2)
+        quantise(("q", 1, 2))
         q_transpose(1, 3)
         q_out(1, 3)
-        stage1_part(0, scalar_only, (0,))
-        v_widen_part(1, (1,))
-        quantise(("q", 1, 0))
-        v_interleave_part(1)
-        v_widen_part(2)
-        quantise(("v", 1, 1))
-        v_interleave_part(2)
-        quantise(("q", 1, 1))
-        quantise(("v", 1, 2))
-        stage2_half(1, range(8))
-        stage1_part(0, scalar_only, (1,))
-        v_widen_part(3)
-        quantise(("q", 1, 2))
+        stage2_open(1, range(2))
+        stage2_half(1, range(0, 8), 2)
+        stage1_part(0, (True, True, True, True,), (0, 1))
         quantise(("m", 1, 0))
-        v_interleave_part(3)
         quantise(("q", 1, 3))
-        quantise(("v", 1, 3))
-        v_widen_part(4)
-        stage1_part(1, scalar_only)
+        v_widen_part(2, (1,), False)
+        v_widen_part(3, (0,), False)
+        stage1_part(1, (True, True, True, True,), (0, 1))
         quantise(("m", 1, 1))
-        v_interleave_part(4)
-        stage1_part(2, scalar_only)
+        v_interleave_part(2)
+        v_widen_part(3, (1,), False)
+        quantise(("v", 1, 2))
+        v_interleave_part(3)
+        quantise(("v", 1, 3))
+        stage2_part(0, 0, 2, (True, True, True, True,))
+        stage2_part(1, 0, 2, (True, True, True, True,))
+        stage1_part(2, (True, True, True, True,), (0, 1))
         quantise(("m", 1, 2))
-        quantise(("v", 1, 4))
-        stage2_part(0, 0, 2, scalar_only)
-        stage1_part(3, (True, False))
+        stage1_part(3, (True, False, True, False,), (0, 1))
         quantise(("m", 1, 3))
-        stage2_part(1, 0, 2, (True, False, True, False))
-        stage1_part(4, (True, False))
-        quantise(("m", 1, 4))
-        stage2_part(2, 0, 2, (True, False, True, False))
-        stage2_part(3, 0, 4, (True, False))
-        stage2_part(4, 0, 4, (True,))
-        stage2_part(4, 4, 2, (False, True))
+        stage2_part(2, 0, 2, (True, True, False, True,))
+        stage2_part(3, 0, 2, (False, True, False,))
+        stage2_part(3, 6, 1, (True, False,))

@@ -87,7 +87,7 @@ def tile_efficientattention_kernel(tc, q, k, v_bytes, v_scale, out):
             nc.vector.tensor_scalar(
                 out=t[:].rearrange("p (t m j) -> p m j t", t=PACK, j=PACK),
                 in0=k_raw[b, G, g].rearrange("p j (m t) -> p m j t", t=PACK),
-                scalar1=INV, scalar2=None, op0=MULT)
+                scalar1=INV * INV, scalar2=None, op0=MULT)
             grouped["k", b, G, g] = t
 
         def widen(dst, src, g, j, on_scalar):
@@ -175,18 +175,20 @@ def tile_efficientattention_kernel(tc, q, k, v_bytes, v_scale, out):
             emptied(key)
 
         def stage1_half(G, h, passes=(0, 1), pairs=(0, 1)):
-            for c in range(2 * pairs[0], 2 * pairs[-1] + 2):
+            for pair in pairs:
+                tiles = (2 * pair, 2 * pair + 1)
                 for g in passes:
-                    kv_passes(0, G, g, [(("m", 0, G, h, c), codes["v", 0, h, g], c)])
+                    kv_passes(0, G, g, [(("m", 0, G, h, c), codes["v", 0, h, g], c) for c in tiles])
                 if passes[-1] == 1:
-                    kv_out(("m", 0, G, h, c), ("m", 0, G, h), HALF * PACK, c, True)
+                    for c in tiles:
+                        kv_out(("m", 0, G, h, c), ("m", 0, G, h), HALF * PACK, c, True)
 
         def stage1_part(n, shares, halves=(0, 1)):
             tiles = PARTS[n][1] // P
             for G in halves:
+                for g in range(2):
+                    kv_passes(1, G, g, [(("m", 1, n, G * tiles + c), codes["v", 1, n], g * tiles + c) for c in range(tiles)])
                 for at in range(G * tiles, (G + 1) * tiles):
-                    for g in range(2):
-                        kv_passes(1, G, g, [(("m", 1, n, at), codes["v", 1, n], g * tiles + at % tiles)])
                     kv_out(("m", 1, n, at), ("m", 1, n), 2 * tiles * HALF, at, shares[at])
 
         def out_passes(dst, b, row, operands):
@@ -198,10 +200,7 @@ def tile_efficientattention_kernel(tc, q, k, v_bytes, v_scale, out):
 
         def out_store(key, b, row, rows, first, width, on_scalar):
             t = work.tile([P, rows, width], F32, name="res", bufs=8)
-            if on_scalar:
-                nc.scalar.activation(out=t[:], in_=bank[key][:], func=COPY, scale=INV)
-            else:
-                nc.vector.tensor_scalar(out=t[:], in0=bank[key][:], scalar1=INV, scalar2=None, op0=MULT)
+            evacuate(t[:], bank[key][:], on_scalar)
             emptied(key)
             nc.sync.dma_start(out=out[b].rearrange("(p r) e -> p r e", r=8)[:, row:row + rows, first:first + width], in_=t[:])
 
@@ -227,6 +226,17 @@ def tile_efficientattention_kernel(tc, q, k, v_bytes, v_scale, out):
                     out_passes(x[:, r, :], 1, row + r, [(G, codes["m", 1, n], slice(G * width, (G + 1) * width)) for G in range(2)])
                 out_store(key, 1, row, rows, first, width, on_scalar)
 
+        def warm_scalar():
+            warm = keep.tile([P, 1], F32, name="warm")
+            nc.vector.memset(warm[:], 0.0)
+            nc.scalar.activation(out=warm[:], in_=warm[:], func=COPY, scale=1.0)
+
+        def warm_tensor(moving, count):
+            if "idle" not in bank:
+                bank["idle"] = psum.tile([P, HALF], F32, name="bank7")
+            for n in range(count):
+                nc.tensor.matmul(bank["idle"][:], lhsT=k_raw[0, 0, 0][:, 0, :P], rhs=moving, start=True, stop=True)
+
         load_v(0, 0)
         load_k_half(0, 0, 0)
         load_q(0, 0)
@@ -240,7 +250,6 @@ def tile_efficientattention_kernel(tc, q, k, v_bytes, v_scale, out):
         load_q(1, 0)
         load_q(1, 1)
         load_k(1, 0)
-        load_v(1, 0)
         load_k(1, 1)
         v_widen(0, 0, False)
         v_interleave(0, 0)
@@ -271,6 +280,7 @@ def tile_efficientattention_kernel(tc, q, k, v_bytes, v_scale, out):
         q_transpose(0, 1)
         q_out(0, 1)
         load_q(1, 3)
+        load_v(1, 0)
         load_v(1, 1)
         stage1_half(0, 0, (1,), (0,))
         q_transpose(0, 2)
@@ -288,56 +298,51 @@ def tile_efficientattention_kernel(tc, q, k, v_bytes, v_scale, out):
         k_interleave(1, 0, 1)
         quantise(("k", 1, 0, 0))
         quantise(("k", 1, 0, 1))
-        q_shuffle(1, 1)
-        q_shuffle(1, 2)
-        q_shuffle(1, 3)
+        v_widen_part(0, (0, 1), False)
         q_transpose(1, 0)
         q_out(1, 0)
-        v_widen_part(0, (0,), True)
         stage1_half(0, 1, (0, 1), (0, 1))
         quantise(("m", 0, 0, 1))
-        v_widen_part(0, (1,), False)
+        v_interleave_part(0)
         k_interleave(1, 1, 0)
-        v_widen_part(1, (0,), False)
+        quantise(("v", 1, 0))
+        k_interleave(1, 1, 1)
+        q_transpose(1, 1)
+        q_out(1, 1)
         stage2_half(0, range(0, 8))
         stage1_half(1, 1, (0, 1), (0, 1))
         quantise(("m", 0, 1, 1))
-        v_interleave_part(0)
         quantise(("k", 1, 1, 0))
-        k_interleave(1, 1, 1)
-        v_widen_part(1, (1,), False)
-        quantise(("v", 1, 0))
-        v_interleave_part(1)
         quantise(("k", 1, 1, 1))
-        quantise(("v", 1, 1))
+        v_widen_part(1, (0, 1), False)
         quantise(("q", 1, 0))
-        q_transpose(1, 1)
-        q_out(1, 1)
+        v_interleave_part(1)
         quantise(("q", 1, 1))
-        v_widen_part(2, (0,), False)
+        quantise(("v", 1, 1))
+        v_widen_part(2, (0, 1), False)
         q_transpose(1, 2)
         q_out(1, 2)
         quantise(("q", 1, 2))
+        stage1_part(0, (True, True, True, True,), (0,))
         q_transpose(1, 3)
         q_out(1, 3)
-        stage2_open(1, range(2))
-        stage2_half(1, range(0, 8), 2)
-        stage1_part(0, (True, True, True, True,), (0, 1))
+        stage2_half(1, range(0, 4))
+        stage1_part(0, (True, True, True, True,), (1,))
         quantise(("m", 1, 0))
         quantise(("q", 1, 3))
-        v_widen_part(2, (1,), False)
+        v_interleave_part(2)
         v_widen_part(3, (0,), False)
+        quantise(("v", 1, 2))
+        v_widen_part(3, (1,), False)
+        stage2_half(1, range(4, 8))
         stage1_part(1, (True, True, True, True,), (0, 1))
         quantise(("m", 1, 1))
-        v_interleave_part(2)
-        v_widen_part(3, (1,), False)
-        quantise(("v", 1, 2))
         v_interleave_part(3)
         quantise(("v", 1, 3))
         stage2_part(0, 0, 2, (True, True, True, True,))
-        stage2_part(1, 0, 2, (True, True, True, True,))
         stage1_part(2, (True, True, True, True,), (0, 1))
         quantise(("m", 1, 2))
+        stage2_part(1, 0, 2, (True, True, False, True,))
         stage1_part(3, (True, False, True, False,), (0, 1))
         quantise(("m", 1, 3))
         stage2_part(2, 0, 2, (True, True, False, True,))

@@ -75,11 +75,14 @@ def tile_efficientattention_kernel(tc, q, k, v_bytes, v_scale, out):
 
         live = {"k": 8, "v": 7, "q": 8, "m": 6}
 
+        starts = {"k": (32, 64), "q": (32, 64), "v": (0, 64), "m": (0, 64)}
+
         def quantise(key):
             words = grouped[key].shape[1] // PACK
-            c = mx.tile([P, words], U32, name="codes_" + key[0], align_bytes=64, bufs=live[key[0]])
-            s = mx.tile([P, words], U8, name="scales_" + key[0], align_bytes=64, bufs=live[key[0]])
-            nc.vector.quantize_mx(out=c[:].bitcast(FP8X4), scales=s[:], in_=grouped[key][:])
+            code_start, scale_start = starts[key[0]]
+            c = mx.tile([P, code_start + words], U32, name="codes_" + key[0], align_bytes=256, bufs=live[key[0]])[:, code_start:]
+            s = mx.tile([P, scale_start + words], U8, name="scales_" + key[0], align_bytes=256, bufs=live[key[0]])[:, scale_start:]
+            nc.vector.quantize_mx(out=c.bitcast(FP8X4), scales=s, in_=grouped[key][:])
             codes[key] = (c, s)
 
         def k_interleave(b, G, g):
@@ -175,20 +178,18 @@ def tile_efficientattention_kernel(tc, q, k, v_bytes, v_scale, out):
             emptied(key)
 
         def stage1_half(G, h, passes=(0, 1), pairs=(0, 1)):
-            for pair in pairs:
-                tiles = (2 * pair, 2 * pair + 1)
+            for c in range(2 * pairs[0], 2 * pairs[-1] + 2):
                 for g in passes:
-                    kv_passes(0, G, g, [(("m", 0, G, h, c), codes["v", 0, h, g], c) for c in tiles])
+                    kv_passes(0, G, g, [(("m", 0, G, h, c), codes["v", 0, h, g], c)])
                 if passes[-1] == 1:
-                    for c in tiles:
-                        kv_out(("m", 0, G, h, c), ("m", 0, G, h), HALF * PACK, c, True)
+                    kv_out(("m", 0, G, h, c), ("m", 0, G, h), HALF * PACK, c, True)
 
         def stage1_part(n, shares, halves=(0, 1)):
             tiles = PARTS[n][1] // P
             for G in halves:
-                for g in range(2):
-                    kv_passes(1, G, g, [(("m", 1, n, G * tiles + c), codes["v", 1, n], g * tiles + c) for c in range(tiles)])
                 for at in range(G * tiles, (G + 1) * tiles):
+                    for g in range(2):
+                        kv_passes(1, G, g, [(("m", 1, n, at), codes["v", 1, n], g * tiles + at % tiles)])
                     kv_out(("m", 1, n, at), ("m", 1, n), 2 * tiles * HALF, at, shares[at])
 
         def out_passes(dst, b, row, operands):
@@ -304,8 +305,9 @@ def tile_efficientattention_kernel(tc, q, k, v_bytes, v_scale, out):
         stage1_half(0, 1, (0, 1), (0, 1))
         quantise(("m", 0, 0, 1))
         v_interleave_part(0)
-        k_interleave(1, 1, 0)
+        quantise(("q", 1, 0))
         quantise(("v", 1, 0))
+        k_interleave(1, 1, 0)
         k_interleave(1, 1, 1)
         q_transpose(1, 1)
         q_out(1, 1)
@@ -315,14 +317,13 @@ def tile_efficientattention_kernel(tc, q, k, v_bytes, v_scale, out):
         quantise(("k", 1, 1, 0))
         quantise(("k", 1, 1, 1))
         v_widen_part(1, (0, 1), False)
-        quantise(("q", 1, 0))
-        v_interleave_part(1)
         quantise(("q", 1, 1))
-        quantise(("v", 1, 1))
-        v_widen_part(2, (0, 1), False)
+        v_interleave_part(1)
         q_transpose(1, 2)
         q_out(1, 2)
         quantise(("q", 1, 2))
+        quantise(("v", 1, 1))
+        v_widen_part(2, (0, 1), False)
         stage1_part(0, (True, True, True, True,), (0,))
         q_transpose(1, 3)
         q_out(1, 3)

@@ -75,14 +75,11 @@ def tile_efficientattention_kernel(tc, q, k, v_bytes, v_scale, out):
 
         live = {"k": 8, "v": 7, "q": 8, "m": 6}
 
-        starts = {"k": (32, 64), "q": (32, 64), "v": (0, 64), "m": (0, 64)}
-
         def quantise(key):
             words = grouped[key].shape[1] // PACK
-            code_start, scale_start = starts[key[0]]
-            c = mx.tile([P, code_start + words], U32, name="codes_" + key[0], align_bytes=256, bufs=live[key[0]])[:, code_start:]
-            s = mx.tile([P, scale_start + words], U8, name="scales_" + key[0], align_bytes=256, bufs=live[key[0]])[:, scale_start:]
-            nc.vector.quantize_mx(out=c.bitcast(FP8X4), scales=s, in_=grouped[key][:])
+            c = mx.tile([P, words], U32, name="codes_" + key[0], align_bytes=64, bufs=live[key[0]])
+            s = mx.tile([P, words], U8, name="scales_" + key[0], align_bytes=64, bufs=live[key[0]])
+            nc.vector.quantize_mx(out=c[:].bitcast(FP8X4), scales=s[:], in_=grouped[key][:])
             codes[key] = (c, s)
 
         def k_interleave(b, G, g):
@@ -347,5 +344,4 @@ def tile_efficientattention_kernel(tc, q, k, v_bytes, v_scale, out):
         stage1_part(3, (True, False, True, False,), (0, 1))
         quantise(("m", 1, 3))
         stage2_part(2, 0, 2, (True, True, False, True,))
-        stage2_part(3, 0, 2, (False, True, False,))
-        stage2_part(3, 6, 1, (True, False,))
+        stage2_part(3, 0, 2, (False, True, False, True,))

@@ -39,7 +39,7 @@ def tile_efficientattention_kernel(tc, q, k, v_bytes, v_scale, out):
         make_identity(nc, ident[:])
 
         k_raw, v_raw, q_raw = {}, {}, {}
-        q_split = {}
+        q_split, res = {}, {}
         v_wide, grouped, codes, bank = {}, {}, {}, {}
 
         free_banks, held = list(range(8)), {}
@@ -197,10 +197,17 @@ def tile_efficientattention_kernel(tc, q, k, v_bytes, v_scale, out):
                                     rhs=mc[:, cols].bitcast(FP8X4), rhs_scale=ms[:, cols], start=(G == 0), stop=(G == 1))
 
         def out_store(key, b, row, rows, first, width, on_scalar):
-            t = work.tile([P, rows, width], F32, name="res", bufs=8)
-            evacuate(t[:], bank[key][:], on_scalar)
+            second = (row // rows) % 2
+            if not second:
+                res[b, first] = work.tile([P, 2 * rows, width], F32, name="res", bufs=5)
+            t = res[b, first]
+            evacuate(t[:, second * rows:(second + 1) * rows, :], bank[key][:], on_scalar)
             emptied(key)
-            nc.sync.dma_start(out=out[b].rearrange("(p r) e -> p r e", r=8)[:, row:row + rows, first:first + width], in_=t[:])
+            rows_out = out[b].rearrange("(p r) e -> p r e", r=8)
+            if b == 1 and first == E - width and row >= 4:
+                nc.sync.dma_start(out=rows_out[:, row:row + rows, first:first + width], in_=t[:, second * rows:(second + 1) * rows, :])
+            elif second:
+                nc.sync.dma_start(out=rows_out[:, row - rows:row + rows, first:first + width], in_=t[:])
 
         def stage2_open(h, rows):
             for row in rows:

@@ -204,9 +204,7 @@ def tile_efficientattention_kernel(tc, q, k, v_bytes, v_scale, out):
             evacuate(t[:, second * rows:(second + 1) * rows, :], bank[key][:], on_scalar)
             emptied(key)
             rows_out = out[b].rearrange("(p r) e -> p r e", r=8)
-            if b == 1 and first == E - width and row >= 4:
-                nc.sync.dma_start(out=rows_out[:, row:row + rows, first:first + width], in_=t[:, second * rows:(second + 1) * rows, :])
-            elif second:
+            if second:
                 nc.sync.dma_start(out=rows_out[:, row - rows:row + rows, first:first + width], in_=t[:])
 
         def stage2_open(h, rows):
@@ -241,6 +239,26 @@ def tile_efficientattention_kernel(tc, q, k, v_bytes, v_scale, out):
                 bank["idle"] = psum.tile([P, HALF], F32, name="bank7")
             for n in range(count):
                 nc.tensor.matmul(bank["idle"][:], lhsT=k_raw[0, 0, 0][:, 0, :P], rhs=moving, start=True, stop=True)
+
+        def last_stores():
+            rows_out = out[1].rearrange("(p r) e -> p r e", r=8)
+            groups = [([(2, 0, True)], nc.scalar),
+                      ([(2, 2, True), (2, 4, False)], nc.sync),
+                      ([(2, 6, False), (3, 6, True)], nc.scalar),
+                      ([(3, 0, True), (3, 2, False)], nc.sync),
+                      ([(3, 4, True)], nc.scalar)]
+            for banks, queue in groups:
+                (n0, row0, e0), (n1, row1, e1) = banks[0], banks[-1]
+                rows, width = row1 - row0 + 2, (n1 - n0 + 1) * QUARTER
+                t = work.tile([P, rows, width], F32, name="res", bufs=5)
+                for n, row, on_scalar in banks:
+                    key = ("o", 1, n, row)
+                    x = take_bank(key, [P, 2, QUARTER])
+                    for r in range(2):
+                        out_passes(x[:, r, :], 1, row + r, [(G, codes["m", 1, n], slice(G * QUARTER, (G + 1) * QUARTER)) for G in range(2)])
+                    evacuate(t[:, row - row0:row - row0 + 2, (n - n0) * QUARTER:(n - n0 + 1) * QUARTER], x[:], on_scalar)
+                    emptied(key)
+                queue.dma_start(out=rows_out[:, row0:row0 + rows, n0 * QUARTER:n0 * QUARTER + width], in_=t[:])
 
         load_v(0, 0)
         load_k_half(0, 0, 0)
@@ -350,5 +368,4 @@ def tile_efficientattention_kernel(tc, q, k, v_bytes, v_scale, out):
         stage2_part(1, 0, 2, (True, True, False, True,))
         stage1_part(3, (True, False, True, False,), (0, 1))
         quantise(("m", 1, 3))
-        stage2_part(2, 0, 2, (True, True, False, True,))
-        stage2_part(3, 0, 2, (False, True, False, True,))
+        last_stores()

@@ -69,9 +69,14 @@ def tile_efficientattention_kernel(tc, q, k, v_bytes, v_scale, out):
             v_raw[b, g] = t
 
         def load_q(b, i):
-            t = raw.tile([P, 2, D], BF16, name="q_raw", bufs=6)
+            t = raw.tile([P, 2, D], BF16, name="q_raw", bufs=2)
             nc.sync.dma_start(out=t[:], in_=q[b].rearrange("(p r) d -> p r d", r=8)[:, 2 * i:2 * i + 2, :])
             q_raw[b, i] = t
+
+        def load_q_pair(b, i):
+            t = raw.tile([P, 4, D], BF16, name="q_pair", bufs=2)
+            nc.sync.dma_start(out=t[:], in_=q[b].rearrange("(p r) d -> p r d", r=8)[:, 2 * i:2 * i + 4, :])
+            q_raw[b, i], q_raw[b, i + 1] = t[:, 0:2, :], t[:, 2:4, :]
 
         live = {"k": 8, "v": 7, "q": 8, "m": 6}
 
@@ -199,7 +204,7 @@ def tile_efficientattention_kernel(tc, q, k, v_bytes, v_scale, out):
         def out_store(key, b, row, rows, first, width, on_scalar):
             second = (row // rows) % 2
             if not second:
-                res[b, first] = work.tile([P, 2 * rows, width], F32, name="res", bufs=5)
+                res[b, first] = work.tile([P, 2 * rows, width], F32, name="res", bufs=4)
             t = res[b, first]
             evacuate(t[:, second * rows:(second + 1) * rows, :], bank[key][:], on_scalar)
             emptied(key)
@@ -242,15 +247,14 @@ def tile_efficientattention_kernel(tc, q, k, v_bytes, v_scale, out):
 
         def last_stores():
             rows_out = out[1].rearrange("(p r) e -> p r e", r=8)
-            groups = [([(2, 0, True)], nc.scalar),
-                      ([(2, 2, True), (2, 4, False)], nc.sync),
-                      ([(2, 6, False), (3, 6, True)], nc.scalar),
-                      ([(3, 0, True), (3, 2, False)], nc.sync),
-                      ([(3, 4, True)], nc.scalar)]
-            for banks, queue in groups:
+            groups = [[(2, 0, True)],
+                      [(2, 2, True), (2, 4, False)],
+                      [(2, 6, True), (3, 6, False)],
+                      [(3, 0, True), (3, 2, False), (3, 4, True)]]
+            for banks in groups:
                 (n0, row0, e0), (n1, row1, e1) = banks[0], banks[-1]
                 rows, width = row1 - row0 + 2, (n1 - n0 + 1) * QUARTER
-                t = work.tile([P, rows, width], F32, name="res", bufs=5)
+                t = work.tile([P, rows, width], F32, name="res", bufs=4)
                 for n, row, on_scalar in banks:
                     key = ("o", 1, n, row)
                     x = take_bank(key, [P, 2, QUARTER])
@@ -258,20 +262,18 @@ def tile_efficientattention_kernel(tc, q, k, v_bytes, v_scale, out):
                         out_passes(x[:, r, :], 1, row + r, [(G, codes["m", 1, n], slice(G * QUARTER, (G + 1) * QUARTER)) for G in range(2)])
                     evacuate(t[:, row - row0:row - row0 + 2, (n - n0) * QUARTER:(n - n0 + 1) * QUARTER], x[:], on_scalar)
                     emptied(key)
-                queue.dma_start(out=rows_out[:, row0:row0 + rows, n0 * QUARTER:n0 * QUARTER + width], in_=t[:])
+                nc.sync.dma_start(out=rows_out[:, row0:row0 + rows, n0 * QUARTER:n0 * QUARTER + width], in_=t[:])
 
         load_v(0, 0)
         load_k_half(0, 0, 0)
         load_q(0, 0)
         load_v(0, 1)
         load_k_half(0, 0, 1)
-        load_q(0, 1)
-        load_q(0, 2)
+        load_q_pair(0, 1)
         load_k_half(0, 1, 0)
         load_k_half(0, 1, 1)
         load_q(0, 3)
-        load_q(1, 0)
-        load_q(1, 1)
+        load_q_pair(1, 0)
         load_k(1, 0)
         load_k(1, 1)
         v_widen(0, 0, False)
@@ -282,7 +284,6 @@ def tile_efficientattention_kernel(tc, q, k, v_bytes, v_scale, out):
         k_interleave(0, 0, 1)
         v_widen(1, 0, True)
         q_transpose(0, 0)
-        load_q(1, 2)
         v_widen(0, 1, True)
         v_interleave(0, 1)
         quantise(("k", 0, 0, 1))
@@ -302,12 +303,12 @@ def tile_efficientattention_kernel(tc, q, k, v_bytes, v_scale, out):
         stage1_half(0, 0, (0,), (0, 1))
         q_transpose(0, 1)
         q_out(0, 1)
-        load_q(1, 3)
-        load_v(1, 0)
-        load_v(1, 1)
         stage1_half(0, 0, (1,), (0,))
         q_transpose(0, 2)
         q_out(0, 2)
+        load_q_pair(1, 2)
+        load_v(1, 0)
+        load_v(1, 1)
         stage1_half(0, 0, (1,), (1,))
         quantise(("m", 0, 0, 0))
         q_transpose(0, 3)

@@ -18,9 +18,7 @@ MULT = mybir.AluOpType.mult
 P = 128
 PACK = 4
 HALF = 512
-QUARTER = 256
 INV = 1.0 / 32.0
-PARTS = ((0, 256), (256, 256), (512, 256), (768, 256))
 
 
 def tile_efficientattention_kernel(tc, q, k, v_bytes, v_scale, out):
@@ -28,19 +26,23 @@ def tile_efficientattention_kernel(tc, q, k, v_bytes, v_scale, out):
     with ExitStack() as ctx:
         keep = ctx.enter_context(tc.tile_pool(name="keep", bufs=1))
         raw = ctx.enter_context(tc.tile_pool(name="raw", bufs=1))
-        work = ctx.enter_context(tc.tile_pool(name="work", bufs=3))
-        mx = ctx.enter_context(tc.tile_pool(name="mx", bufs=8))
+        work = ctx.enter_context(tc.tile_pool(name="work", bufs=1))
+        mx = ctx.enter_context(tc.tile_pool(name="mx", bufs=1))
         psum = ctx.enter_context(tc.psum_pool(name="psum", bufs=1))
         ctx.enter_context(tc.manual_schedule())
+
+        bufs = {'v_raw': 2, 'q_raw1': 4, 'q_raw2': 1, 'k_grp': 2, 'v_wide': 4, 'v_grp': 3, 'q_grp': 6, 'm_grp': 3, 'q_split': 2, 'res1': 1, 'res2': 4, 'res3': 1, 'codes_k': 4, 'codes_v': 4, 'codes_q': 6, 'codes_m': 4}
 
         scl = keep.tile([P, 2, PACK], F32, name="scl")
         nc.scalar.dma_start(out=scl[:], in_=v_scale.rearrange("o (g p j) x -> p (o g) (j x)", p=P, j=PACK))
         ident = keep.tile([P, P], F32, name="ident")
         make_identity(nc, ident[:])
+        ident_bf = keep.tile([P, P], BF16, name="ident_bf")
+        make_identity(nc, ident_bf[:])
 
-        k_raw, v_raw, q_raw = {}, {}, {}
-        q_split, res = {}, {}
-        v_wide, grouped, codes, bank = {}, {}, {}, {}
+        k_raw, v_raw, q_raw, q_split = {}, {}, {}, {}
+        v_wide, grouped, res, bank = {}, {}, {}, {}
+        k_codes, v_codes, q_codes, m_codes = {}, {}, {}, {}
 
         free_banks, held = list(range(8)), {}
 
@@ -49,324 +51,474 @@ def tile_efficientattention_kernel(tc, q, k, v_bytes, v_scale, out):
             bank[key] = psum.tile(shape, dtype, name="bank%d" % held[key])
             return bank[key]
 
-        def emptied(key):
+        def evacuate(key, dst, src, on_scalar):
+            if on_scalar:
+                nc.scalar.copy(out=dst, in_=src)
+            else:
+                nc.vector.tensor_copy(out=dst, in_=src)
             free_banks.append(held[key])
 
-        def load_k_half(b, G, g):
-            t = raw.tile([P, PACK, HALF], BF16, name="k_half", bufs=4)
-            nc.sync.dma_start(out=t[:], in_=k[b].rearrange("(g p j) d -> g p j d", p=P, j=PACK)[g][:, :, G * HALF:(G + 1) * HALF])
-            k_raw[b, G, g] = t[:]
-
-        def load_k(b, g):
-            t = raw.tile([P, PACK, D], BF16, name="k_full", bufs=2)
-            nc.sync.dma_start(out=t[:], in_=k[b].rearrange("(g p j) d -> g p j d", p=P, j=PACK)[g])
-            for G in range(2):
-                k_raw[b, G, g] = t[:, :, G * HALF:(G + 1) * HALF]
+        def load_k(b, g, first, halves):
+            t = raw.tile([P, PACK, halves * HALF], BF16, name="k_raw%d%d%d" % (b, g, first))
+            rows = k[b].rearrange("(g p j) d -> g p j d", p=P, j=PACK)[g]
+            nc.sync.dma_start(out=t[:], in_=rows[:, :, first * HALF:(first + halves) * HALF])
+            for n in range(halves):
+                k_raw[b, first + n, g] = t[:, :, n * HALF:(n + 1) * HALF]
 
         def load_v(b, g):
-            t = raw.tile([P, PACK, E], U8, name="v_raw", bufs=4)
+            t = raw.tile([P, PACK, E], U8, name="v_raw", bufs=bufs["v_raw"])
             nc.sync.dma_start(out=t[:], in_=v_bytes[b].rearrange("(g p j) e -> g p j e", p=P, j=PACK)[g])
-            v_raw[b, g] = t
+            for j in range(PACK):
+                v_raw[b, g, j] = t[:, j, :]
 
-        def load_q(b, i):
-            t = raw.tile([P, 2, D], BF16, name="q_raw", bufs=2)
-            nc.sync.dma_start(out=t[:], in_=q[b].rearrange("(p r) d -> p r d", r=8)[:, 2 * i:2 * i + 2, :])
-            q_raw[b, i] = t
+        def load_v_rows(b, g, j):
+            t = raw.tile([P, 2, E], U8, name="v_rows%d%d%d" % (b, g, j))
+            nc.sync.dma_start(out=t[:], in_=v_bytes[b].rearrange("(g p j) e -> g p j e", p=P, j=PACK)[g][:, j:j + 2, :])
+            for n in range(2):
+                v_raw[b, g, j + n] = t[:, n, :]
 
-        def load_q_pair(b, i):
-            t = raw.tile([P, 4, D], BF16, name="q_pair", bufs=2)
-            nc.sync.dma_start(out=t[:], in_=q[b].rearrange("(p r) d -> p r d", r=8)[:, 2 * i:2 * i + 4, :])
-            q_raw[b, i], q_raw[b, i + 1] = t[:, 0:2, :], t[:, 2:4, :]
+        def load_q(b, first, pieces):
+            t = raw.tile([P, 2 * pieces, D], BF16, name="q_raw%d" % pieces, bufs=bufs["q_raw%d" % pieces])
+            nc.sync.dma_start(out=t[:], in_=q[b].rearrange("(p r) d -> p r d", r=8)[:, 2 * first:2 * (first + pieces), :])
+            for n in range(pieces):
+                q_raw[b, first + n] = t[:, 2 * n:2 * n + 2, :]
 
-        live = {"k": 8, "v": 7, "q": 8, "m": 6}
-
-        def quantise(key):
-            words = grouped[key].shape[1] // PACK
-            c = mx.tile([P, words], U32, name="codes_" + key[0], align_bytes=64, bufs=live[key[0]])
-            s = mx.tile([P, words], U8, name="scales_" + key[0], align_bytes=64, bufs=live[key[0]])
-            nc.vector.quantize_mx(out=c[:].bitcast(FP8X4), scales=s[:], in_=grouped[key][:])
-            codes[key] = (c, s)
+        def quantise(src, kind):
+            words = src.shape[1] // PACK
+            c = mx.tile([P, words], U32, name="codes_" + kind, align_bytes=64, bufs=bufs["codes_" + kind])
+            s = mx.tile([P, words], U8, name="scales_" + kind, align_bytes=64, bufs=bufs["codes_" + kind])
+            nc.vector.quantize_mx(out=c[:].bitcast(FP8X4), scales=s[:], in_=src[:])
+            return c, s
 
         def k_interleave(b, G, g):
-            t = work.tile([P, HALF * PACK], BF16, name="k_grp", align_bytes=64, bufs=2)
+            t = work.tile([P, HALF * PACK], BF16, name="k_grp", align_bytes=64, bufs=bufs["k_grp"])
             nc.vector.tensor_scalar(
                 out=t[:].rearrange("p (t m j) -> p m j t", t=PACK, j=PACK),
                 in0=k_raw[b, G, g].rearrange("p j (m t) -> p m j t", t=PACK),
                 scalar1=INV * INV, scalar2=None, op0=MULT)
             grouped["k", b, G, g] = t
 
-        def widen(dst, src, g, j, on_scalar):
-            if on_scalar:
-                nc.scalar.activation(out=dst, in_=src.bitcast(FP8), func=COPY, scale=scl[:, g, j:j + 1])
-            else:
-                nc.vector.tensor_scalar(out=dst, in0=src.bitcast(FP8), scalar1=scl[:, g, j:j + 1], scalar2=None, op0=MULT)
+        def k_quantise(b, G, g):
+            k_codes[b, G, g] = quantise(grouped["k", b, G, g], "k")
 
-        def v_widen(h, g, on_scalar, rows=range(PACK)):
-            if (0, h, g) not in v_wide:
-                v_wide[0, h, g] = work.tile([P, PACK, HALF], BF16, name="v_wide", bufs=4)
+        def v_widen(unit, g, rows, on_scalar):
+            b, passes, first, tiles = unit
+            if unit not in v_wide:
+                v_wide[unit] = work.tile([P, len(passes), PACK, tiles * P], BF16, name="v_wide", bufs=bufs["v_wide"])
             for j in rows:
-                widen(v_wide[0, h, g][:, j, :], v_raw[0, g][:, j, h * HALF:(h + 1) * HALF], g, j, on_scalar)
+                dst, codes = v_wide[unit][:, passes.index(g), j, :], v_raw[b, g, j][:, first * P:(first + tiles) * P].bitcast(FP8)
+                if on_scalar:
+                    nc.scalar.activation(out=dst, in_=codes, func=COPY, scale=scl[:, g, j:j + 1])
+                else:
+                    nc.vector.tensor_scalar(out=dst, in0=codes, scalar1=scl[:, g, j:j + 1], scalar2=None, op0=MULT)
 
-        def v_interleave(h, g):
-            t = work.tile([P, HALF * PACK], BF16, name="v_grp", align_bytes=64, bufs=2)
-            nc.vector.tensor_copy(out=t[:].rearrange("p (c i j) -> p c j i", i=4, j=PACK),
-                                  in_=v_wide[0, h, g][:].rearrange("p j (c i) -> p c j i", i=4))
-            grouped["v", 0, h, g] = t
-
-        def v_widen_part(n, passes=(0, 1), on_scalar=False):
-            first, width = PARTS[n]
-            if (1, n) not in v_wide:
-                v_wide[1, n] = work.tile([P, 2, PACK, width], BF16, name="v_wide", bufs=4)
-            for g in passes:
-                for j in range(PACK):
-                    widen(v_wide[1, n][:, g, j, :], v_raw[1, g][:, j, first:first + width], g, j, on_scalar)
-
-        def v_interleave_part(n):
-            t = work.tile([P, 2 * PACK * PARTS[n][1]], BF16, name="v_grp", align_bytes=64, bufs=2)
-            nc.vector.tensor_copy(out=t[:].rearrange("p (g c i j) -> p g c j i", g=2, i=4, j=PACK),
-                                  in_=v_wide[1, n][:].rearrange("p g j (c i) -> p g c j i", i=4))
-            grouped["v", 1, n] = t
-
-        def evacuate(dst, src, on_scalar):
+        def v_interleave(unit, part=None, on_scalar=False):
+            b, passes, first, tiles = unit
+            if ("v", unit) not in grouped:
+                grouped["v", unit] = work.tile([P, len(passes) * PACK * tiles * P], BF16, name="v_grp", align_bytes=64, bufs=bufs["v_grp"])
+            dst = grouped["v", unit][:].rearrange("p (g c i j) -> p g c j i", g=len(passes), i=4, j=PACK)
+            src = v_wide[unit][:].rearrange("p g j (c i) -> p g c j i", i=4)
+            if part is not None:
+                dst, src = dst[:, 0, part[0] * 32:part[1] * 32], src[:, 0, part[0] * 32:part[1] * 32]
             if on_scalar:
                 nc.scalar.copy(out=dst, in_=src)
             else:
                 nc.vector.tensor_copy(out=dst, in_=src)
 
+        def v_weave(unit, a):
+            x = take_bank(("w", unit, a), [P, 2, P, PACK], BF16)
+            for n in range(2):
+                cols = slice((2 * a + n) * P, (2 * a + n + 1) * P)
+                nc.tensor.matmul(x[:, n].rearrange("p c j -> p j c"), lhsT=ident_bf[:], rhs=v_wide[unit][:, 0, :, cols], start=True, stop=True)
+
+        def v_weave_out(unit, a, on_scalar):
+            if ("v", unit) not in grouped:
+                grouped["v", unit] = work.tile([P, HALF * PACK], BF16, name="v_grp", align_bytes=64, bufs=bufs["v_grp"])
+            evacuate(("w", unit, a), grouped["v", unit][:, a * 1024:(a + 1) * 1024], bank["w", unit, a][:].rearrange("p n c j -> p (n c j)"), on_scalar)
+
+        def v_quantise(unit):
+            b, passes, first, tiles = unit
+            c, s = quantise(grouped["v", unit], "v")
+            for n, g in enumerate(passes):
+                for a in range(tiles):
+                    v_codes[b, g, first + a] = (c, s, (n * tiles + a) * P)
+
         def q_shuffle(b, i):
-            t = work.tile([P, 4, 2, P, 2], BF16, name="q_split", bufs=3)
-            nc.vector.tensor_copy(out=t[:].rearrange("p a u n e -> p a n u e"),
-                                  in_=q_raw[b, i][:].rearrange("p r (G n u e) -> p (r G) n u e", G=2, u=2, e=2))
+            t = work.tile([P, 4, 2, P], F32, name="q_split", bufs=bufs["q_split"])
+            nc.vector.tensor_copy(out=t[:].rearrange("p a u (n e) -> p a n u e", e=2),
+                                  in_=q_raw[b, i].bitcast(F32).rearrange("p r (G n e u) -> p (r G) n u e", G=2, e=2, u=2))
             q_split[b, i] = t
 
-        def q_transpose(b, i):
-            for G in range(2):
-                x = take_bank(("q", b, i, G), [P, 2, 2, P])
-                for r in range(2):
-                    words = q_raw[b, i][:, r, :].bitcast(F32)
-                    for u in range(2):
-                        if (b, i) in q_split:
-                            src = q_split[b, i][:, 2 * r + G, u].rearrange("p n e -> p (n e)").bitcast(F32)
-                        else:
-                            src = words[:, 256 * G + u:256 * (G + 1):2]
-                        nc.tensor.transpose(x[:, r, u, :], src, ident[:])
+        def q_transpose(b, i, G):
+            x = take_bank(("q", b, i, G), [P, 2, 2, P])
+            for r in range(2):
+                words = q_raw[b, i][:, r, :].bitcast(F32)
+                for u in range(2):
+                    if (b, i) in q_split:
+                        src = q_split[b, i][:, 2 * r + G, u]
+                    else:
+                        src = words[:, 256 * G + u:256 * (G + 1):2]
+                    nc.tensor.transpose(x[:, r, u, :], src, ident[:])
 
-        def q_out(b, i):
-            t = work.tile([P, HALF * PACK], BF16, name="q_grp", align_bytes=64, bufs=4)
-            for G in range(2):
-                dst = t[:, G * 1024:(G + 1) * 1024].bitcast(F32).rearrange("p (r n u) -> p r n u", r=2, u=2)
-                evacuate(dst, bank["q", b, i, G][:].rearrange("p r u n -> p r n u"), True)
-                emptied(("q", b, i, G))
-            grouped["q", b, i] = t
+        def q_out(b, i, G, on_scalar):
+            if ("q", b, i) not in grouped:
+                grouped["q", b, i] = work.tile([P, HALF * PACK], BF16, name="q_grp", align_bytes=64, bufs=bufs["q_grp"])
+            dst = grouped["q", b, i][:, G * 1024:(G + 1) * 1024].bitcast(F32).rearrange("p (r n u) -> p r n u", r=2, u=2)
+            evacuate(("q", b, i, G), dst, bank["q", b, i, G][:].rearrange("p r u n -> p r n u"), on_scalar)
 
-        def kv_passes(b, G, g, targets):
+        def q_quantise(b, i):
+            q_codes[b, i] = quantise(grouped["q", b, i], "q")
+
+        def kv_passes(b, G, c, g):
             if g == 0:
-                for key, operand, at in targets:
-                    take_bank(key, [P, PACK, P])
-            kc, ks = codes["k", b, G, g]
+                take_bank(("m", b, G, c), [P, PACK, P])
+            kc, ks = k_codes[b, G, g]
+            vc, vs, at = v_codes[b, g, c]
             for t in range(PACK):
                 m = slice(t * P, (t + 1) * P)
-                for key, (vc, vs), at in targets:
-                    cols = slice(at * P, (at + 1) * P)
-                    nc.tensor.matmul_mx(out=bank[key][:, t, :], lhsT=kc[:, m].bitcast(FP8X4), lhsT_scale=ks[:, m],
-                                        rhs=vc[:, cols].bitcast(FP8X4), rhs_scale=vs[:, cols],
-                                        start=(g == 0 and t == 0), stop=(g == 1 and t == PACK - 1))
+                nc.tensor.matmul_mx(out=bank["m", b, G, c][:, t, :], lhsT=kc[:, m].bitcast(FP8X4), lhsT_scale=ks[:, m],
+                                    rhs=vc[:, at:at + P].bitcast(FP8X4), rhs_scale=vs[:, at:at + P],
+                                    start=(g == 0 and t == 0), stop=(g == 1 and t == PACK - 1))
 
-        def kv_out(key, group, width, at, on_scalar):
-            if group not in grouped:
-                grouped[group] = work.tile([P, width], BF16, name="m_grp", align_bytes=64, bufs=4)
-            dst = grouped[group][:, at * HALF:(at + 1) * HALF].rearrange("p (n t) -> p n t", t=PACK)
-            evacuate(dst, bank[key][:].rearrange("p t n -> p n t"), on_scalar)
-            emptied(key)
+        def kv_out(unit, G, c, on_scalar):
+            b, halves, first, tiles = unit
+            if ("m", unit) not in grouped:
+                grouped["m", unit] = work.tile([P, len(halves) * tiles * HALF], BF16, name="m_grp", align_bytes=64, bufs=bufs["m_grp"])
+            at = halves.index(G) * tiles + c - first
+            dst = grouped["m", unit][:, at * HALF:(at + 1) * HALF].rearrange("p (n t) -> p n t", t=PACK)
+            evacuate(("m", b, G, c), dst, bank["m", b, G, c][:].rearrange("p t n -> p n t"), on_scalar)
 
-        def stage1_half(G, h, passes=(0, 1), pairs=(0, 1)):
-            for c in range(2 * pairs[0], 2 * pairs[-1] + 2):
-                for g in passes:
-                    kv_passes(0, G, g, [(("m", 0, G, h, c), codes["v", 0, h, g], c)])
-                if passes[-1] == 1:
-                    kv_out(("m", 0, G, h, c), ("m", 0, G, h), HALF * PACK, c, True)
+        def kv_quantise(unit):
+            b, halves, first, tiles = unit
+            c, s = quantise(grouped["m", unit], "m")
+            for n, G in enumerate(halves):
+                for a in range(tiles):
+                    m_codes[b, G, first + a] = (c, s, (n * tiles + a) * P)
 
-        def stage1_part(n, shares, halves=(0, 1)):
-            tiles = PARTS[n][1] // P
-            for G in halves:
-                for at in range(G * tiles, (G + 1) * tiles):
-                    for g in range(2):
-                        kv_passes(1, G, g, [(("m", 1, n, at), codes["v", 1, n], g * tiles + at % tiles)])
-                    kv_out(("m", 1, n, at), ("m", 1, n), 2 * tiles * HALF, at, shares[at])
+        def out_passes(b, row, rows, first, tiles, halves):
+            key, width = ("o", b, row, first), tiles * P
+            if halves[0] == 0:
+                take_bank(key, [P, rows, width])
+            order = [(r, G) for r in range(rows) for G in halves]
+            for r, G in order:
+                qc, qs = q_codes[b, (row + r) // 2]
+                mc, ms, at = m_codes[b, G, first]
+                m = slice(G * 2 * P + ((row + r) % 2) * P, G * 2 * P + ((row + r) % 2 + 1) * P)
+                nc.tensor.matmul_mx(out=bank[key][:, r, :], lhsT=qc[:, m].bitcast(FP8X4), lhsT_scale=qs[:, m],
+                                    rhs=mc[:, at:at + width].bitcast(FP8X4), rhs_scale=ms[:, at:at + width],
+                                    start=((r, G) == (0, 0)), stop=((r, G) == (rows - 1, 1)))
 
-        def out_passes(dst, b, row, operands):
-            qc, qs = codes["q", b, row // 2]
-            for G, (mc, ms), cols in operands:
-                m = slice(G * QUARTER + (row % 2) * P, G * QUARTER + (row % 2 + 1) * P)
-                nc.tensor.matmul_mx(out=dst, lhsT=qc[:, m].bitcast(FP8X4), lhsT_scale=qs[:, m],
-                                    rhs=mc[:, cols].bitcast(FP8X4), rhs_scale=ms[:, cols], start=(G == 0), stop=(G == 1))
+        def out_copy(block, row, rows, first, tiles, on_scalar):
+            b, row0, all_rows, first0, all_tiles = block
+            if block not in res:
+                res[block] = work.tile([P, all_rows, all_tiles * P], F32, name="res%d" % (all_rows * all_tiles // 4), bufs=bufs["res%d" % (all_rows * all_tiles // 4)])
+            dst = res[block][:, row - row0:row - row0 + rows, (first - first0) * P:(first - first0 + tiles) * P]
+            evacuate(("o", b, row, first), dst, bank["o", b, row, first][:], on_scalar)
 
-        def out_store(key, b, row, rows, first, width, on_scalar):
-            second = (row // rows) % 2
-            if not second:
-                res[b, first] = work.tile([P, 2 * rows, width], F32, name="res", bufs=4)
-            t = res[b, first]
-            evacuate(t[:, second * rows:(second + 1) * rows, :], bank[key][:], on_scalar)
-            emptied(key)
+        def store(block):
+            b, row0, all_rows, first0, all_tiles = block
             rows_out = out[b].rearrange("(p r) e -> p r e", r=8)
-            if second:
-                nc.sync.dma_start(out=rows_out[:, row - rows:row + rows, first:first + width], in_=t[:])
+            nc.sync.dma_start(out=rows_out[:, row0:row0 + all_rows, first0 * P:(first0 + all_tiles) * P], in_=res[block][:])
 
-        def stage2_open(h, rows):
-            for row in rows:
-                out_passes(take_bank(("o", 0, h, row), [P, 1, HALF])[:, 0, :], 0, row, [(0, codes["m", 0, 0, h], slice(0, HALF))])
-
-        def stage2_half(h, rows, early=0):
-            for n, row in enumerate(rows):
-                key = ("o", 0, h, row)
-                if n >= early:
-                    take_bank(key, [P, 1, HALF])
-                out_passes(bank[key][:, 0, :], 0, row, [(G, codes["m", 0, G, h], slice(0, HALF)) for G in range(1 if n < early else 0, 2)])
-                out_store(key, 0, row, 1, h * HALF, HALF, True)
-
-        def stage2_part(n, first_row, rows, shares):
-            first, width = PARTS[n]
-            for i, on_scalar in enumerate(shares):
-                row = first_row + i * rows
-                key = ("o", 1, n, row)
-                x = take_bank(key, [P, rows, width])
-                for r in range(rows):
-                    out_passes(x[:, r, :], 1, row + r, [(G, codes["m", 1, n], slice(G * width, (G + 1) * width)) for G in range(2)])
-                out_store(key, 1, row, rows, first, width, on_scalar)
-
-        def warm_scalar():
-            warm = keep.tile([P, 1], F32, name="warm")
-            nc.vector.memset(warm[:], 0.0)
-            nc.scalar.activation(out=warm[:], in_=warm[:], func=COPY, scale=1.0)
-
-        def warm_tensor(moving, count):
-            if "idle" not in bank:
-                bank["idle"] = psum.tile([P, HALF], F32, name="bank7")
-            for n in range(count):
-                nc.tensor.matmul(bank["idle"][:], lhsT=k_raw[0, 0, 0][:, 0, :P], rhs=moving, start=True, stop=True)
-
-        def last_stores():
-            rows_out = out[1].rearrange("(p r) e -> p r e", r=8)
-            groups = [[(2, 0, True)],
-                      [(2, 2, True), (2, 4, False)],
-                      [(2, 6, True), (3, 6, False)],
-                      [(3, 0, True), (3, 2, False), (3, 4, True)]]
-            for banks in groups:
-                (n0, row0, e0), (n1, row1, e1) = banks[0], banks[-1]
-                rows, width = row1 - row0 + 2, (n1 - n0 + 1) * QUARTER
-                t = work.tile([P, rows, width], F32, name="res", bufs=4)
-                for n, row, on_scalar in banks:
-                    key = ("o", 1, n, row)
-                    x = take_bank(key, [P, 2, QUARTER])
-                    for r in range(2):
-                        out_passes(x[:, r, :], 1, row + r, [(G, codes["m", 1, n], slice(G * QUARTER, (G + 1) * QUARTER)) for G in range(2)])
-                    evacuate(t[:, row - row0:row - row0 + 2, (n - n0) * QUARTER:(n - n0 + 1) * QUARTER], x[:], on_scalar)
-                    emptied(key)
-                nc.sync.dma_start(out=rows_out[:, row0:row0 + rows, n0 * QUARTER:n0 * QUARTER + width], in_=t[:])
-
-        load_v(0, 0)
-        load_k_half(0, 0, 0)
-        load_q(0, 0)
+        load_v_rows(0, 0, 0)
+        load_v_rows(0, 0, 2)
         load_v(0, 1)
-        load_k_half(0, 0, 1)
-        load_q_pair(0, 1)
-        load_k_half(0, 1, 0)
-        load_k_half(0, 1, 1)
-        load_q(0, 3)
-        load_q_pair(1, 0)
-        load_k(1, 0)
-        load_k(1, 1)
-        v_widen(0, 0, False)
-        v_interleave(0, 0)
-        k_interleave(0, 0, 0)
-        quantise(("v", 0, 0, 0))
-        quantise(("k", 0, 0, 0))
-        k_interleave(0, 0, 1)
-        v_widen(1, 0, True)
-        q_transpose(0, 0)
-        v_widen(0, 1, True)
-        v_interleave(0, 1)
-        quantise(("k", 0, 0, 1))
-        quantise(("v", 0, 0, 1))
-        k_interleave(0, 1, 0)
-        v_widen(1, 1, False, range(3, 4))
-        k_interleave(0, 1, 1)
-        quantise(("k", 0, 1, 0))
-        quantise(("k", 0, 1, 1))
-        v_interleave(1, 0)
-        q_out(0, 0)
-        v_widen(1, 1, True, range(0, 3))
-        v_interleave(1, 1)
-        quantise(("v", 0, 1, 0))
-        quantise(("v", 0, 1, 1))
-        quantise(("q", 0, 0))
-        stage1_half(0, 0, (0,), (0, 1))
-        q_transpose(0, 1)
-        q_out(0, 1)
-        stage1_half(0, 0, (1,), (0,))
-        q_transpose(0, 2)
-        q_out(0, 2)
-        load_q_pair(1, 2)
+        load_k(0, 0, 0, 1)
+        load_k(0, 1, 0, 1)
+        load_q(0, 0, 1)
+        load_q(0, 1, 1)
+        load_k(0, 0, 1, 1)
+        load_q(0, 2, 1)
+        load_k(0, 1, 1, 1)
+        load_q(0, 3, 1)
+        load_q(1, 0, 2)
+        load_k(1, 0, 0, 2)
+        load_k(1, 1, 0, 2)
         load_v(1, 0)
+        v_widen((0, (0,), 4, 4), 0, (0, 1, 2), True)
+        v_widen((0, (0,), 0, 4), 0, (0, 1, 2, 3), False)
+        v_widen((0, (0,), 4, 4), 0, (3,), False)
+        v_widen((0, (1,), 0, 4), 1, (0, 1, 2, 3), False)
+        v_weave((0, (0,), 0, 4), 0)
+        v_widen((0, (1,), 4, 4), 1, (0, 1), True)
+        v_weave((0, (0,), 0, 4), 1)
+        k_interleave(0, 0, 0)
+        v_weave_out((0, (0,), 0, 4), 0, True)
+        v_widen((0, (1,), 4, 4), 1, (2,), True)
+        v_weave((0, (1,), 0, 4), 0)
+        k_interleave(0, 0, 1)
+        v_weave_out((0, (0,), 0, 4), 1, True)
+        v_widen((0, (1,), 4, 4), 1, (3,), True)
         load_v(1, 1)
-        stage1_half(0, 0, (1,), (1,))
-        quantise(("m", 0, 0, 0))
-        q_transpose(0, 3)
-        q_out(0, 3)
-        stage1_half(1, 0, (0, 1), (0, 1))
-        quantise(("m", 0, 1, 0))
-        quantise(("q", 0, 1))
-        quantise(("q", 0, 2))
-        quantise(("q", 0, 3))
+        v_weave((0, (1,), 0, 4), 1)
+        k_quantise(0, 0, 0)
+        v_weave_out((0, (1,), 0, 4), 0, True)
+        v_quantise((0, (0,), 0, 4))
+        q_transpose(0, 0, 0)
+        k_quantise(0, 0, 1)
+        v_weave_out((0, (1,), 0, 4), 1, True)
+        q_transpose(0, 0, 1)
+        q_out(0, 0, 0, True)
+        q_transpose(0, 1, 0)
+        v_quantise((0, (1,), 0, 4))
+        q_out(0, 0, 1, True)
+        kv_passes(0, 0, 0, 0)
+        k_interleave(0, 1, 0)
+        kv_passes(0, 0, 1, 0)
+        q_out(0, 1, 0, True)
+        kv_passes(0, 0, 2, 0)
+        v_interleave((0, (1,), 4, 4), (0, 2), True)
+        kv_passes(0, 0, 3, 0)
+        kv_passes(0, 0, 0, 1)
+        v_interleave((0, (0,), 4, 4))
+        kv_passes(0, 0, 1, 1)
+        q_transpose(0, 1, 1)
+        kv_out((0, (0,), 0, 4), 0, 0, True)
+        q_transpose(0, 2, 0)
+        k_interleave(0, 1, 1)
+        kv_out((0, (0,), 0, 4), 0, 1, True)
+        q_transpose(0, 2, 1)
+        q_out(0, 1, 1, True)
+        kv_passes(0, 0, 2, 1)
+        k_quantise(0, 1, 0)
+        q_out(0, 2, 0, True)
+        kv_passes(0, 0, 3, 1)
+        q_transpose(0, 3, 0)
+        k_quantise(0, 1, 1)
+        q_out(0, 2, 1, True)
+        q_transpose(0, 3, 1)
+        kv_out((0, (0,), 0, 4), 0, 2, True)
+        v_interleave((0, (1,), 4, 4), (2, 4), False)
+        kv_passes(0, 1, 0, 0)
+        kv_out((0, (0,), 0, 4), 0, 3, True)
+        kv_passes(0, 1, 0, 1)
+        q_out(0, 3, 0, True)
+        v_quantise((0, (0,), 4, 4))
+        kv_passes(0, 1, 1, 0)
+        q_out(0, 3, 1, True)
+        q_shuffle(1, 0)
+        kv_passes(0, 1, 1, 1)
+        kv_out((0, (1,), 0, 4), 1, 0, True)
+        kv_passes(0, 1, 2, 0)
+        q_shuffle(1, 1)
+        load_q(1, 2, 2)
+        kv_out((0, (1,), 0, 4), 1, 1, True)
+        v_quantise((0, (1,), 4, 4))
+        kv_passes(0, 1, 2, 1)
+        kv_passes(0, 1, 3, 0)
+        q_quantise(0, 0)
+        kv_out((0, (1,), 0, 4), 1, 2, True)
+        kv_passes(0, 1, 3, 1)
+        kv_quantise((0, (0,), 0, 4))
+        q_transpose(1, 0, 0)
+        kv_out((0, (1,), 0, 4), 1, 3, True)
+        q_transpose(1, 0, 1)
+        q_out(1, 0, 0, True)
+        q_transpose(1, 1, 0)
+        kv_quantise((0, (1,), 0, 4))
+        q_out(1, 0, 1, True)
+        q_transpose(1, 1, 1)
+        q_quantise(0, 1)
+        q_out(1, 1, 0, True)
+        kv_passes(0, 0, 4, 0)
+        q_quantise(0, 2)
+        q_out(1, 1, 1, True)
+        kv_passes(0, 0, 4, 1)
+        q_quantise(0, 3)
+        kv_passes(0, 0, 5, 0)
+        kv_out((0, (0,), 4, 4), 0, 4, True)
         k_interleave(1, 0, 0)
+        kv_passes(0, 0, 5, 1)
+        kv_passes(0, 0, 6, 0)
+        kv_out((0, (0,), 4, 4), 0, 5, True)
+        kv_passes(0, 0, 6, 1)
         k_interleave(1, 0, 1)
-        quantise(("k", 1, 0, 0))
-        quantise(("k", 1, 0, 1))
-        v_widen_part(0, (0, 1), False)
-        q_transpose(1, 0)
-        q_out(1, 0)
-        stage1_half(0, 1, (0, 1), (0, 1))
-        quantise(("m", 0, 0, 1))
-        v_interleave_part(0)
-        quantise(("q", 1, 0))
-        quantise(("v", 1, 0))
+        kv_passes(0, 0, 7, 0)
+        kv_out((0, (0,), 4, 4), 0, 6, True)
+        kv_passes(0, 0, 7, 1)
+        out_passes(0, 0, 1, 0, 4, (0, 1))
+        kv_out((0, (0,), 4, 4), 0, 7, True)
+        out_passes(0, 1, 1, 0, 4, (0, 1))
+        out_copy((0, 0, 2, 0, 4), 0, 1, 0, 4, True)
+        out_passes(0, 2, 1, 0, 4, (0, 1))
+        kv_quantise((0, (0,), 4, 4))
+        out_copy((0, 0, 2, 0, 4), 1, 1, 0, 4, True)
+        out_passes(0, 3, 1, 0, 4, (0, 1))
+        k_quantise(1, 0, 0)
+        out_copy((0, 2, 2, 0, 4), 2, 1, 0, 4, True)
+        kv_passes(0, 1, 4, 0)
+        store((0, 0, 2, 0, 4))
+        k_quantise(1, 0, 1)
+        out_copy((0, 2, 2, 0, 4), 3, 1, 0, 4, True)
+        kv_passes(0, 1, 4, 1)
+        q_shuffle(1, 2)
+        kv_passes(0, 1, 5, 0)
+        store((0, 2, 2, 0, 4))
+        kv_out((0, (1,), 4, 4), 1, 4, True)
+        v_widen((1, (0, 1), 0, 2), 0, (0, 1, 2, 3), False)
+        kv_passes(0, 1, 5, 1)
+        v_widen((1, (0, 1), 0, 2), 1, (0, 1, 2, 3), False)
+        kv_passes(0, 1, 6, 0)
+        kv_out((0, (1,), 4, 4), 1, 5, True)
         k_interleave(1, 1, 0)
+        kv_passes(0, 1, 6, 1)
+        kv_passes(0, 1, 7, 0)
+        kv_out((0, (1,), 4, 4), 1, 6, True)
+        kv_passes(0, 1, 7, 1)
+        out_passes(0, 4, 1, 0, 4, (0, 1))
+        kv_out((0, (1,), 4, 4), 1, 7, True)
+        out_passes(0, 5, 1, 0, 4, (0, 1))
+        out_copy((0, 4, 2, 0, 4), 4, 1, 0, 4, True)
+        out_passes(0, 6, 1, 0, 4, (0, 1))
+        kv_quantise((0, (1,), 4, 4))
+        out_copy((0, 4, 2, 0, 4), 5, 1, 0, 4, True)
+        out_passes(0, 7, 1, 0, 4, (0, 1))
+        v_interleave((1, (0, 1), 0, 2))
+        out_copy((0, 6, 2, 0, 4), 6, 1, 0, 4, True)
+        q_transpose(1, 2, 0)
+        store((0, 4, 2, 0, 4))
+        out_copy((0, 6, 2, 0, 4), 7, 1, 0, 4, True)
+        q_transpose(1, 2, 1)
         k_interleave(1, 1, 1)
-        q_transpose(1, 1)
-        q_out(1, 1)
-        stage2_half(0, range(0, 8))
-        stage1_half(1, 1, (0, 1), (0, 1))
-        quantise(("m", 0, 1, 1))
-        quantise(("k", 1, 1, 0))
-        quantise(("k", 1, 1, 1))
-        v_widen_part(1, (0, 1), False)
-        quantise(("q", 1, 1))
-        v_interleave_part(1)
-        q_transpose(1, 2)
-        q_out(1, 2)
-        quantise(("q", 1, 2))
-        quantise(("v", 1, 1))
-        v_widen_part(2, (0, 1), False)
-        stage1_part(0, (True, True, True, True,), (0,))
-        q_transpose(1, 3)
-        q_out(1, 3)
-        stage2_half(1, range(0, 4))
-        stage1_part(0, (True, True, True, True,), (1,))
-        quantise(("m", 1, 0))
-        quantise(("q", 1, 3))
-        v_interleave_part(2)
-        v_widen_part(3, (0,), False)
-        quantise(("v", 1, 2))
-        v_widen_part(3, (1,), False)
-        stage2_half(1, range(4, 8))
-        stage1_part(1, (True, True, True, True,), (0, 1))
-        quantise(("m", 1, 1))
-        v_interleave_part(3)
-        quantise(("v", 1, 3))
-        stage2_part(0, 0, 2, (True, True, True, True,))
-        stage1_part(2, (True, True, True, True,), (0, 1))
-        quantise(("m", 1, 2))
-        stage2_part(1, 0, 2, (True, True, False, True,))
-        stage1_part(3, (True, False, True, False,), (0, 1))
-        quantise(("m", 1, 3))
-        last_stores()
+        q_out(1, 2, 0, True)
+        q_transpose(1, 3, 0)
+        store((0, 6, 2, 0, 4))
+        q_out(1, 2, 1, True)
+        q_transpose(1, 3, 1)
+        v_quantise((1, (0, 1), 0, 2))
+        q_out(1, 3, 0, True)
+        out_passes(0, 0, 1, 4, 4, (0, 1))
+        v_widen((1, (0, 1), 2, 2), 0, (0, 1, 2, 3), False)
+        q_out(1, 3, 1, True)
+        out_passes(0, 1, 1, 4, 4, (0, 1))
+        v_widen((1, (0, 1), 2, 2), 1, (0, 1, 2, 3), False)
+        out_copy((0, 0, 2, 4, 4), 0, 1, 4, 4, True)
+        out_passes(0, 2, 1, 4, 4, (0, 1))
+        k_quantise(1, 1, 0)
+        out_copy((0, 0, 2, 4, 4), 1, 1, 4, 4, True)
+        out_passes(0, 3, 1, 4, 4, (0, 1))
+        out_copy((0, 2, 2, 4, 4), 2, 1, 4, 4, True)
+        v_interleave((1, (0, 1), 2, 2))
+        out_passes(0, 4, 1, 4, 4, (0, 1))
+        store((0, 0, 2, 4, 4))
+        out_copy((0, 2, 2, 4, 4), 3, 1, 4, 4, True)
+        out_passes(0, 5, 1, 4, 4, (0, 1))
+        out_copy((0, 4, 2, 4, 4), 4, 1, 4, 4, True)
+        k_quantise(1, 1, 1)
+        out_passes(0, 6, 1, 4, 4, (0, 1))
+        store((0, 2, 2, 4, 4))
+        out_copy((0, 4, 2, 4, 4), 5, 1, 4, 4, True)
+        v_quantise((1, (0, 1), 2, 2))
+        out_passes(0, 7, 1, 4, 4, (0, 1))
+        out_copy((0, 6, 2, 4, 4), 6, 1, 4, 4, True)
+        q_quantise(1, 0)
+        kv_passes(1, 0, 0, 0)
+        store((0, 4, 2, 4, 4))
+        out_copy((0, 6, 2, 4, 4), 7, 1, 4, 4, True)
+        q_quantise(1, 1)
+        kv_passes(1, 0, 0, 1)
+        kv_passes(1, 0, 1, 0)
+        q_quantise(1, 2)
+        store((0, 6, 2, 4, 4))
+        kv_out((1, (0, 1), 0, 2), 0, 0, True)
+        kv_passes(1, 0, 1, 1)
+        kv_passes(1, 1, 0, 0)
+        kv_out((1, (0, 1), 0, 2), 0, 1, True)
+        kv_passes(1, 1, 0, 1)
+        kv_passes(1, 1, 1, 0)
+        kv_out((1, (0, 1), 0, 2), 1, 0, True)
+        kv_passes(1, 1, 1, 1)
+        kv_passes(1, 0, 2, 0)
+        kv_out((1, (0, 1), 0, 2), 1, 1, True)
+        kv_passes(1, 0, 2, 1)
+        kv_passes(1, 0, 3, 0)
+        kv_quantise((1, (0, 1), 0, 2))
+        kv_out((1, (0, 1), 2, 2), 0, 2, True)
+        kv_passes(1, 0, 3, 1)
+        q_quantise(1, 3)
+        kv_passes(1, 1, 2, 0)
+        kv_out((1, (0, 1), 2, 2), 0, 3, True)
+        v_widen((1, (0, 1), 4, 2), 0, (0, 1, 2, 3), False)
+        kv_passes(1, 1, 2, 1)
+        kv_passes(1, 1, 3, 0)
+        v_widen((1, (0, 1), 4, 2), 1, (0, 1, 2, 3), False)
+        kv_out((1, (0, 1), 2, 2), 1, 2, True)
+        kv_passes(1, 1, 3, 1)
+        out_passes(1, 0, 2, 0, 2, (0, 1))
+        kv_out((1, (0, 1), 2, 2), 1, 3, True)
+        out_passes(1, 2, 2, 0, 2, (0, 1))
+        out_copy((1, 0, 4, 0, 2), 0, 2, 0, 2, True)
+        out_passes(1, 4, 2, 0, 2, (0, 1))
+        kv_quantise((1, (0, 1), 2, 2))
+        out_copy((1, 0, 4, 0, 2), 2, 2, 0, 2, True)
+        out_passes(1, 6, 2, 0, 2, (0, 1))
+        v_interleave((1, (0, 1), 4, 2))
+        out_copy((1, 4, 4, 0, 2), 4, 2, 0, 2, True)
+        out_passes(1, 0, 2, 2, 2, (0, 1))
+        store((1, 0, 4, 0, 2))
+        out_copy((1, 4, 4, 0, 2), 6, 2, 0, 2, True)
+        out_passes(1, 2, 2, 2, 2, (0, 1))
+        v_widen((1, (0, 1), 6, 1), 0, (0, 1, 2, 3), False)
+        out_copy((1, 0, 4, 2, 2), 0, 2, 2, 2, True)
+        v_widen((1, (0, 1), 6, 1), 1, (0, 1, 2, 3), False)
+        out_passes(1, 4, 2, 2, 2, (0, 1))
+        store((1, 4, 4, 0, 2))
+        v_quantise((1, (0, 1), 4, 2))
+        out_copy((1, 0, 4, 2, 2), 2, 2, 2, 2, True)
+        out_passes(1, 6, 2, 2, 2, (0, 1))
+        v_interleave((1, (0, 1), 6, 1))
+        out_copy((1, 4, 4, 2, 2), 4, 2, 2, 2, True)
+        kv_passes(1, 0, 4, 0)
+        store((1, 0, 4, 2, 2))
+        v_widen((1, (0, 1), 7, 1), 0, (0, 1, 2, 3), False)
+        out_copy((1, 4, 4, 2, 2), 6, 2, 2, 2, True)
+        v_widen((1, (0, 1), 7, 1), 1, (0, 1, 2, 3), False)
+        kv_passes(1, 0, 4, 1)
+        v_quantise((1, (0, 1), 6, 1))
+        kv_passes(1, 0, 5, 0)
+        v_interleave((1, (0, 1), 7, 1))
+        store((1, 4, 4, 2, 2))
+        kv_out((1, (0, 1), 4, 2), 0, 4, True)
+        kv_passes(1, 0, 5, 1)
+        kv_passes(1, 1, 4, 0)
+        v_quantise((1, (0, 1), 7, 1))
+        kv_out((1, (0, 1), 4, 2), 0, 5, True)
+        kv_passes(1, 1, 4, 1)
+        kv_passes(1, 1, 5, 0)
+        kv_out((1, (0, 1), 4, 2), 1, 4, True)
+        kv_passes(1, 1, 5, 1)
+        kv_passes(1, 0, 6, 0)
+        kv_out((1, (0, 1), 4, 2), 1, 5, True)
+        kv_passes(1, 0, 6, 1)
+        kv_passes(1, 1, 6, 0)
+        kv_quantise((1, (0, 1), 4, 2))
+        kv_out((1, (0, 1), 6, 2), 0, 6, True)
+        kv_passes(1, 1, 6, 1)
+        kv_passes(1, 0, 7, 0)
+        kv_out((1, (0, 1), 6, 2), 1, 6, False)
+        kv_passes(1, 0, 7, 1)
+        kv_passes(1, 1, 7, 0)
+        kv_out((1, (0, 1), 6, 2), 0, 7, True)
+        kv_passes(1, 1, 7, 1)
+        out_passes(1, 0, 2, 4, 2, (0, 1))
+        kv_out((1, (0, 1), 6, 2), 1, 7, False)
+        out_passes(1, 2, 2, 4, 2, (0, 1))
+        out_copy((1, 0, 2, 4, 2), 0, 2, 4, 2, True)
+        out_passes(1, 4, 2, 4, 2, (0, 1))
+        kv_quantise((1, (0, 1), 6, 2))
+        out_copy((1, 2, 4, 4, 2), 2, 2, 4, 2, True)
+        out_passes(1, 6, 2, 4, 2, (0, 1))
+        store((1, 0, 2, 4, 2))
+        out_copy((1, 2, 4, 4, 2), 4, 2, 4, 2, False)
+        out_passes(1, 6, 2, 6, 2, (0, 1))
+        out_copy((1, 6, 2, 4, 4), 6, 2, 4, 2, True)
+        out_passes(1, 0, 2, 6, 2, (0, 1))
+        store((1, 2, 4, 4, 2))
+        out_copy((1, 6, 2, 4, 4), 6, 2, 6, 2, False)
+        out_passes(1, 2, 2, 6, 2, (0, 1))
+        out_copy((1, 0, 6, 6, 2), 0, 2, 6, 2, True)
+        out_passes(1, 4, 2, 6, 2, (0, 1))
+        store((1, 6, 2, 4, 4))
+        out_copy((1, 0, 6, 6, 2), 2, 2, 6, 2, False)
+        out_copy((1, 0, 6, 6, 2), 4, 2, 6, 2, True)
+        store((1, 0, 6, 6, 2))

@@ -31,7 +31,7 @@ def tile_efficientattention_kernel(tc, q, k, v_bytes, v_scale, out):
         psum = ctx.enter_context(tc.psum_pool(name="psum", bufs=1))
         ctx.enter_context(tc.manual_schedule())
 
-        bufs = {'v_raw': 2, 'q_raw1': 4, 'q_raw2': 1, 'k_grp': 2, 'v_wide': 4, 'v_grp': 3, 'q_grp': 6, 'm_grp': 3, 'q_split': 2, 'res1': 1, 'res2': 4, 'res3': 1, 'codes_k': 4, 'codes_v': 4, 'codes_q': 6, 'codes_m': 4}
+        bufs = {'v_raw': 2, 'q_raw1': 2, 'q_raw2': 3, 'k_grp': 2, 'v_wide': 4, 'v_grp': 3, 'q_grp': 6, 'm_grp': 3, 'q_split': 2, 'res1': 1, 'res2': 4, 'res3': 1, 'codes_k': 4, 'codes_v': 4, 'codes_q': 6, 'codes_m': 4}
 
         scl = keep.tile([P, 2, PACK], F32, name="scl")
         nc.scalar.dma_start(out=scl[:], in_=v_scale.rearrange("o (g p j) x -> p (o g) (j x)", p=P, j=PACK))
@@ -222,13 +222,12 @@ def tile_efficientattention_kernel(tc, q, k, v_bytes, v_scale, out):
 
         load_v_rows(0, 0, 0)
         load_v_rows(0, 0, 2)
-        load_v(0, 1)
         load_k(0, 0, 0, 1)
-        load_k(0, 1, 0, 1)
+        load_v(0, 1)
         load_q(0, 0, 1)
-        load_q(0, 1, 1)
+        load_k(0, 1, 0, 1)
+        load_q(0, 1, 2)
         load_k(0, 0, 1, 1)
-        load_q(0, 2, 1)
         load_k(0, 1, 1, 1)
         load_q(0, 3, 1)
         load_q(1, 0, 2)
@@ -238,79 +237,74 @@ def tile_efficientattention_kernel(tc, q, k, v_bytes, v_scale, out):
         v_widen((0, (0,), 4, 4), 0, (0, 1, 2), True)
         v_widen((0, (0,), 0, 4), 0, (0, 1, 2, 3), False)
         v_widen((0, (0,), 4, 4), 0, (3,), False)
-        v_widen((0, (1,), 0, 4), 1, (0, 1, 2, 3), False)
-        v_weave((0, (0,), 0, 4), 0)
-        v_widen((0, (1,), 4, 4), 1, (0, 1), True)
-        v_weave((0, (0,), 0, 4), 1)
         k_interleave(0, 0, 0)
-        v_weave_out((0, (0,), 0, 4), 0, True)
-        v_widen((0, (1,), 4, 4), 1, (2,), True)
-        v_weave((0, (1,), 0, 4), 0)
-        k_interleave(0, 0, 1)
-        v_weave_out((0, (0,), 0, 4), 1, True)
-        v_widen((0, (1,), 4, 4), 1, (3,), True)
-        load_v(1, 1)
-        v_weave((0, (1,), 0, 4), 1)
-        k_quantise(0, 0, 0)
-        v_weave_out((0, (1,), 0, 4), 0, True)
-        v_quantise((0, (0,), 0, 4))
-        q_transpose(0, 0, 0)
-        k_quantise(0, 0, 1)
-        v_weave_out((0, (1,), 0, 4), 1, True)
-        q_transpose(0, 0, 1)
-        q_out(0, 0, 0, True)
-        q_transpose(0, 1, 0)
-        v_quantise((0, (1,), 0, 4))
-        q_out(0, 0, 1, True)
-        kv_passes(0, 0, 0, 0)
-        k_interleave(0, 1, 0)
-        kv_passes(0, 0, 1, 0)
-        q_out(0, 1, 0, True)
-        kv_passes(0, 0, 2, 0)
-        v_interleave((0, (1,), 4, 4), (0, 2), True)
-        kv_passes(0, 0, 3, 0)
-        kv_passes(0, 0, 0, 1)
+        v_weave((0, (0,), 0, 4), 0)
+        v_weave((0, (0,), 0, 4), 1)
         v_interleave((0, (0,), 4, 4))
-        kv_passes(0, 0, 1, 1)
+        v_weave_out((0, (0,), 0, 4), 0, True)
+        v_widen((0, (1,), 0, 4), 1, (0,), True)
+        q_transpose(0, 0, 0)
+        k_quantise(0, 0, 0)
+        v_weave_out((0, (0,), 0, 4), 1, True)
+        q_transpose(0, 0, 1)
+        v_widen((0, (1,), 0, 4), 1, (1, 2, 3), True)
+        v_quantise((0, (0,), 0, 4))
+        k_interleave(0, 0, 1)
+        kv_passes(0, 0, 0, 0)
+        kv_passes(0, 0, 1, 0)
+        q_out(0, 0, 0, True)
+        kv_passes(0, 0, 2, 0)
+        v_interleave((0, (1,), 0, 4))
+        kv_passes(0, 0, 3, 0)
+        q_out(0, 0, 1, True)
+        q_transpose(0, 1, 0)
+        v_widen((0, (1,), 4, 4), 1, (0, 1, 2, 3), True)
+        load_v(1, 1)
+        load_q(1, 2, 2)
         q_transpose(0, 1, 1)
-        kv_out((0, (0,), 0, 4), 0, 0, True)
+        k_quantise(0, 0, 1)
+        v_quantise((0, (1,), 0, 4))
+        k_interleave(0, 1, 0)
+        kv_passes(0, 0, 0, 1)
+        q_out(0, 1, 0, True)
+        kv_passes(0, 0, 1, 1)
         q_transpose(0, 2, 0)
-        k_interleave(0, 1, 1)
-        kv_out((0, (0,), 0, 4), 0, 1, True)
-        q_transpose(0, 2, 1)
         q_out(0, 1, 1, True)
+        v_quantise((0, (0,), 4, 4))
+        q_transpose(0, 2, 1)
+        kv_out((0, (0,), 0, 4), 0, 0, True)
+        k_interleave(0, 1, 1)
         kv_passes(0, 0, 2, 1)
-        k_quantise(0, 1, 0)
-        q_out(0, 2, 0, True)
+        kv_out((0, (0,), 0, 4), 0, 1, True)
         kv_passes(0, 0, 3, 1)
         q_transpose(0, 3, 0)
-        k_quantise(0, 1, 1)
-        q_out(0, 2, 1, True)
+        q_out(0, 2, 0, True)
+        k_quantise(0, 1, 0)
         q_transpose(0, 3, 1)
-        kv_out((0, (0,), 0, 4), 0, 2, True)
-        v_interleave((0, (1,), 4, 4), (2, 4), False)
+        q_out(0, 2, 1, True)
+        k_quantise(0, 1, 1)
         kv_passes(0, 1, 0, 0)
+        kv_out((0, (0,), 0, 4), 0, 2, True)
+        v_interleave((0, (1,), 4, 4))
         kv_out((0, (0,), 0, 4), 0, 3, True)
         kv_passes(0, 1, 0, 1)
-        q_out(0, 3, 0, True)
-        v_quantise((0, (0,), 4, 4))
         kv_passes(0, 1, 1, 0)
-        q_out(0, 3, 1, True)
+        q_out(0, 3, 0, True)
         q_shuffle(1, 0)
         kv_passes(0, 1, 1, 1)
-        kv_out((0, (1,), 0, 4), 1, 0, True)
+        q_out(0, 3, 1, True)
         kv_passes(0, 1, 2, 0)
         q_shuffle(1, 1)
-        load_q(1, 2, 2)
-        kv_out((0, (1,), 0, 4), 1, 1, True)
-        v_quantise((0, (1,), 4, 4))
+        kv_out((0, (1,), 0, 4), 1, 0, True)
         kv_passes(0, 1, 2, 1)
+        v_quantise((0, (1,), 4, 4))
+        kv_out((0, (1,), 0, 4), 1, 1, True)
         kv_passes(0, 1, 3, 0)
         q_quantise(0, 0)
         kv_out((0, (1,), 0, 4), 1, 2, True)
         kv_passes(0, 1, 3, 1)
-        kv_quantise((0, (0,), 0, 4))
         q_transpose(1, 0, 0)
+        kv_quantise((0, (0,), 0, 4))
         kv_out((0, (1,), 0, 4), 1, 3, True)
         q_transpose(1, 0, 1)
         q_out(1, 0, 0, True)
@@ -345,15 +339,12 @@ def tile_efficientattention_kernel(tc, q, k, v_bytes, v_scale, out):
         out_copy((0, 0, 2, 0, 4), 1, 1, 0, 4, True)
         out_passes(0, 3, 1, 0, 4, (0, 1))
         k_quantise(1, 0, 0)
-        out_copy((0, 2, 2, 0, 4), 2, 1, 0, 4, True)
         kv_passes(0, 1, 4, 0)
         store((0, 0, 2, 0, 4))
         k_quantise(1, 0, 1)
-        out_copy((0, 2, 2, 0, 4), 3, 1, 0, 4, True)
         kv_passes(0, 1, 4, 1)
         q_shuffle(1, 2)
         kv_passes(0, 1, 5, 0)
-        store((0, 2, 2, 0, 4))
         kv_out((0, (1,), 4, 4), 1, 4, True)
         v_widen((1, (0, 1), 0, 2), 0, (0, 1, 2, 3), False)
         kv_passes(0, 1, 5, 1)
@@ -368,58 +359,58 @@ def tile_efficientattention_kernel(tc, q, k, v_bytes, v_scale, out):
         out_passes(0, 4, 1, 0, 4, (0, 1))
         kv_out((0, (1,), 4, 4), 1, 7, True)
         out_passes(0, 5, 1, 0, 4, (0, 1))
-        out_copy((0, 4, 2, 0, 4), 4, 1, 0, 4, True)
+        out_copy((0, 2, 2, 0, 4), 2, 1, 0, 4, True)
         out_passes(0, 6, 1, 0, 4, (0, 1))
         kv_quantise((0, (1,), 4, 4))
-        out_copy((0, 4, 2, 0, 4), 5, 1, 0, 4, True)
+        out_copy((0, 2, 2, 0, 4), 3, 1, 0, 4, True)
         out_passes(0, 7, 1, 0, 4, (0, 1))
         v_interleave((1, (0, 1), 0, 2))
-        out_copy((0, 6, 2, 0, 4), 6, 1, 0, 4, True)
+        out_copy((0, 4, 2, 0, 4), 4, 1, 0, 4, True)
         q_transpose(1, 2, 0)
-        store((0, 4, 2, 0, 4))
-        out_copy((0, 6, 2, 0, 4), 7, 1, 0, 4, True)
+        store((0, 2, 2, 0, 4))
+        out_copy((0, 4, 2, 0, 4), 5, 1, 0, 4, True)
         q_transpose(1, 2, 1)
         k_interleave(1, 1, 1)
-        q_out(1, 2, 0, True)
+        out_copy((0, 6, 2, 0, 4), 6, 1, 0, 4, True)
         q_transpose(1, 3, 0)
-        store((0, 6, 2, 0, 4))
-        q_out(1, 2, 1, True)
+        store((0, 4, 2, 0, 4))
+        out_copy((0, 6, 2, 0, 4), 7, 1, 0, 4, True)
         q_transpose(1, 3, 1)
         v_quantise((1, (0, 1), 0, 2))
-        q_out(1, 3, 0, True)
+        q_out(1, 2, 0, True)
         out_passes(0, 0, 1, 4, 4, (0, 1))
+        store((0, 6, 2, 0, 4))
         v_widen((1, (0, 1), 2, 2), 0, (0, 1, 2, 3), False)
-        q_out(1, 3, 1, True)
+        q_out(1, 2, 1, True)
         out_passes(0, 1, 1, 4, 4, (0, 1))
         v_widen((1, (0, 1), 2, 2), 1, (0, 1, 2, 3), False)
-        out_copy((0, 0, 2, 4, 4), 0, 1, 4, 4, True)
+        q_out(1, 3, 0, True)
         out_passes(0, 2, 1, 4, 4, (0, 1))
         k_quantise(1, 1, 0)
-        out_copy((0, 0, 2, 4, 4), 1, 1, 4, 4, True)
+        q_out(1, 3, 1, True)
         out_passes(0, 3, 1, 4, 4, (0, 1))
-        out_copy((0, 2, 2, 4, 4), 2, 1, 4, 4, True)
+        out_copy((0, 0, 2, 4, 4), 0, 1, 4, 4, True)
         v_interleave((1, (0, 1), 2, 2))
         out_passes(0, 4, 1, 4, 4, (0, 1))
-        store((0, 0, 2, 4, 4))
-        out_copy((0, 2, 2, 4, 4), 3, 1, 4, 4, True)
+        out_copy((0, 0, 2, 4, 4), 1, 1, 4, 4, True)
         out_passes(0, 5, 1, 4, 4, (0, 1))
-        out_copy((0, 4, 2, 4, 4), 4, 1, 4, 4, True)
+        out_copy((0, 2, 2, 4, 4), 2, 1, 4, 4, True)
         k_quantise(1, 1, 1)
         out_passes(0, 6, 1, 4, 4, (0, 1))
-        store((0, 2, 2, 4, 4))
-        out_copy((0, 4, 2, 4, 4), 5, 1, 4, 4, True)
+        store((0, 0, 2, 4, 4))
+        out_copy((0, 2, 2, 4, 4), 3, 1, 4, 4, True)
         v_quantise((1, (0, 1), 2, 2))
         out_passes(0, 7, 1, 4, 4, (0, 1))
-        out_copy((0, 6, 2, 4, 4), 6, 1, 4, 4, True)
+        out_copy((0, 4, 2, 4, 4), 4, 1, 4, 4, True)
         q_quantise(1, 0)
         kv_passes(1, 0, 0, 0)
-        store((0, 4, 2, 4, 4))
-        out_copy((0, 6, 2, 4, 4), 7, 1, 4, 4, True)
+        store((0, 2, 2, 4, 4))
+        out_copy((0, 4, 2, 4, 4), 5, 1, 4, 4, True)
         q_quantise(1, 1)
         kv_passes(1, 0, 0, 1)
         kv_passes(1, 0, 1, 0)
         q_quantise(1, 2)
-        store((0, 6, 2, 4, 4))
+        store((0, 4, 2, 4, 4))
         kv_out((1, (0, 1), 0, 2), 0, 0, True)
         kv_passes(1, 0, 1, 1)
         kv_passes(1, 1, 0, 0)
@@ -447,37 +438,37 @@ def tile_efficientattention_kernel(tc, q, k, v_bytes, v_scale, out):
         out_passes(1, 0, 2, 0, 2, (0, 1))
         kv_out((1, (0, 1), 2, 2), 1, 3, True)
         out_passes(1, 2, 2, 0, 2, (0, 1))
-        out_copy((1, 0, 4, 0, 2), 0, 2, 0, 2, True)
+        out_copy((0, 6, 2, 4, 4), 6, 1, 4, 4, True)
         out_passes(1, 4, 2, 0, 2, (0, 1))
         kv_quantise((1, (0, 1), 2, 2))
-        out_copy((1, 0, 4, 0, 2), 2, 2, 0, 2, True)
+        out_copy((0, 6, 2, 4, 4), 7, 1, 4, 4, True)
         out_passes(1, 6, 2, 0, 2, (0, 1))
         v_interleave((1, (0, 1), 4, 2))
-        out_copy((1, 4, 4, 0, 2), 4, 2, 0, 2, True)
+        out_copy((1, 0, 4, 0, 2), 0, 2, 0, 2, True)
         out_passes(1, 0, 2, 2, 2, (0, 1))
-        store((1, 0, 4, 0, 2))
-        out_copy((1, 4, 4, 0, 2), 6, 2, 0, 2, True)
+        store((0, 6, 2, 4, 4))
+        out_copy((1, 0, 4, 0, 2), 2, 2, 0, 2, True)
         out_passes(1, 2, 2, 2, 2, (0, 1))
         v_widen((1, (0, 1), 6, 1), 0, (0, 1, 2, 3), False)
-        out_copy((1, 0, 4, 2, 2), 0, 2, 2, 2, True)
+        out_copy((1, 4, 4, 0, 2), 4, 2, 0, 2, True)
         v_widen((1, (0, 1), 6, 1), 1, (0, 1, 2, 3), False)
         out_passes(1, 4, 2, 2, 2, (0, 1))
-        store((1, 4, 4, 0, 2))
+        store((1, 0, 4, 0, 2))
         v_quantise((1, (0, 1), 4, 2))
-        out_copy((1, 0, 4, 2, 2), 2, 2, 2, 2, True)
+        out_copy((1, 4, 4, 0, 2), 6, 2, 0, 2, True)
         out_passes(1, 6, 2, 2, 2, (0, 1))
         v_interleave((1, (0, 1), 6, 1))
-        out_copy((1, 4, 4, 2, 2), 4, 2, 2, 2, True)
+        out_copy((1, 0, 4, 2, 2), 0, 2, 2, 2, True)
         kv_passes(1, 0, 4, 0)
-        store((1, 0, 4, 2, 2))
+        store((1, 4, 4, 0, 2))
         v_widen((1, (0, 1), 7, 1), 0, (0, 1, 2, 3), False)
-        out_copy((1, 4, 4, 2, 2), 6, 2, 2, 2, True)
+        out_copy((1, 0, 4, 2, 2), 2, 2, 2, 2, True)
         v_widen((1, (0, 1), 7, 1), 1, (0, 1, 2, 3), False)
         kv_passes(1, 0, 4, 1)
         v_quantise((1, (0, 1), 6, 1))
         kv_passes(1, 0, 5, 0)
         v_interleave((1, (0, 1), 7, 1))
-        store((1, 4, 4, 2, 2))
+        store((1, 0, 4, 2, 2))
         kv_out((1, (0, 1), 4, 2), 0, 4, True)
         kv_passes(1, 0, 5, 1)
         kv_passes(1, 1, 4, 0)
@@ -490,12 +481,15 @@ def tile_efficientattention_kernel(tc, q, k, v_bytes, v_scale, out):
         kv_passes(1, 0, 6, 0)
         kv_out((1, (0, 1), 4, 2), 1, 5, True)
         kv_passes(1, 0, 6, 1)
+        out_copy((1, 4, 4, 2, 2), 4, 2, 2, 2, True)
         kv_passes(1, 1, 6, 0)
         kv_quantise((1, (0, 1), 4, 2))
-        kv_out((1, (0, 1), 6, 2), 0, 6, True)
+        out_copy((1, 4, 4, 2, 2), 6, 2, 2, 2, True)
         kv_passes(1, 1, 6, 1)
         kv_passes(1, 0, 7, 0)
+        kv_out((1, (0, 1), 6, 2), 0, 6, True)
         kv_out((1, (0, 1), 6, 2), 1, 6, False)
+        store((1, 4, 4, 2, 2))
         kv_passes(1, 0, 7, 1)
         kv_passes(1, 1, 7, 0)
         kv_out((1, (0, 1), 6, 2), 0, 7, True)

@@ -18,6 +18,7 @@ MULT = mybir.AluOpType.mult
 P = 128
 PACK = 4
 HALF = 512
+UNIT = PACK * HALF
 INV = 1.0 / 32.0
 
 
@@ -31,7 +32,7 @@ def tile_efficientattention_kernel(tc, q, k, v_bytes, v_scale, out):
         psum = ctx.enter_context(tc.psum_pool(name="psum", bufs=1))
         ctx.enter_context(tc.manual_schedule())
 
-        bufs = {'v_raw': 2, 'q_raw1': 2, 'q_raw2': 3, 'k_grp': 2, 'v_wide': 4, 'v_grp': 3, 'q_grp': 6, 'm_grp': 3, 'q_split': 2, 'res1': 1, 'res2': 4, 'res3': 1, 'codes_k': 4, 'codes_v': 4, 'codes_q': 6, 'codes_m': 4}
+        bufs = {'v_raw': 2, 'q_raw1': 2, 'q_raw2': 2, 'k_grp': 2, 'v_wide': 3, 'v_grp': 3, 'q_grp': 3, 'm_grp': 3, 'q_split': 2, 'res1': 4, 'res2': 4, 'res3': 1, 'codes_k': 2, 'codes_v': 4, 'codes_q': 3, 'codes_m': 4}
 
         scl = keep.tile([P, 2, PACK], F32, name="scl")
         nc.scalar.dma_start(out=scl[:], in_=v_scale.rearrange("o (g p j) x -> p (o g) (j x)", p=P, j=PACK))
@@ -42,7 +43,7 @@ def tile_efficientattention_kernel(tc, q, k, v_bytes, v_scale, out):
 
         k_raw, v_raw, q_raw, q_split = {}, {}, {}, {}
         v_wide, grouped, res, bank = {}, {}, {}, {}
-        k_codes, v_codes, q_codes, m_codes = {}, {}, {}, {}
+        codes, v_codes, m_codes = {}, {}, {}
 
         free_banks, held = list(range(8)), {}
 
@@ -83,23 +84,26 @@ def tile_efficientattention_kernel(tc, q, k, v_bytes, v_scale, out):
             for n in range(pieces):
                 q_raw[b, first + n] = t[:, 2 * n:2 * n + 2, :]
 
-        def quantise(src, kind):
-            words = src.shape[1] // PACK
-            c = mx.tile([P, words], U32, name="codes_" + kind, align_bytes=64, bufs=bufs["codes_" + kind])
-            s = mx.tile([P, words], U8, name="scales_" + kind, align_bytes=64, bufs=bufs["codes_" + kind])
-            nc.vector.quantize_mx(out=c[:].bitcast(FP8X4), scales=s[:], in_=src[:])
-            return c, s
+        def quantise(key, first, width):
+            kind, words = key[0], grouped[key].shape[1] // PACK
+            if key not in codes:
+                c = mx.tile([P, words], U32, name="codes_" + kind, align_bytes=64, bufs=bufs["codes_" + kind])
+                s = mx.tile([P, words], U8, name="scales_" + kind, align_bytes=64, bufs=bufs["codes_" + kind])
+                codes[key] = (c, s)
+            c, s = codes[key]
+            part = slice(first // PACK, (first + width) // PACK)
+            nc.vector.quantize_mx(out=c[:, part].bitcast(FP8X4), scales=s[:, part], in_=grouped[key][:, first:first + width])
 
         def k_interleave(b, G, g):
-            t = work.tile([P, HALF * PACK], BF16, name="k_grp", align_bytes=64, bufs=bufs["k_grp"])
+            if ("k", b, G) not in grouped:
+                grouped["k", b, G] = work.tile([P, 2 * UNIT], BF16, name="k_grp", align_bytes=64, bufs=bufs["k_grp"])
             nc.vector.tensor_scalar(
-                out=t[:].rearrange("p (t m j) -> p m j t", t=PACK, j=PACK),
+                out=grouped["k", b, G][:, g * UNIT:(g + 1) * UNIT].rearrange("p (t m j) -> p m j t", t=PACK, j=PACK),
                 in0=k_raw[b, G, g].rearrange("p j (m t) -> p m j t", t=PACK),
                 scalar1=INV * INV, scalar2=None, op0=MULT)
-            grouped["k", b, G, g] = t
 
-        def k_quantise(b, G, g):
-            k_codes[b, G, g] = quantise(grouped["k", b, G, g], "k")
+        def k_quantise(b, G, passes):
+            quantise(("k", b, G), passes[0] * UNIT, len(passes) * UNIT)
 
         def v_widen(unit, g, rows, on_scalar):
             b, passes, first, tiles = unit
@@ -112,24 +116,19 @@ def tile_efficientattention_kernel(tc, q, k, v_bytes, v_scale, out):
                 else:
                     nc.vector.tensor_scalar(out=dst, in0=codes, scalar1=scl[:, g, j:j + 1], scalar2=None, op0=MULT)
 
-        def v_interleave(unit, part=None, on_scalar=False):
+        def v_interleave(unit, wide):
             b, passes, first, tiles = unit
-            if ("v", unit) not in grouped:
-                grouped["v", unit] = work.tile([P, len(passes) * PACK * tiles * P], BF16, name="v_grp", align_bytes=64, bufs=bufs["v_grp"])
-            dst = grouped["v", unit][:].rearrange("p (g c i j) -> p g c j i", g=len(passes), i=4, j=PACK)
-            src = v_wide[unit][:].rearrange("p g j (c i) -> p g c j i", i=4)
-            if part is not None:
-                dst, src = dst[:, 0, part[0] * 32:part[1] * 32], src[:, 0, part[0] * 32:part[1] * 32]
-            if on_scalar:
-                nc.scalar.copy(out=dst, in_=src)
-            else:
-                nc.vector.tensor_copy(out=dst, in_=src)
+            t = work.tile([P, len(passes) * PACK * tiles * P], BF16, name="v_grp", align_bytes=64, bufs=bufs["v_grp"])
+            cols = slice((first - wide[2]) * P, (first - wide[2] + tiles) * P)
+            nc.vector.tensor_copy(out=t[:].rearrange("p (g c i j) -> p g c j i", g=len(passes), i=4, j=PACK),
+                                  in_=v_wide[wide][:, passes[0]:passes[-1] + 1, :, cols].rearrange("p g j (c i) -> p g c j i", i=4))
+            grouped["v", unit] = t
 
-        def v_weave(unit, a):
+        def v_weave(unit, a, wide):
             x = take_bank(("w", unit, a), [P, 2, P, PACK], BF16)
             for n in range(2):
                 cols = slice((2 * a + n) * P, (2 * a + n + 1) * P)
-                nc.tensor.matmul(x[:, n].rearrange("p c j -> p j c"), lhsT=ident_bf[:], rhs=v_wide[unit][:, 0, :, cols], start=True, stop=True)
+                nc.tensor.matmul(x[:, n].rearrange("p c j -> p j c"), lhsT=ident_bf[:], rhs=v_wide[wide][:, unit[1][0], :, cols], start=True, stop=True)
 
         def v_weave_out(unit, a, on_scalar):
             if ("v", unit) not in grouped:
@@ -138,10 +137,10 @@ def tile_efficientattention_kernel(tc, q, k, v_bytes, v_scale, out):
 
         def v_quantise(unit):
             b, passes, first, tiles = unit
-            c, s = quantise(grouped["v", unit], "v")
+            quantise(("v", unit), 0, len(passes) * tiles * HALF)
             for n, g in enumerate(passes):
                 for a in range(tiles):
-                    v_codes[b, g, first + a] = (c, s, (n * tiles + a) * P)
+                    v_codes[b, g, first + a] = codes["v", unit] + ((n * tiles + a) * P,)
 
         def q_shuffle(b, i):
             t = work.tile([P, 4, 2, P], F32, name="q_split", bufs=bufs["q_split"])
@@ -161,21 +160,22 @@ def tile_efficientattention_kernel(tc, q, k, v_bytes, v_scale, out):
                     nc.tensor.transpose(x[:, r, u, :], src, ident[:])
 
         def q_out(b, i, G, on_scalar):
-            if ("q", b, i) not in grouped:
-                grouped["q", b, i] = work.tile([P, HALF * PACK], BF16, name="q_grp", align_bytes=64, bufs=bufs["q_grp"])
-            dst = grouped["q", b, i][:, G * 1024:(G + 1) * 1024].bitcast(F32).rearrange("p (r n u) -> p r n u", r=2, u=2)
+            key, at = ("q", b, i // 2), (i % 2) * UNIT + G * 1024
+            if key not in grouped:
+                grouped[key] = work.tile([P, 2 * UNIT], BF16, name="q_grp", align_bytes=64, bufs=bufs["q_grp"])
+            dst = grouped[key][:, at:at + 1024].bitcast(F32).rearrange("p (r n u) -> p r n u", r=2, u=2)
             evacuate(("q", b, i, G), dst, bank["q", b, i, G][:].rearrange("p r u n -> p r n u"), on_scalar)
 
-        def q_quantise(b, i):
-            q_codes[b, i] = quantise(grouped["q", b, i], "q")
+        def q_quantise(b, first, pieces):
+            quantise(("q", b, first // 2), (first % 2) * UNIT, pieces * UNIT)
 
         def kv_passes(b, G, c, g):
             if g == 0:
                 take_bank(("m", b, G, c), [P, PACK, P])
-            kc, ks = k_codes[b, G, g]
+            kc, ks = codes["k", b, G]
             vc, vs, at = v_codes[b, g, c]
             for t in range(PACK):
-                m = slice(t * P, (t + 1) * P)
+                m = slice(g * HALF + t * P, g * HALF + (t + 1) * P)
                 nc.tensor.matmul_mx(out=bank["m", b, G, c][:, t, :], lhsT=kc[:, m].bitcast(FP8X4), lhsT_scale=ks[:, m],
                                     rhs=vc[:, at:at + P].bitcast(FP8X4), rhs_scale=vs[:, at:at + P],
                                     start=(g == 0 and t == 0), stop=(g == 1 and t == PACK - 1))
@@ -188,12 +188,11 @@ def tile_efficientattention_kernel(tc, q, k, v_bytes, v_scale, out):
             dst = grouped["m", unit][:, at * HALF:(at + 1) * HALF].rearrange("p (n t) -> p n t", t=PACK)
             evacuate(("m", b, G, c), dst, bank["m", b, G, c][:].rearrange("p t n -> p n t"), on_scalar)
 
-        def kv_quantise(unit):
+        def kv_quantise(unit, slot, slots):
             b, halves, first, tiles = unit
-            c, s = quantise(grouped["m", unit], "m")
-            for n, G in enumerate(halves):
-                for a in range(tiles):
-                    m_codes[b, G, first + a] = (c, s, (n * tiles + a) * P)
+            quantise(("m", unit), slot * HALF, slots * HALF)
+            for at in range(slot, slot + slots):
+                m_codes[b, halves[at // tiles], first + at % tiles] = codes["m", unit] + (at * P,)
 
         def out_passes(b, row, rows, first, tiles, halves):
             key, width = ("o", b, row, first), tiles * P
@@ -201,9 +200,10 @@ def tile_efficientattention_kernel(tc, q, k, v_bytes, v_scale, out):
                 take_bank(key, [P, rows, width])
             order = [(r, G) for r in range(rows) for G in halves]
             for r, G in order:
-                qc, qs = q_codes[b, (row + r) // 2]
+                qc, qs = codes["q", b, (row + r) // 4]
                 mc, ms, at = m_codes[b, G, first]
-                m = slice(G * 2 * P + ((row + r) % 2) * P, G * 2 * P + ((row + r) % 2 + 1) * P)
+                left = ((row + r) // 2 % 2) * HALF + G * 2 * P + ((row + r) % 2) * P
+                m = slice(left, left + P)
                 nc.tensor.matmul_mx(out=bank[key][:, r, :], lhsT=qc[:, m].bitcast(FP8X4), lhsT_scale=qs[:, m],
                                     rhs=mc[:, at:at + width].bitcast(FP8X4), rhs_scale=ms[:, at:at + width],
                                     start=((r, G) == (0, 0)), stop=((r, G) == (rows - 1, 1)))
@@ -234,35 +234,34 @@ def tile_efficientattention_kernel(tc, q, k, v_bytes, v_scale, out):
         load_k(1, 0, 0, 2)
         load_k(1, 1, 0, 2)
         load_v(1, 0)
-        v_widen((0, (0,), 4, 4), 0, (0, 1, 2), True)
-        v_widen((0, (0,), 0, 4), 0, (0, 1, 2, 3), False)
-        v_widen((0, (0,), 4, 4), 0, (3,), False)
+        v_widen((0, (0, 1), 4, 4), 0, (0, 1, 2), True)
+        v_widen((0, (0, 1), 0, 4), 0, (0, 1, 2, 3), False)
+        v_widen((0, (0, 1), 4, 4), 0, (3,), False)
         k_interleave(0, 0, 0)
-        v_weave((0, (0,), 0, 4), 0)
-        v_weave((0, (0,), 0, 4), 1)
-        v_interleave((0, (0,), 4, 4))
+        v_weave((0, (0,), 0, 4), 0, (0, (0, 1), 0, 4))
+        v_weave((0, (0,), 0, 4), 1, (0, (0, 1), 0, 4))
+        v_interleave((0, (0,), 4, 4), (0, (0, 1), 4, 4))
         v_weave_out((0, (0,), 0, 4), 0, True)
-        v_widen((0, (1,), 0, 4), 1, (0,), True)
+        v_widen((0, (0, 1), 0, 4), 1, (0,), True)
         q_transpose(0, 0, 0)
-        k_quantise(0, 0, 0)
+        k_quantise(0, 0, (0,))
         v_weave_out((0, (0,), 0, 4), 1, True)
         q_transpose(0, 0, 1)
-        v_widen((0, (1,), 0, 4), 1, (1, 2, 3), True)
+        v_widen((0, (0, 1), 0, 4), 1, (1, 2, 3), True)
         v_quantise((0, (0,), 0, 4))
         k_interleave(0, 0, 1)
         kv_passes(0, 0, 0, 0)
         kv_passes(0, 0, 1, 0)
         q_out(0, 0, 0, True)
         kv_passes(0, 0, 2, 0)
-        v_interleave((0, (1,), 0, 4))
+        v_interleave((0, (1,), 0, 4), (0, (0, 1), 0, 4))
         kv_passes(0, 0, 3, 0)
         q_out(0, 0, 1, True)
         q_transpose(0, 1, 0)
-        v_widen((0, (1,), 4, 4), 1, (0, 1, 2, 3), True)
+        v_widen((0, (0, 1), 4, 4), 1, (0, 1, 2, 3), True)
         load_v(1, 1)
-        load_q(1, 2, 2)
         q_transpose(0, 1, 1)
-        k_quantise(0, 0, 1)
+        k_quantise(0, 0, (1,))
         v_quantise((0, (1,), 0, 4))
         k_interleave(0, 1, 0)
         kv_passes(0, 0, 0, 1)
@@ -272,6 +271,7 @@ def tile_efficientattention_kernel(tc, q, k, v_bytes, v_scale, out):
         q_out(0, 1, 1, True)
         v_quantise((0, (0,), 4, 4))
         q_transpose(0, 2, 1)
+        load_q(1, 2, 2)
         kv_out((0, (0,), 0, 4), 0, 0, True)
         k_interleave(0, 1, 1)
         kv_passes(0, 0, 2, 1)
@@ -279,13 +279,13 @@ def tile_efficientattention_kernel(tc, q, k, v_bytes, v_scale, out):
         kv_passes(0, 0, 3, 1)
         q_transpose(0, 3, 0)
         q_out(0, 2, 0, True)
-        k_quantise(0, 1, 0)
+        k_quantise(0, 1, (0,))
         q_transpose(0, 3, 1)
         q_out(0, 2, 1, True)
-        k_quantise(0, 1, 1)
+        k_quantise(0, 1, (1,))
         kv_passes(0, 1, 0, 0)
         kv_out((0, (0,), 0, 4), 0, 2, True)
-        v_interleave((0, (1,), 4, 4))
+        v_interleave((0, (1,), 4, 4), (0, (0, 1), 4, 4))
         kv_out((0, (0,), 0, 4), 0, 3, True)
         kv_passes(0, 1, 0, 1)
         kv_passes(0, 1, 1, 0)
@@ -300,33 +300,31 @@ def tile_efficientattention_kernel(tc, q, k, v_bytes, v_scale, out):
         v_quantise((0, (1,), 4, 4))
         kv_out((0, (1,), 0, 4), 1, 1, True)
         kv_passes(0, 1, 3, 0)
-        q_quantise(0, 0)
+        q_quantise(0, 0, 2)
         kv_out((0, (1,), 0, 4), 1, 2, True)
         kv_passes(0, 1, 3, 1)
         q_transpose(1, 0, 0)
-        kv_quantise((0, (0,), 0, 4))
         kv_out((0, (1,), 0, 4), 1, 3, True)
         q_transpose(1, 0, 1)
+        kv_quantise((0, (0,), 0, 4), 0, 4)
         q_out(1, 0, 0, True)
         q_transpose(1, 1, 0)
-        kv_quantise((0, (1,), 0, 4))
+        kv_quantise((0, (1,), 0, 4), 0, 4)
         q_out(1, 0, 1, True)
         q_transpose(1, 1, 1)
-        q_quantise(0, 1)
+        q_quantise(0, 2, 2)
         q_out(1, 1, 0, True)
         kv_passes(0, 0, 4, 0)
-        q_quantise(0, 2)
         q_out(1, 1, 1, True)
         kv_passes(0, 0, 4, 1)
-        q_quantise(0, 3)
+        k_interleave(1, 0, 0)
         kv_passes(0, 0, 5, 0)
         kv_out((0, (0,), 4, 4), 0, 4, True)
-        k_interleave(1, 0, 0)
         kv_passes(0, 0, 5, 1)
         kv_passes(0, 0, 6, 0)
+        k_interleave(1, 0, 1)
         kv_out((0, (0,), 4, 4), 0, 5, True)
         kv_passes(0, 0, 6, 1)
-        k_interleave(1, 0, 1)
         kv_passes(0, 0, 7, 0)
         kv_out((0, (0,), 4, 4), 0, 6, True)
         kv_passes(0, 0, 7, 1)
@@ -335,23 +333,24 @@ def tile_efficientattention_kernel(tc, q, k, v_bytes, v_scale, out):
         out_passes(0, 1, 1, 0, 4, (0, 1))
         out_copy((0, 0, 2, 0, 4), 0, 1, 0, 4, True)
         out_passes(0, 2, 1, 0, 4, (0, 1))
-        kv_quantise((0, (0,), 4, 4))
+        kv_quantise((0, (0,), 4, 4), 0, 4)
         out_copy((0, 0, 2, 0, 4), 1, 1, 0, 4, True)
         out_passes(0, 3, 1, 0, 4, (0, 1))
-        k_quantise(1, 0, 0)
+        k_quantise(1, 0, (0, 1))
+        out_copy((0, 2, 2, 0, 4), 2, 1, 0, 4, True)
         kv_passes(0, 1, 4, 0)
         store((0, 0, 2, 0, 4))
-        k_quantise(1, 0, 1)
+        out_copy((0, 2, 2, 0, 4), 3, 1, 0, 4, True)
         kv_passes(0, 1, 4, 1)
-        q_shuffle(1, 2)
+        v_widen((1, (0, 1), 0, 4), 0, (0, 1, 2, 3), False)
         kv_passes(0, 1, 5, 0)
+        store((0, 2, 2, 0, 4))
         kv_out((0, (1,), 4, 4), 1, 4, True)
-        v_widen((1, (0, 1), 0, 2), 0, (0, 1, 2, 3), False)
         kv_passes(0, 1, 5, 1)
-        v_widen((1, (0, 1), 0, 2), 1, (0, 1, 2, 3), False)
+        q_shuffle(1, 2)
         kv_passes(0, 1, 6, 0)
         kv_out((0, (1,), 4, 4), 1, 5, True)
-        k_interleave(1, 1, 0)
+        v_widen((1, (0, 1), 0, 4), 1, (0, 1, 2, 3), False)
         kv_passes(0, 1, 6, 1)
         kv_passes(0, 1, 7, 0)
         kv_out((0, (1,), 4, 4), 1, 6, True)
@@ -359,58 +358,53 @@ def tile_efficientattention_kernel(tc, q, k, v_bytes, v_scale, out):
         out_passes(0, 4, 1, 0, 4, (0, 1))
         kv_out((0, (1,), 4, 4), 1, 7, True)
         out_passes(0, 5, 1, 0, 4, (0, 1))
-        out_copy((0, 2, 2, 0, 4), 2, 1, 0, 4, True)
-        out_passes(0, 6, 1, 0, 4, (0, 1))
-        kv_quantise((0, (1,), 4, 4))
-        out_copy((0, 2, 2, 0, 4), 3, 1, 0, 4, True)
-        out_passes(0, 7, 1, 0, 4, (0, 1))
-        v_interleave((1, (0, 1), 0, 2))
         out_copy((0, 4, 2, 0, 4), 4, 1, 0, 4, True)
-        q_transpose(1, 2, 0)
-        store((0, 2, 2, 0, 4))
+        out_passes(0, 6, 1, 0, 4, (0, 1))
+        kv_quantise((0, (1,), 4, 4), 0, 4)
         out_copy((0, 4, 2, 0, 4), 5, 1, 0, 4, True)
-        q_transpose(1, 2, 1)
-        k_interleave(1, 1, 1)
+        out_passes(0, 7, 1, 0, 4, (0, 1))
+        v_interleave((1, (0, 1), 0, 2), (1, (0, 1), 0, 4))
         out_copy((0, 6, 2, 0, 4), 6, 1, 0, 4, True)
-        q_transpose(1, 3, 0)
+        q_transpose(1, 2, 0)
         store((0, 4, 2, 0, 4))
         out_copy((0, 6, 2, 0, 4), 7, 1, 0, 4, True)
+        q_transpose(1, 2, 1)
+        k_interleave(1, 1, 0)
+        q_out(1, 2, 0, True)
+        q_transpose(1, 3, 0)
+        store((0, 6, 2, 0, 4))
+        q_out(1, 2, 1, True)
         q_transpose(1, 3, 1)
         v_quantise((1, (0, 1), 0, 2))
-        q_out(1, 2, 0, True)
-        out_passes(0, 0, 1, 4, 4, (0, 1))
-        store((0, 6, 2, 0, 4))
-        v_widen((1, (0, 1), 2, 2), 0, (0, 1, 2, 3), False)
-        q_out(1, 2, 1, True)
-        out_passes(0, 1, 1, 4, 4, (0, 1))
-        v_widen((1, (0, 1), 2, 2), 1, (0, 1, 2, 3), False)
         q_out(1, 3, 0, True)
-        out_passes(0, 2, 1, 4, 4, (0, 1))
-        k_quantise(1, 1, 0)
+        out_passes(0, 0, 1, 4, 4, (0, 1))
+        k_interleave(1, 1, 1)
         q_out(1, 3, 1, True)
-        out_passes(0, 3, 1, 4, 4, (0, 1))
+        out_passes(0, 1, 1, 4, 4, (0, 1))
         out_copy((0, 0, 2, 4, 4), 0, 1, 4, 4, True)
-        v_interleave((1, (0, 1), 2, 2))
-        out_passes(0, 4, 1, 4, 4, (0, 1))
+        out_passes(0, 2, 1, 4, 4, (0, 1))
         out_copy((0, 0, 2, 4, 4), 1, 1, 4, 4, True)
-        out_passes(0, 5, 1, 4, 4, (0, 1))
+        k_quantise(1, 1, (0,))
+        out_passes(0, 3, 1, 4, 4, (0, 1))
         out_copy((0, 2, 2, 4, 4), 2, 1, 4, 4, True)
-        k_quantise(1, 1, 1)
-        out_passes(0, 6, 1, 4, 4, (0, 1))
+        v_interleave((1, (0, 1), 2, 2), (1, (0, 1), 0, 4))
+        out_passes(0, 4, 1, 4, 4, (0, 1))
         store((0, 0, 2, 4, 4))
         out_copy((0, 2, 2, 4, 4), 3, 1, 4, 4, True)
-        v_quantise((1, (0, 1), 2, 2))
-        out_passes(0, 7, 1, 4, 4, (0, 1))
+        out_passes(0, 5, 1, 4, 4, (0, 1))
         out_copy((0, 4, 2, 4, 4), 4, 1, 4, 4, True)
-        q_quantise(1, 0)
-        kv_passes(1, 0, 0, 0)
+        k_quantise(1, 1, (1,))
+        out_passes(0, 6, 1, 4, 4, (0, 1))
         store((0, 2, 2, 4, 4))
         out_copy((0, 4, 2, 4, 4), 5, 1, 4, 4, True)
-        q_quantise(1, 1)
+        v_quantise((1, (0, 1), 2, 2))
+        out_passes(0, 7, 1, 4, 4, (0, 1))
+        q_quantise(1, 0, 2)
+        kv_passes(1, 0, 0, 0)
+        store((0, 4, 2, 4, 4))
         kv_passes(1, 0, 0, 1)
         kv_passes(1, 0, 1, 0)
-        q_quantise(1, 2)
-        store((0, 4, 2, 4, 4))
+        q_quantise(1, 2, 1)
         kv_out((1, (0, 1), 0, 2), 0, 0, True)
         kv_passes(1, 0, 1, 1)
         kv_passes(1, 1, 0, 0)
@@ -423,10 +417,10 @@ def tile_efficientattention_kernel(tc, q, k, v_bytes, v_scale, out):
         kv_out((1, (0, 1), 0, 2), 1, 1, True)
         kv_passes(1, 0, 2, 1)
         kv_passes(1, 0, 3, 0)
-        kv_quantise((1, (0, 1), 0, 2))
+        kv_quantise((1, (0, 1), 0, 2), 0, 4)
         kv_out((1, (0, 1), 2, 2), 0, 2, True)
         kv_passes(1, 0, 3, 1)
-        q_quantise(1, 3)
+        q_quantise(1, 3, 1)
         kv_passes(1, 1, 2, 0)
         kv_out((1, (0, 1), 2, 2), 0, 3, True)
         v_widen((1, (0, 1), 4, 2), 0, (0, 1, 2, 3), False)
@@ -440,79 +434,86 @@ def tile_efficientattention_kernel(tc, q, k, v_bytes, v_scale, out):
         out_passes(1, 2, 2, 0, 2, (0, 1))
         out_copy((0, 6, 2, 4, 4), 6, 1, 4, 4, True)
         out_passes(1, 4, 2, 0, 2, (0, 1))
-        kv_quantise((1, (0, 1), 2, 2))
+        kv_quantise((1, (0, 1), 2, 2), 0, 4)
         out_copy((0, 6, 2, 4, 4), 7, 1, 4, 4, True)
         out_passes(1, 6, 2, 0, 2, (0, 1))
-        v_interleave((1, (0, 1), 4, 2))
+        v_interleave((1, (0, 1), 4, 2), (1, (0, 1), 4, 2))
         out_copy((1, 0, 4, 0, 2), 0, 2, 0, 2, True)
         out_passes(1, 0, 2, 2, 2, (0, 1))
         store((0, 6, 2, 4, 4))
         out_copy((1, 0, 4, 0, 2), 2, 2, 0, 2, True)
         out_passes(1, 2, 2, 2, 2, (0, 1))
-        v_widen((1, (0, 1), 6, 1), 0, (0, 1, 2, 3), False)
+        v_widen((1, (0, 1), 6, 2), 0, (0, 1, 2, 3), False)
         out_copy((1, 4, 4, 0, 2), 4, 2, 0, 2, True)
-        v_widen((1, (0, 1), 6, 1), 1, (0, 1, 2, 3), False)
         out_passes(1, 4, 2, 2, 2, (0, 1))
         store((1, 0, 4, 0, 2))
         v_quantise((1, (0, 1), 4, 2))
         out_copy((1, 4, 4, 0, 2), 6, 2, 0, 2, True)
         out_passes(1, 6, 2, 2, 2, (0, 1))
-        v_interleave((1, (0, 1), 6, 1))
+        v_widen((1, (0, 1), 6, 2), 1, (0, 1, 2, 3), False)
         out_copy((1, 0, 4, 2, 2), 0, 2, 2, 2, True)
         kv_passes(1, 0, 4, 0)
         store((1, 4, 4, 0, 2))
-        v_widen((1, (0, 1), 7, 1), 0, (0, 1, 2, 3), False)
         out_copy((1, 0, 4, 2, 2), 2, 2, 2, 2, True)
-        v_widen((1, (0, 1), 7, 1), 1, (0, 1, 2, 3), False)
+        v_interleave((1, (0, 1), 6, 1), (1, (0, 1), 6, 2))
         kv_passes(1, 0, 4, 1)
-        v_quantise((1, (0, 1), 6, 1))
         kv_passes(1, 0, 5, 0)
-        v_interleave((1, (0, 1), 7, 1))
+        v_interleave((1, (0, 1), 7, 1), (1, (0, 1), 6, 2))
         store((1, 0, 4, 2, 2))
         kv_out((1, (0, 1), 4, 2), 0, 4, True)
         kv_passes(1, 0, 5, 1)
+        v_quantise((1, (0, 1), 6, 1))
         kv_passes(1, 1, 4, 0)
         v_quantise((1, (0, 1), 7, 1))
         kv_out((1, (0, 1), 4, 2), 0, 5, True)
         kv_passes(1, 1, 4, 1)
         kv_passes(1, 1, 5, 0)
+        kv_quantise((1, (0, 1), 4, 2), 0, 2)
         kv_out((1, (0, 1), 4, 2), 1, 4, True)
+        out_copy((1, 4, 4, 2, 2), 6, 2, 2, 2, False)
         kv_passes(1, 1, 5, 1)
         kv_passes(1, 0, 6, 0)
         kv_out((1, (0, 1), 4, 2), 1, 5, True)
         kv_passes(1, 0, 6, 1)
         out_copy((1, 4, 4, 2, 2), 4, 2, 2, 2, True)
         kv_passes(1, 1, 6, 0)
-        kv_quantise((1, (0, 1), 4, 2))
-        out_copy((1, 4, 4, 2, 2), 6, 2, 2, 2, True)
+        kv_quantise((1, (0, 1), 4, 2), 2, 2)
+        kv_out((1, (0, 1), 6, 1), 0, 6, True)
         kv_passes(1, 1, 6, 1)
-        kv_passes(1, 0, 7, 0)
-        kv_out((1, (0, 1), 6, 2), 0, 6, True)
-        kv_out((1, (0, 1), 6, 2), 1, 6, False)
         store((1, 4, 4, 2, 2))
+        out_passes(1, 0, 2, 4, 2, (0,))
+        out_passes(1, 2, 2, 4, 2, (0,))
+        kv_out((1, (0, 1), 6, 1), 1, 6, False)
+        out_passes(1, 0, 2, 4, 2, (1,))
+        out_passes(1, 2, 2, 4, 2, (1,))
+        out_passes(1, 4, 2, 4, 2, (0, 1))
+        out_copy((1, 0, 4, 4, 2), 0, 2, 4, 2, True)
+        out_copy((1, 0, 4, 4, 2), 2, 2, 4, 2, False)
+        out_passes(1, 6, 2, 4, 2, (0, 1))
+        out_copy((1, 4, 4, 4, 2), 4, 2, 4, 2, True)
+        kv_quantise((1, (0, 1), 6, 1), 0, 2)
+        kv_passes(1, 0, 7, 0)
+        store((1, 0, 4, 4, 2))
+        out_copy((1, 4, 4, 4, 2), 6, 2, 4, 2, False)
         kv_passes(1, 0, 7, 1)
         kv_passes(1, 1, 7, 0)
-        kv_out((1, (0, 1), 6, 2), 0, 7, True)
+        store((1, 4, 4, 4, 2))
+        kv_out((1, (0, 1), 7, 1), 0, 7, True)
         kv_passes(1, 1, 7, 1)
-        out_passes(1, 0, 2, 4, 2, (0, 1))
-        kv_out((1, (0, 1), 6, 2), 1, 7, False)
-        out_passes(1, 2, 2, 4, 2, (0, 1))
-        out_copy((1, 0, 2, 4, 2), 0, 2, 4, 2, True)
-        out_passes(1, 4, 2, 4, 2, (0, 1))
-        kv_quantise((1, (0, 1), 6, 2))
-        out_copy((1, 2, 4, 4, 2), 2, 2, 4, 2, True)
-        out_passes(1, 6, 2, 4, 2, (0, 1))
-        store((1, 0, 2, 4, 2))
-        out_copy((1, 2, 4, 4, 2), 4, 2, 4, 2, False)
-        out_passes(1, 6, 2, 6, 2, (0, 1))
-        out_copy((1, 6, 2, 4, 4), 6, 2, 4, 2, True)
-        out_passes(1, 0, 2, 6, 2, (0, 1))
-        store((1, 2, 4, 4, 2))
-        out_copy((1, 6, 2, 4, 4), 6, 2, 6, 2, False)
-        out_passes(1, 2, 2, 6, 2, (0, 1))
-        out_copy((1, 0, 6, 6, 2), 0, 2, 6, 2, True)
-        out_passes(1, 4, 2, 6, 2, (0, 1))
-        store((1, 6, 2, 4, 4))
-        out_copy((1, 0, 6, 6, 2), 2, 2, 6, 2, False)
-        out_copy((1, 0, 6, 6, 2), 4, 2, 6, 2, True)
-        store((1, 0, 6, 6, 2))
+        out_passes(1, 0, 4, 6, 1, (0, 1))
+        kv_quantise((1, (0, 1), 7, 1), 0, 1)
+        kv_out((1, (0, 1), 7, 1), 1, 7, True)
+        out_passes(1, 4, 4, 6, 1, (0, 1))
+        out_copy((1, 0, 4, 6, 1), 0, 4, 6, 1, False)
+        out_passes(1, 0, 4, 7, 1, (0,))
+        out_passes(1, 4, 4, 7, 1, (0,))
+        out_copy((1, 4, 4, 6, 1), 4, 4, 6, 1, True)
+        kv_quantise((1, (0, 1), 7, 1), 1, 1)
+        store((1, 0, 4, 6, 1))
+        out_passes(1, 0, 4, 7, 1, (1,))
+        out_passes(1, 4, 4, 7, 1, (1,))
+        store((1, 4, 4, 6, 1))
+        out_copy((1, 0, 4, 7, 1), 0, 4, 7, 1, True)
+        out_copy((1, 4, 4, 7, 1), 4, 4, 7, 1, False)
+        store((1, 0, 4, 7, 1))
+        store((1, 4, 4, 7, 1))

@@ -34,8 +34,9 @@ def tile_efficientattention_kernel(tc, q, k, v_bytes, v_scale, out):
 
         bufs = {'v_raw': 2, 'q_raw1': 2, 'q_raw2': 2, 'k_grp': 2, 'v_wide': 3, 'v_grp': 3, 'q_grp': 3, 'm_grp': 3, 'q_split': 2, 'res1': 4, 'res2': 4, 'res3': 1, 'codes_k': 2, 'codes_v': 4, 'codes_q': 3, 'codes_m': 4}
 
+        row_scale = keep.tile([P, 2, PACK], F32, name="row_scale")
+        nc.scalar.dma_start(out=row_scale[:], in_=v_scale.rearrange("o (g p j) x -> p (o g) (j x)", p=P, j=PACK))
         scl = keep.tile([P, 2, PACK], F32, name="scl")
-        nc.scalar.dma_start(out=scl[:], in_=v_scale.rearrange("o (g p j) x -> p (o g) (j x)", p=P, j=PACK))
         ident = keep.tile([P, P], F32, name="ident")
         make_identity(nc, ident[:])
         ident_bf = keep.tile([P, P], BF16, name="ident_bf")
@@ -97,10 +98,17 @@ def tile_efficientattention_kernel(tc, q, k, v_bytes, v_scale, out):
         def k_interleave(b, G, g):
             if ("k", b, G) not in grouped:
                 grouped["k", b, G] = work.tile([P, 2 * UNIT], BF16, name="k_grp", align_bytes=64, bufs=bufs["k_grp"])
-            nc.vector.tensor_scalar(
-                out=grouped["k", b, G][:, g * UNIT:(g + 1) * UNIT].rearrange("p (t m j) -> p m j t", t=PACK, j=PACK),
-                in0=k_raw[b, G, g].rearrange("p j (m t) -> p m j t", t=PACK),
-                scalar1=INV * INV, scalar2=None, op0=MULT)
+            dst = grouped["k", b, G][:, g * UNIT:(g + 1) * UNIT]
+            if (b, g) == (0, 0):
+                nc.vector.tensor_scalar(out=dst.rearrange("p (t m j) -> p m j t", t=PACK, j=PACK),
+                                        in0=k_raw[b, G, g].rearrange("p j (m t) -> p m j t", t=PACK),
+                                        scalar1=INV * INV, scalar2=None, op0=MULT)
+            else:
+                nc.vector.tensor_copy(out=dst.rearrange("p (t m u e) -> p m u t e", t=PACK, u=2, e=2),
+                                      in_=k_raw[b, G, g].rearrange("p (u e) (m t) -> p m u t e", t=PACK, e=2))
+
+        def fold_factor():
+            nc.vector.tensor_scalar(out=scl[:], in0=row_scale[:], scalar1=INV * INV, scalar2=None, op0=MULT)
 
         def k_quantise(b, G, passes):
             quantise(("k", b, G), passes[0] * UNIT, len(passes) * UNIT)
@@ -109,12 +117,13 @@ def tile_efficientattention_kernel(tc, q, k, v_bytes, v_scale, out):
             b, passes, first, tiles = unit
             if unit not in v_wide:
                 v_wide[unit] = work.tile([P, len(passes), PACK, tiles * P], BF16, name="v_wide", bufs=bufs["v_wide"])
+            scales = row_scale if (b, g) == (0, 0) else scl
             for j in rows:
                 dst, codes = v_wide[unit][:, passes.index(g), j, :], v_raw[b, g, j][:, first * P:(first + tiles) * P].bitcast(FP8)
                 if on_scalar:
-                    nc.scalar.activation(out=dst, in_=codes, func=COPY, scale=scl[:, g, j:j + 1])
+                    nc.scalar.activation(out=dst, in_=codes, func=COPY, scale=scales[:, g, j:j + 1])
                 else:
-                    nc.vector.tensor_scalar(out=dst, in0=codes, scalar1=scl[:, g, j:j + 1], scalar2=None, op0=MULT)
+                    nc.vector.tensor_scalar(out=dst, in0=codes, scalar1=scales[:, g, j:j + 1], scalar2=None, op0=MULT)
 
         def v_interleave(unit, wide):
             b, passes, first, tiles = unit
@@ -127,12 +136,13 @@ def tile_efficientattention_kernel(tc, q, k, v_bytes, v_scale, out):
         def v_weave(unit, a, wide):
             x = take_bank(("w", unit, a), [P, 2, P, PACK], BF16)
             for n in range(2):
-                cols = slice((2 * a + n) * P, (2 * a + n + 1) * P)
+                left = (unit[2] - wide[2] + 2 * a + n) * P
+                cols = slice(left, left + P)
                 nc.tensor.matmul(x[:, n].rearrange("p c j -> p j c"), lhsT=ident_bf[:], rhs=v_wide[wide][:, unit[1][0], :, cols], start=True, stop=True)
 
         def v_weave_out(unit, a, on_scalar):
             if ("v", unit) not in grouped:
-                grouped["v", unit] = work.tile([P, HALF * PACK], BF16, name="v_grp", align_bytes=64, bufs=bufs["v_grp"])
+                grouped["v", unit] = work.tile([P, unit[3] * HALF], BF16, name="v_grp", align_bytes=64, bufs=bufs["v_grp"])
             evacuate(("w", unit, a), grouped["v", unit][:, a * 1024:(a + 1) * 1024], bank["w", unit, a][:].rearrange("p n c j -> p (n c j)"), on_scalar)
 
         def v_quantise(unit):
@@ -151,12 +161,11 @@ def tile_efficientattention_kernel(tc, q, k, v_bytes, v_scale, out):
         def q_transpose(b, i, G):
             x = take_bank(("q", b, i, G), [P, 2, 2, P])
             for r in range(2):
-                words = q_raw[b, i][:, r, :].bitcast(F32)
                 for u in range(2):
                     if (b, i) in q_split:
                         src = q_split[b, i][:, 2 * r + G, u]
                     else:
-                        src = words[:, 256 * G + u:256 * (G + 1):2]
+                        src = q_raw[b, i][:, r, :].bitcast(F32)[:, 256 * G + u:256 * (G + 1):2]
                     nc.tensor.transpose(x[:, r, u, :], src, ident[:])
 
         def q_out(b, i, G, on_scalar):
@@ -237,8 +246,9 @@ def tile_efficientattention_kernel(tc, q, k, v_bytes, v_scale, out):
         v_widen((0, (0, 1), 4, 4), 0, (0, 1, 2), True)
         v_widen((0, (0, 1), 0, 4), 0, (0, 1, 2, 3), False)
         v_widen((0, (0, 1), 4, 4), 0, (3,), False)
-        k_interleave(0, 0, 0)
+        fold_factor()
         v_weave((0, (0,), 0, 4), 0, (0, (0, 1), 0, 4))
+        k_interleave(0, 0, 0)
         v_weave((0, (0,), 0, 4), 1, (0, (0, 1), 0, 4))
         v_interleave((0, (0,), 4, 4), (0, (0, 1), 4, 4))
         v_weave_out((0, (0,), 0, 4), 0, True)
@@ -407,6 +417,7 @@ def tile_efficientattention_kernel(tc, q, k, v_bytes, v_scale, out):
         q_quantise(1, 2, 1)
         kv_out((1, (0, 1), 0, 2), 0, 0, True)
         kv_passes(1, 0, 1, 1)
+        v_widen((1, (0, 1), 4, 2), 0, (0, 1, 2, 3), False)
         kv_passes(1, 1, 0, 0)
         kv_out((1, (0, 1), 0, 2), 0, 1, True)
         kv_passes(1, 1, 0, 1)
@@ -423,10 +434,9 @@ def tile_efficientattention_kernel(tc, q, k, v_bytes, v_scale, out):
         q_quantise(1, 3, 1)
         kv_passes(1, 1, 2, 0)
         kv_out((1, (0, 1), 2, 2), 0, 3, True)
-        v_widen((1, (0, 1), 4, 2), 0, (0, 1, 2, 3), False)
+        v_widen((1, (0, 1), 4, 2), 1, (0, 1, 2, 3), False)
         kv_passes(1, 1, 2, 1)
         kv_passes(1, 1, 3, 0)
-        v_widen((1, (0, 1), 4, 2), 1, (0, 1, 2, 3), False)
         kv_out((1, (0, 1), 2, 2), 1, 2, True)
         kv_passes(1, 1, 3, 1)
         out_passes(1, 0, 2, 0, 2, (0, 1))

@@ -32,7 +32,7 @@ def tile_efficientattention_kernel(tc, q, k, v_bytes, v_scale, out):
         psum = ctx.enter_context(tc.psum_pool(name="psum", bufs=1))
         ctx.enter_context(tc.manual_schedule())
 
-        bufs = {'v_raw': 2, 'q_raw1': 2, 'q_raw2': 2, 'k_grp': 2, 'v_wide': 3, 'v_grp': 3, 'q_grp': 3, 'm_grp': 3, 'q_split': 2, 'res1': 4, 'res2': 4, 'res3': 1, 'codes_k': 2, 'codes_v': 4, 'codes_q': 3, 'codes_m': 4}
+        bufs = {'k_raw': 3, 'v_raw': 2, 'q_raw1': 3, 'q_raw2': 2, 'k_grp': 2, 'v_wide': 3, 'v_grp': 3, 'q_grp': 4, 'm_grp': 3, 'q_split': 2, 'res1': 4, 'res2': 4, 'codes_k': 2, 'codes_v': 4, 'codes_q': 3, 'codes_m': 4}
 
         row_scale = keep.tile([P, 2, PACK], F32, name="row_scale")
         nc.scalar.dma_start(out=row_scale[:], in_=v_scale.rearrange("o (g p j) x -> p (o g) (j x)", p=P, j=PACK))
@@ -42,7 +42,7 @@ def tile_efficientattention_kernel(tc, q, k, v_bytes, v_scale, out):
         ident_bf = keep.tile([P, P], BF16, name="ident_bf")
         make_identity(nc, ident_bf[:])
 
-        k_raw, v_raw, q_raw, q_split = {}, {}, {}, {}
+        k_tile, k_raw, v_raw, q_raw, q_split = {}, {}, {}, {}, {}
         v_wide, grouped, res, bank = {}, {}, {}, {}
         codes, v_codes, m_codes = {}, {}, {}
 
@@ -61,9 +61,13 @@ def tile_efficientattention_kernel(tc, q, k, v_bytes, v_scale, out):
             free_banks.append(held[key])
 
         def load_k(b, g, first, halves):
-            t = raw.tile([P, PACK, halves * HALF], BF16, name="k_raw%d%d%d" % (b, g, first))
+            key = (b, "pass", g) if halves == 2 else (b, "half", first)
+            if key not in k_tile:
+                k_tile[key] = raw.tile([P, 2 * UNIT], BF16, name="k_raw", bufs=bufs["k_raw"])
+            part = k_tile[key][:] if halves == 2 else k_tile[key][:, g * UNIT:(g + 1) * UNIT]
+            t = part.rearrange("p (j d) -> p j d", j=PACK)
             rows = k[b].rearrange("(g p j) d -> g p j d", p=P, j=PACK)[g]
-            nc.sync.dma_start(out=t[:], in_=rows[:, :, first * HALF:(first + halves) * HALF])
+            nc.sync.dma_start(out=t, in_=rows[:, :, first * HALF:(first + halves) * HALF])
             for n in range(halves):
                 k_raw[b, first + n, g] = t[:, :, n * HALF:(n + 1) * HALF]
 
@@ -132,6 +136,13 @@ def tile_efficientattention_kernel(tc, q, k, v_bytes, v_scale, out):
             nc.vector.tensor_copy(out=t[:].rearrange("p (g c i j) -> p g c j i", g=len(passes), i=4, j=PACK),
                                   in_=v_wide[wide][:, passes[0]:passes[-1] + 1, :, cols].rearrange("p g j (c i) -> p g c j i", i=4))
             grouped["v", unit] = t
+
+        def v_interleave_half(unit, a, wide):
+            if ("v", unit) not in grouped:
+                grouped["v", unit] = work.tile([P, UNIT], BF16, name="v_grp", align_bytes=64, bufs=bufs["v_grp"])
+            left = (unit[2] - wide[2] + 2 * a) * P
+            nc.vector.tensor_copy(out=grouped["v", unit][:, a * 1024:(a + 1) * 1024].rearrange("p (c i j) -> p c j i", i=4, j=PACK),
+                                  in_=v_wide[wide][:, unit[1][0], :, left:left + 2 * P].rearrange("p j (c i) -> p c j i", i=4))
 
         def v_weave(unit, a, wide):
             x = take_bank(("w", unit, a), [P, 2, P, PACK], BF16)
@@ -232,192 +243,194 @@ def tile_efficientattention_kernel(tc, q, k, v_bytes, v_scale, out):
         load_v_rows(0, 0, 0)
         load_v_rows(0, 0, 2)
         load_k(0, 0, 0, 1)
-        load_v(0, 1)
         load_q(0, 0, 1)
+        load_v(0, 1)
+        load_q(0, 1, 1)
+        load_q(0, 2, 1)
         load_k(0, 1, 0, 1)
-        load_q(0, 1, 2)
-        load_k(0, 0, 1, 1)
-        load_k(0, 1, 1, 1)
-        load_q(0, 3, 1)
-        load_q(1, 0, 2)
-        load_k(1, 0, 0, 2)
-        load_k(1, 1, 0, 2)
-        load_v(1, 0)
         v_widen((0, (0, 1), 4, 4), 0, (0, 1, 2), True)
         v_widen((0, (0, 1), 0, 4), 0, (0, 1, 2, 3), False)
         v_widen((0, (0, 1), 4, 4), 0, (3,), False)
-        fold_factor()
+        v_interleave_half((0, (0,), 0, 4), 1, (0, (0, 1), 0, 4))
         v_weave((0, (0,), 0, 4), 0, (0, (0, 1), 0, 4))
         k_interleave(0, 0, 0)
-        v_weave((0, (0,), 0, 4), 1, (0, (0, 1), 0, 4))
-        v_interleave((0, (0,), 4, 4), (0, (0, 1), 4, 4))
+        v_weave((0, (0,), 4, 4), 0, (0, (0, 1), 4, 4))
         v_weave_out((0, (0,), 0, 4), 0, True)
-        v_widen((0, (0, 1), 0, 4), 1, (0,), True)
+        fold_factor()
+        v_interleave_half((0, (0,), 4, 4), 1, (0, (0, 1), 4, 4))
         q_transpose(0, 0, 0)
-        k_quantise(0, 0, (0,))
-        v_weave_out((0, (0,), 0, 4), 1, True)
-        q_transpose(0, 0, 1)
-        v_widen((0, (0, 1), 0, 4), 1, (1, 2, 3), True)
+        v_weave_out((0, (0,), 4, 4), 0, True)
         v_quantise((0, (0,), 0, 4))
-        k_interleave(0, 0, 1)
-        kv_passes(0, 0, 0, 0)
-        kv_passes(0, 0, 1, 0)
+        q_transpose(0, 0, 1)
+        load_q(0, 3, 1)
+        load_k(0, 0, 1, 1)
+        load_q(1, 0, 2)
+        load_k(0, 1, 1, 1)
+        load_k(1, 0, 0, 2)
+        v_widen((0, (0, 1), 0, 4), 1, (0,), True)
+        k_quantise(0, 0, (0,))
         q_out(0, 0, 0, True)
-        kv_passes(0, 0, 2, 0)
-        v_interleave((0, (1,), 0, 4), (0, (0, 1), 0, 4))
-        kv_passes(0, 0, 3, 0)
-        q_out(0, 0, 1, True)
-        q_transpose(0, 1, 0)
-        v_widen((0, (0, 1), 4, 4), 1, (0, 1, 2, 3), True)
-        load_v(1, 1)
-        q_transpose(0, 1, 1)
-        k_quantise(0, 0, (1,))
-        v_quantise((0, (1,), 0, 4))
-        k_interleave(0, 1, 0)
-        kv_passes(0, 0, 0, 1)
-        q_out(0, 1, 0, True)
-        kv_passes(0, 0, 1, 1)
-        q_transpose(0, 2, 0)
-        q_out(0, 1, 1, True)
         v_quantise((0, (0,), 4, 4))
+        kv_passes(0, 0, 0, 0)
+        q_out(0, 0, 1, True)
+        v_widen((0, (0, 1), 0, 4), 1, (1, 2, 3), False)
+        kv_passes(0, 0, 1, 0)
+        q_transpose(0, 1, 0)
+        v_widen((0, (0, 1), 4, 4), 1, (0, 1, 2), True)
+        q_transpose(0, 1, 1)
+        v_interleave((0, (1,), 0, 4), (0, (0, 1), 0, 4))
+        kv_passes(0, 0, 2, 0)
+        q_transpose(0, 2, 0)
+        q_out(0, 1, 0, True)
         q_transpose(0, 2, 1)
+        k_interleave(0, 0, 1)
+        load_k(1, 1, 0, 2)
         load_q(1, 2, 2)
-        kv_out((0, (0,), 0, 4), 0, 0, True)
-        k_interleave(0, 1, 1)
-        kv_passes(0, 0, 2, 1)
-        kv_out((0, (0,), 0, 4), 0, 1, True)
-        kv_passes(0, 0, 3, 1)
+        load_v(1, 0)
+        q_out(0, 1, 1, True)
+        kv_passes(0, 0, 3, 0)
         q_transpose(0, 3, 0)
-        q_out(0, 2, 0, True)
-        k_quantise(0, 1, (0,))
+        v_widen((0, (0, 1), 4, 4), 1, (3,), True)
+        load_v(1, 1)
+        v_quantise((0, (1,), 0, 4))
         q_transpose(0, 3, 1)
+        q_out(0, 2, 0, True)
+        k_quantise(0, 0, (1,))
         q_out(0, 2, 1, True)
-        k_quantise(0, 1, (1,))
-        kv_passes(0, 1, 0, 0)
-        kv_out((0, (0,), 0, 4), 0, 2, True)
         v_interleave((0, (1,), 4, 4), (0, (0, 1), 4, 4))
+        q_out(0, 3, 0, True)
+        kv_passes(0, 0, 0, 1)
+        kv_passes(0, 0, 1, 1)
+        q_out(0, 3, 1, True)
+        kv_passes(0, 0, 2, 1)
+        k_interleave(0, 1, 0)
+        kv_passes(0, 0, 3, 1)
+        kv_out((0, (0,), 0, 4), 0, 0, True)
+        kv_passes(0, 0, 4, 0)
+        kv_out((0, (0,), 0, 4), 0, 1, True)
+        kv_passes(0, 0, 5, 0)
+        kv_passes(0, 0, 6, 0)
+        v_quantise((0, (1,), 4, 4))
+        kv_out((0, (0,), 0, 4), 0, 2, True)
+        kv_passes(0, 0, 7, 0)
         kv_out((0, (0,), 0, 4), 0, 3, True)
+        q_quantise(0, 0, 2)
+        kv_passes(0, 0, 4, 1)
+        kv_passes(0, 0, 5, 1)
+        kv_passes(0, 0, 6, 1)
+        kv_out((0, (0,), 4, 4), 0, 4, True)
+        k_interleave(0, 1, 1)
+        kv_passes(0, 0, 7, 1)
+        kv_out((0, (0,), 4, 4), 0, 5, True)
+        q_transpose(1, 0, 0)
+        kv_out((0, (0,), 4, 4), 0, 6, True)
+        q_transpose(1, 0, 1)
+        k_quantise(0, 1, (0,))
+        kv_out((0, (0,), 4, 4), 0, 7, True)
+        q_transpose(1, 1, 0)
+        k_quantise(0, 1, (1,))
+        q_out(1, 0, 0, True)
+        kv_passes(0, 1, 0, 0)
+        q_quantise(0, 2, 2)
+        q_out(1, 0, 1, True)
         kv_passes(0, 1, 0, 1)
         kv_passes(0, 1, 1, 0)
-        q_out(0, 3, 0, True)
-        q_shuffle(1, 0)
-        kv_passes(0, 1, 1, 1)
-        q_out(0, 3, 1, True)
-        kv_passes(0, 1, 2, 0)
-        q_shuffle(1, 1)
-        kv_out((0, (1,), 0, 4), 1, 0, True)
-        kv_passes(0, 1, 2, 1)
-        v_quantise((0, (1,), 4, 4))
-        kv_out((0, (1,), 0, 4), 1, 1, True)
-        kv_passes(0, 1, 3, 0)
-        q_quantise(0, 0, 2)
-        kv_out((0, (1,), 0, 4), 1, 2, True)
-        kv_passes(0, 1, 3, 1)
-        q_transpose(1, 0, 0)
-        kv_out((0, (1,), 0, 4), 1, 3, True)
-        q_transpose(1, 0, 1)
-        kv_quantise((0, (0,), 0, 4), 0, 4)
-        q_out(1, 0, 0, True)
-        q_transpose(1, 1, 0)
-        kv_quantise((0, (1,), 0, 4), 0, 4)
-        q_out(1, 0, 1, True)
-        q_transpose(1, 1, 1)
-        q_quantise(0, 2, 2)
         q_out(1, 1, 0, True)
-        kv_passes(0, 0, 4, 0)
-        q_out(1, 1, 1, True)
-        kv_passes(0, 0, 4, 1)
+        kv_quantise((0, (0,), 0, 4), 0, 4)
+        kv_out((0, (1,), 0, 4), 1, 0, True)
+        kv_passes(0, 1, 1, 1)
+        kv_passes(0, 1, 2, 0)
         k_interleave(1, 0, 0)
-        kv_passes(0, 0, 5, 0)
-        kv_out((0, (0,), 4, 4), 0, 4, True)
-        kv_passes(0, 0, 5, 1)
-        kv_passes(0, 0, 6, 0)
+        kv_out((0, (1,), 0, 4), 1, 1, True)
+        kv_passes(0, 1, 2, 1)
+        kv_passes(0, 1, 3, 0)
+        kv_out((0, (1,), 0, 4), 1, 2, True)
         k_interleave(1, 0, 1)
-        kv_out((0, (0,), 4, 4), 0, 5, True)
-        kv_passes(0, 0, 6, 1)
-        kv_passes(0, 0, 7, 0)
-        kv_out((0, (0,), 4, 4), 0, 6, True)
-        kv_passes(0, 0, 7, 1)
-        out_passes(0, 0, 1, 0, 4, (0, 1))
-        kv_out((0, (0,), 4, 4), 0, 7, True)
-        out_passes(0, 1, 1, 0, 4, (0, 1))
-        out_copy((0, 0, 2, 0, 4), 0, 1, 0, 4, True)
-        out_passes(0, 2, 1, 0, 4, (0, 1))
-        kv_quantise((0, (0,), 4, 4), 0, 4)
-        out_copy((0, 0, 2, 0, 4), 1, 1, 0, 4, True)
-        out_passes(0, 3, 1, 0, 4, (0, 1))
-        k_quantise(1, 0, (0, 1))
-        out_copy((0, 2, 2, 0, 4), 2, 1, 0, 4, True)
+        kv_passes(0, 1, 3, 1)
         kv_passes(0, 1, 4, 0)
-        store((0, 0, 2, 0, 4))
-        out_copy((0, 2, 2, 0, 4), 3, 1, 0, 4, True)
+        kv_out((0, (1,), 0, 4), 1, 3, True)
         kv_passes(0, 1, 4, 1)
-        v_widen((1, (0, 1), 0, 4), 0, (0, 1, 2, 3), False)
         kv_passes(0, 1, 5, 0)
-        store((0, 2, 2, 0, 4))
+        kv_quantise((0, (1,), 0, 4), 0, 4)
         kv_out((0, (1,), 4, 4), 1, 4, True)
         kv_passes(0, 1, 5, 1)
-        q_shuffle(1, 2)
+        kv_quantise((0, (0,), 4, 4), 0, 4)
         kv_passes(0, 1, 6, 0)
         kv_out((0, (1,), 4, 4), 1, 5, True)
-        v_widen((1, (0, 1), 0, 4), 1, (0, 1, 2, 3), False)
+        k_quantise(1, 0, (0, 1))
         kv_passes(0, 1, 6, 1)
         kv_passes(0, 1, 7, 0)
         kv_out((0, (1,), 4, 4), 1, 6, True)
         kv_passes(0, 1, 7, 1)
-        out_passes(0, 4, 1, 0, 4, (0, 1))
+        q_shuffle(1, 2)
+        out_passes(0, 0, 1, 0, 4, (0, 1))
         kv_out((0, (1,), 4, 4), 1, 7, True)
+        q_shuffle(1, 3)
+        out_passes(0, 1, 1, 0, 4, (0, 1))
+        out_copy((0, 0, 2, 0, 4), 0, 1, 0, 4, True)
+        v_widen((1, (0, 1), 0, 4), 0, (0, 1, 2, 3), False)
+        out_passes(0, 2, 1, 0, 4, (0, 1))
+        out_copy((0, 0, 2, 0, 4), 1, 1, 0, 4, True)
+        out_passes(0, 3, 1, 0, 4, (0, 1))
+        out_copy((0, 2, 2, 0, 4), 2, 1, 0, 4, True)
+        kv_quantise((0, (1,), 4, 4), 0, 4)
+        out_passes(0, 4, 1, 0, 4, (0, 1))
+        store((0, 0, 2, 0, 4))
+        out_copy((0, 2, 2, 0, 4), 3, 1, 0, 4, True)
+        v_widen((1, (0, 1), 0, 4), 1, (0, 1, 2, 3), False)
         out_passes(0, 5, 1, 0, 4, (0, 1))
         out_copy((0, 4, 2, 0, 4), 4, 1, 0, 4, True)
         out_passes(0, 6, 1, 0, 4, (0, 1))
-        kv_quantise((0, (1,), 4, 4), 0, 4)
+        store((0, 2, 2, 0, 4))
         out_copy((0, 4, 2, 0, 4), 5, 1, 0, 4, True)
+        k_interleave(1, 1, 0)
         out_passes(0, 7, 1, 0, 4, (0, 1))
-        v_interleave((1, (0, 1), 0, 2), (1, (0, 1), 0, 4))
         out_copy((0, 6, 2, 0, 4), 6, 1, 0, 4, True)
-        q_transpose(1, 2, 0)
+        q_transpose(1, 1, 1)
         store((0, 4, 2, 0, 4))
         out_copy((0, 6, 2, 0, 4), 7, 1, 0, 4, True)
+        v_interleave((1, (0, 1), 0, 2), (1, (0, 1), 0, 4))
+        q_transpose(1, 2, 0)
+        q_out(1, 1, 1, True)
         q_transpose(1, 2, 1)
-        k_interleave(1, 1, 0)
+        store((0, 6, 2, 0, 4))
         q_out(1, 2, 0, True)
         q_transpose(1, 3, 0)
-        store((0, 6, 2, 0, 4))
+        k_interleave(1, 1, 1)
         q_out(1, 2, 1, True)
         q_transpose(1, 3, 1)
-        v_quantise((1, (0, 1), 0, 2))
         q_out(1, 3, 0, True)
         out_passes(0, 0, 1, 4, 4, (0, 1))
-        k_interleave(1, 1, 1)
+        v_quantise((1, (0, 1), 0, 2))
         q_out(1, 3, 1, True)
         out_passes(0, 1, 1, 4, 4, (0, 1))
+        k_quantise(1, 1, (0,))
         out_copy((0, 0, 2, 4, 4), 0, 1, 4, 4, True)
         out_passes(0, 2, 1, 4, 4, (0, 1))
+        v_interleave((1, (0, 1), 2, 2), (1, (0, 1), 0, 4))
         out_copy((0, 0, 2, 4, 4), 1, 1, 4, 4, True)
-        k_quantise(1, 1, (0,))
         out_passes(0, 3, 1, 4, 4, (0, 1))
         out_copy((0, 2, 2, 4, 4), 2, 1, 4, 4, True)
-        v_interleave((1, (0, 1), 2, 2), (1, (0, 1), 0, 4))
         out_passes(0, 4, 1, 4, 4, (0, 1))
         store((0, 0, 2, 4, 4))
+        k_quantise(1, 1, (1,))
         out_copy((0, 2, 2, 4, 4), 3, 1, 4, 4, True)
         out_passes(0, 5, 1, 4, 4, (0, 1))
+        v_quantise((1, (0, 1), 2, 2))
         out_copy((0, 4, 2, 4, 4), 4, 1, 4, 4, True)
-        k_quantise(1, 1, (1,))
         out_passes(0, 6, 1, 4, 4, (0, 1))
         store((0, 2, 2, 4, 4))
-        out_copy((0, 4, 2, 4, 4), 5, 1, 4, 4, True)
-        v_quantise((1, (0, 1), 2, 2))
-        out_passes(0, 7, 1, 4, 4, (0, 1))
         q_quantise(1, 0, 2)
+        out_copy((0, 4, 2, 4, 4), 5, 1, 4, 4, True)
+        out_passes(0, 7, 1, 4, 4, (0, 1))
         kv_passes(1, 0, 0, 0)
         store((0, 4, 2, 4, 4))
+        q_quantise(1, 2, 1)
         kv_passes(1, 0, 0, 1)
         kv_passes(1, 0, 1, 0)
-        q_quantise(1, 2, 1)
+        v_widen((1, (0, 1), 4, 2), 0, (0, 1, 2, 3), False)
         kv_out((1, (0, 1), 0, 2), 0, 0, True)
         kv_passes(1, 0, 1, 1)
-        v_widen((1, (0, 1), 4, 2), 0, (0, 1, 2, 3), False)
         kv_passes(1, 1, 0, 0)
         kv_out((1, (0, 1), 0, 2), 0, 1, True)
         kv_passes(1, 1, 0, 1)

@@ -17,9 +17,16 @@ MULT = mybir.AluOpType.mult
 
 P = 128
 PACK = 4
-HALF = 512
-UNIT = PACK * HALF
-INV = 1.0 / 32.0
+PASS = P * PACK
+UNIT = PACK * PASS
+SLOTS = S // P
+BOTH = (0, 1)
+ROWS = (0, 1, 2, 3)
+FACTOR = 1.0 / S
+SCALAR, VECTOR = True, False
+
+BUFS = {"k_raw": 3, "v_raw": 2, "q_raw1": 3, "q_raw2": 2, "v_wide": 3, "q_split": 2, "res1": 4, "res2": 4,
+        "k_grp": 2, "v_grp": 3, "q_grp": 4, "m_grp": 3, "k_mx": 2, "v_mx": 4, "q_mx": 3, "m_mx": 4}
 
 
 def tile_efficientattention_kernel(tc, q, k, v_bytes, v_scale, out):
@@ -32,19 +39,17 @@ def tile_efficientattention_kernel(tc, q, k, v_bytes, v_scale, out):
         psum = ctx.enter_context(tc.psum_pool(name="psum", bufs=1))
         ctx.enter_context(tc.manual_schedule())
 
-        bufs = {'k_raw': 3, 'v_raw': 2, 'q_raw1': 3, 'q_raw2': 2, 'k_grp': 2, 'v_wide': 3, 'v_grp': 3, 'q_grp': 4, 'm_grp': 3, 'q_split': 2, 'res1': 4, 'res2': 4, 'codes_k': 2, 'codes_v': 4, 'codes_q': 3, 'codes_m': 4}
-
         row_scale = keep.tile([P, 2, PACK], F32, name="row_scale")
         nc.scalar.dma_start(out=row_scale[:], in_=v_scale.rearrange("o (g p j) x -> p (o g) (j x)", p=P, j=PACK))
-        scl = keep.tile([P, 2, PACK], F32, name="scl")
+        folded_scale = keep.tile([P, 2, PACK], F32, name="folded_scale")
         ident = keep.tile([P, P], F32, name="ident")
         make_identity(nc, ident[:])
         ident_bf = keep.tile([P, P], BF16, name="ident_bf")
         make_identity(nc, ident_bf[:])
 
-        k_tile, k_raw, v_raw, q_raw, q_split = {}, {}, {}, {}, {}
-        v_wide, grouped, res, bank = {}, {}, {}, {}
-        codes, v_codes, m_codes = {}, {}, {}
+        k_tile, k_raw, v_raw, q_raw, q_split, v_wide = {}, {}, {}, {}, {}, {}
+        grouped, quantised, v_at, kv_at = {}, {}, {}, {}
+        bank, res, res_left = {}, {}, {}
 
         free_banks, held = list(range(8)), {}
 
@@ -53,490 +58,348 @@ def tile_efficientattention_kernel(tc, q, k, v_bytes, v_scale, out):
             bank[key] = psum.tile(shape, dtype, name="bank%d" % held[key])
             return bank[key]
 
-        def evacuate(key, dst, src, on_scalar):
-            if on_scalar:
+        def empty_bank(key, dst, src, engine):
+            if engine == SCALAR:
                 nc.scalar.copy(out=dst, in_=src)
             else:
                 nc.vector.tensor_copy(out=dst, in_=src)
             free_banks.append(held[key])
 
-        def load_k(b, g, first, halves):
-            key = (b, "pass", g) if halves == 2 else (b, "half", first)
-            if key not in k_tile:
-                k_tile[key] = raw.tile([P, 2 * UNIT], BF16, name="k_raw", bufs=bufs["k_raw"])
-            part = k_tile[key][:] if halves == 2 else k_tile[key][:, g * UNIT:(g + 1) * UNIT]
-            t = part.rearrange("p (j d) -> p j d", j=PACK)
-            rows = k[b].rearrange("(g p j) d -> g p j d", p=P, j=PACK)[g]
-            nc.sync.dma_start(out=t, in_=rows[:, :, first * HALF:(first + halves) * HALF])
-            for n in range(halves):
-                k_raw[b, first + n, g] = t[:, :, n * HALF:(n + 1) * HALF]
-
-        def load_v(b, g):
-            t = raw.tile([P, PACK, E], U8, name="v_raw", bufs=bufs["v_raw"])
-            nc.sync.dma_start(out=t[:], in_=v_bytes[b].rearrange("(g p j) e -> g p j e", p=P, j=PACK)[g])
-            for j in range(PACK):
-                v_raw[b, g, j] = t[:, j, :]
-
-        def load_v_rows(b, g, j):
-            t = raw.tile([P, 2, E], U8, name="v_rows%d%d%d" % (b, g, j))
-            nc.sync.dma_start(out=t[:], in_=v_bytes[b].rearrange("(g p j) e -> g p j e", p=P, j=PACK)[g][:, j:j + 2, :])
-            for n in range(2):
-                v_raw[b, g, j + n] = t[:, n, :]
-
-        def load_q(b, first, pieces):
-            t = raw.tile([P, 2 * pieces, D], BF16, name="q_raw%d" % pieces, bufs=bufs["q_raw%d" % pieces])
-            nc.sync.dma_start(out=t[:], in_=q[b].rearrange("(p r) d -> p r d", r=8)[:, 2 * first:2 * (first + pieces), :])
-            for n in range(pieces):
-                q_raw[b, first + n] = t[:, 2 * n:2 * n + 2, :]
+        def grouped_tile(key, width):
+            if key not in grouped:
+                grouped[key] = work.tile([P, width], BF16, name=key[0] + "_grp", align_bytes=64, bufs=BUFS[key[0] + "_grp"])
+            return grouped[key]
 
         def quantise(key, first, width):
-            kind, words = key[0], grouped[key].shape[1] // PACK
-            if key not in codes:
-                c = mx.tile([P, words], U32, name="codes_" + kind, align_bytes=64, bufs=bufs["codes_" + kind])
-                s = mx.tile([P, words], U8, name="scales_" + kind, align_bytes=64, bufs=bufs["codes_" + kind])
-                codes[key] = (c, s)
-            c, s = codes[key]
+            words = grouped[key].shape[1] // PACK
+            if key not in quantised:
+                codes = mx.tile([P, words], U32, name=key[0] + "_codes", align_bytes=64, bufs=BUFS[key[0] + "_mx"])
+                scales = mx.tile([P, words], U8, name=key[0] + "_scales", align_bytes=64, bufs=BUFS[key[0] + "_mx"])
+                quantised[key] = (codes, scales)
+            codes, scales = quantised[key]
             part = slice(first // PACK, (first + width) // PACK)
-            nc.vector.quantize_mx(out=c[:, part].bitcast(FP8X4), scales=s[:, part], in_=grouped[key][:, first:first + width])
+            nc.vector.quantize_mx(out=codes[:, part].bitcast(FP8X4), scales=scales[:, part], in_=grouped[key][:, first:first + width])
+
+        def mx_pass(dst, still, still_at, moving, moving_at, width, start, stop):
+            m, n = slice(still_at, still_at + P), slice(moving_at, moving_at + width)
+            nc.tensor.matmul_mx(out=dst, lhsT=still[0][:, m].bitcast(FP8X4), lhsT_scale=still[1][:, m],
+                                rhs=moving[0][:, n].bitcast(FP8X4), rhs_scale=moving[1][:, n], start=start, stop=stop)
+
+        def load_k(b, g, halves):
+            key = (b, "pass", g) if halves == BOTH else (b, "half", halves[0])
+            if key not in k_tile:
+                k_tile[key] = raw.tile([P, 2 * UNIT], BF16, name="k_raw", bufs=BUFS["k_raw"])
+            part = k_tile[key][:] if halves == BOTH else k_tile[key][:, g * UNIT:(g + 1) * UNIT]
+            t = part.rearrange("p (j d) -> p j d", j=PACK)
+            rows = k[b].rearrange("(g p j) d -> g p j d", p=P, j=PACK)[g]
+            nc.sync.dma_start(out=t, in_=rows[:, :, halves[0] * PASS:(halves[-1] + 1) * PASS])
+            for n, G in enumerate(halves):
+                k_raw[b, G, g] = t[:, :, n * PASS:(n + 1) * PASS]
+
+        def load_v(b, g, rows=ROWS):
+            if rows == ROWS:
+                t = raw.tile([P, PACK, E], U8, name="v_raw", bufs=BUFS["v_raw"])
+            else:
+                t = raw.tile([P, len(rows), E], U8, name="v_rows%d" % rows[0])
+            source = v_bytes[b].rearrange("(g p j) e -> g p j e", p=P, j=PACK)[g]
+            nc.sync.dma_start(out=t[:], in_=source[:, rows[0]:rows[-1] + 1, :])
+            for n, j in enumerate(rows):
+                v_raw[b, g, j] = t[:, n, :]
+
+        def load_q(b, pieces):
+            name = "q_raw%d" % len(pieces)
+            t = raw.tile([P, 2 * len(pieces), D], BF16, name=name, bufs=BUFS[name])
+            nc.sync.dma_start(out=t[:], in_=q[b].rearrange("(p r) d -> p r d", r=SLOTS)[:, 2 * pieces[0]:2 * pieces[-1] + 2, :])
+            for n, i in enumerate(pieces):
+                q_raw[b, i] = t[:, 2 * n:2 * n + 2, :]
 
         def k_interleave(b, G, g):
-            if ("k", b, G) not in grouped:
-                grouped["k", b, G] = work.tile([P, 2 * UNIT], BF16, name="k_grp", align_bytes=64, bufs=bufs["k_grp"])
-            dst = grouped["k", b, G][:, g * UNIT:(g + 1) * UNIT]
+            dst = grouped_tile(("k", b, G), 2 * UNIT)[:, g * UNIT:(g + 1) * UNIT]
             if (b, g) == (0, 0):
                 nc.vector.tensor_scalar(out=dst.rearrange("p (t m j) -> p m j t", t=PACK, j=PACK),
                                         in0=k_raw[b, G, g].rearrange("p j (m t) -> p m j t", t=PACK),
-                                        scalar1=INV * INV, scalar2=None, op0=MULT)
+                                        scalar1=FACTOR, scalar2=None, op0=MULT)
             else:
                 nc.vector.tensor_copy(out=dst.rearrange("p (t m u e) -> p m u t e", t=PACK, u=2, e=2),
                                       in_=k_raw[b, G, g].rearrange("p (u e) (m t) -> p m u t e", t=PACK, e=2))
 
-        def fold_factor():
-            nc.vector.tensor_scalar(out=scl[:], in0=row_scale[:], scalar1=INV * INV, scalar2=None, op0=MULT)
-
         def k_quantise(b, G, passes):
             quantise(("k", b, G), passes[0] * UNIT, len(passes) * UNIT)
 
-        def v_widen(unit, g, rows, on_scalar):
-            b, passes, first, tiles = unit
-            if unit not in v_wide:
-                v_wide[unit] = work.tile([P, len(passes), PACK, tiles * P], BF16, name="v_wide", bufs=bufs["v_wide"])
-            scales = row_scale if (b, g) == (0, 0) else scl
+        def v_widen(span, g, rows, engine):
+            b, first, tiles = span
+            if span not in v_wide:
+                v_wide[span] = work.tile([P, 2, PACK, tiles * P], BF16, name="v_wide", bufs=BUFS["v_wide"])
+            scales = row_scale if (b, g) == (0, 0) else folded_scale
             for j in rows:
-                dst, codes = v_wide[unit][:, passes.index(g), j, :], v_raw[b, g, j][:, first * P:(first + tiles) * P].bitcast(FP8)
-                if on_scalar:
-                    nc.scalar.activation(out=dst, in_=codes, func=COPY, scale=scales[:, g, j:j + 1])
+                dst, src = v_wide[span][:, g, j, :], v_raw[b, g, j][:, first * P:(first + tiles) * P].bitcast(FP8)
+                if engine == SCALAR:
+                    nc.scalar.activation(out=dst, in_=src, func=COPY, scale=scales[:, g, j:j + 1])
                 else:
-                    nc.vector.tensor_scalar(out=dst, in0=codes, scalar1=scales[:, g, j:j + 1], scalar2=None, op0=MULT)
+                    nc.vector.tensor_scalar(out=dst, in0=src, scalar1=scales[:, g, j:j + 1], scalar2=None, op0=MULT)
 
-        def v_interleave(unit, wide):
-            b, passes, first, tiles = unit
-            t = work.tile([P, len(passes) * PACK * tiles * P], BF16, name="v_grp", align_bytes=64, bufs=bufs["v_grp"])
-            cols = slice((first - wide[2]) * P, (first - wide[2] + tiles) * P)
-            nc.vector.tensor_copy(out=t[:].rearrange("p (g c i j) -> p g c j i", g=len(passes), i=4, j=PACK),
+        def v_interleave(passes, span, wide):
+            b, first, tiles = span
+            dst = grouped_tile(("v", passes, span), len(passes) * tiles * PASS)
+            cols = slice((first - wide[1]) * P, (first - wide[1] + tiles) * P)
+            nc.vector.tensor_copy(out=dst[:].rearrange("p (g c i j) -> p g c j i", g=len(passes), i=4, j=PACK),
                                   in_=v_wide[wide][:, passes[0]:passes[-1] + 1, :, cols].rearrange("p g j (c i) -> p g c j i", i=4))
-            grouped["v", unit] = t
 
-        def v_interleave_half(unit, a, wide):
-            if ("v", unit) not in grouped:
-                grouped["v", unit] = work.tile([P, UNIT], BF16, name="v_grp", align_bytes=64, bufs=bufs["v_grp"])
-            left = (unit[2] - wide[2] + 2 * a) * P
-            nc.vector.tensor_copy(out=grouped["v", unit][:, a * 1024:(a + 1) * 1024].rearrange("p (c i j) -> p c j i", i=4, j=PACK),
-                                  in_=v_wide[wide][:, unit[1][0], :, left:left + 2 * P].rearrange("p j (c i) -> p c j i", i=4))
+        def v_interleave_pair(g, span, pair):
+            dst = grouped_tile(("v", (g,), span), UNIT)[:, pair * 2 * PASS:(pair + 1) * 2 * PASS]
+            nc.vector.tensor_copy(out=dst.rearrange("p (c i j) -> p c j i", i=4, j=PACK),
+                                  in_=v_wide[span][:, g, :, pair * 2 * P:(pair + 1) * 2 * P].rearrange("p j (c i) -> p c j i", i=4))
 
-        def v_weave(unit, a, wide):
-            x = take_bank(("w", unit, a), [P, 2, P, PACK], BF16)
+        def v_weave(g, span, pair):
+            x = take_bank(("w", span, pair), [P, 2, P, PACK], BF16)
             for n in range(2):
-                left = (unit[2] - wide[2] + 2 * a + n) * P
-                cols = slice(left, left + P)
-                nc.tensor.matmul(x[:, n].rearrange("p c j -> p j c"), lhsT=ident_bf[:], rhs=v_wide[wide][:, unit[1][0], :, cols], start=True, stop=True)
+                col = (2 * pair + n) * P
+                nc.tensor.matmul(x[:, n].rearrange("p c j -> p j c"), lhsT=ident_bf[:], rhs=v_wide[span][:, g, :, col:col + P], start=True, stop=True)
 
-        def v_weave_out(unit, a, on_scalar):
-            if ("v", unit) not in grouped:
-                grouped["v", unit] = work.tile([P, unit[3] * HALF], BF16, name="v_grp", align_bytes=64, bufs=bufs["v_grp"])
-            evacuate(("w", unit, a), grouped["v", unit][:, a * 1024:(a + 1) * 1024], bank["w", unit, a][:].rearrange("p n c j -> p (n c j)"), on_scalar)
+        def v_weave_out(g, span, pair):
+            dst = grouped_tile(("v", (g,), span), UNIT)[:, pair * 2 * PASS:(pair + 1) * 2 * PASS]
+            empty_bank(("w", span, pair), dst, bank["w", span, pair][:].rearrange("p n c j -> p (n c j)"), SCALAR)
 
-        def v_quantise(unit):
-            b, passes, first, tiles = unit
-            quantise(("v", unit), 0, len(passes) * tiles * HALF)
+        def v_quantise(passes, span):
+            b, first, tiles = span
+            quantise(("v", passes, span), 0, len(passes) * tiles * PASS)
             for n, g in enumerate(passes):
                 for a in range(tiles):
-                    v_codes[b, g, first + a] = codes["v", unit] + ((n * tiles + a) * P,)
+                    v_at[b, g, first + a] = (quantised["v", passes, span], (n * tiles + a) * P)
 
-        def q_shuffle(b, i):
-            t = work.tile([P, 4, 2, P], F32, name="q_split", bufs=bufs["q_split"])
+        def q_split_words(b, i):
+            t = work.tile([P, 4, 2, P], F32, name="q_split", bufs=BUFS["q_split"])
             nc.vector.tensor_copy(out=t[:].rearrange("p a u (n e) -> p a n u e", e=2),
                                   in_=q_raw[b, i].bitcast(F32).rearrange("p r (G n e u) -> p (r G) n u e", G=2, e=2, u=2))
             q_split[b, i] = t
 
-        def q_transpose(b, i, G):
-            x = take_bank(("q", b, i, G), [P, 2, 2, P])
-            for r in range(2):
-                for u in range(2):
-                    if (b, i) in q_split:
-                        src = q_split[b, i][:, 2 * r + G, u]
-                    else:
-                        src = q_raw[b, i][:, r, :].bitcast(F32)[:, 256 * G + u:256 * (G + 1):2]
-                    nc.tensor.transpose(x[:, r, u, :], src, ident[:])
+        def q_transpose(b, i, halves):
+            for G in halves:
+                x = take_bank(("q", b, i, G), [P, 2, 2, P])
+                for r in range(2):
+                    for u in range(2):
+                        if (b, i) in q_split:
+                            src = q_split[b, i][:, 2 * r + G, u]
+                        else:
+                            src = q_raw[b, i][:, r, :].bitcast(F32)[:, 256 * G + u:256 * (G + 1):2]
+                        nc.tensor.transpose(x[:, r, u, :], src, ident[:])
 
-        def q_out(b, i, G, on_scalar):
-            key, at = ("q", b, i // 2), (i % 2) * UNIT + G * 1024
-            if key not in grouped:
-                grouped[key] = work.tile([P, 2 * UNIT], BF16, name="q_grp", align_bytes=64, bufs=bufs["q_grp"])
-            dst = grouped[key][:, at:at + 1024].bitcast(F32).rearrange("p (r n u) -> p r n u", r=2, u=2)
-            evacuate(("q", b, i, G), dst, bank["q", b, i, G][:].rearrange("p r u n -> p r n u"), on_scalar)
+        def q_out(b, i, halves):
+            for G in halves:
+                at = (i % 2) * UNIT + G * 2 * PASS
+                dst = grouped_tile(("q", b, i // 2), 2 * UNIT)[:, at:at + 2 * PASS].bitcast(F32).rearrange("p (r n u) -> p r n u", r=2, u=2)
+                empty_bank(("q", b, i, G), dst, bank["q", b, i, G][:].rearrange("p r u n -> p r n u"), SCALAR)
 
-        def q_quantise(b, first, pieces):
-            quantise(("q", b, first // 2), (first % 2) * UNIT, pieces * UNIT)
+        def q_turn(b, i, halves=BOTH):
+            q_transpose(b, i, halves)
+            q_out(b, i, halves)
 
-        def kv_passes(b, G, c, g):
-            if g == 0:
-                take_bank(("m", b, G, c), [P, PACK, P])
-            kc, ks = codes["k", b, G]
-            vc, vs, at = v_codes[b, g, c]
-            for t in range(PACK):
-                m = slice(g * HALF + t * P, g * HALF + (t + 1) * P)
-                nc.tensor.matmul_mx(out=bank["m", b, G, c][:, t, :], lhsT=kc[:, m].bitcast(FP8X4), lhsT_scale=ks[:, m],
-                                    rhs=vc[:, at:at + P].bitcast(FP8X4), rhs_scale=vs[:, at:at + P],
-                                    start=(g == 0 and t == 0), stop=(g == 1 and t == PACK - 1))
+        def q_quantise(b, pair):
+            quantise(("q", b, pair), 0, 2 * UNIT)
 
-        def kv_out(unit, G, c, on_scalar):
-            b, halves, first, tiles = unit
-            if ("m", unit) not in grouped:
-                grouped["m", unit] = work.tile([P, len(halves) * tiles * HALF], BF16, name="m_grp", align_bytes=64, bufs=bufs["m_grp"])
-            at = halves.index(G) * tiles + c - first
-            dst = grouped["m", unit][:, at * HALF:(at + 1) * HALF].rearrange("p (n t) -> p n t", t=PACK)
-            evacuate(("m", b, G, c), dst, bank["m", b, G, c][:].rearrange("p t n -> p n t"), on_scalar)
+        def kv_passes(b, G, c, passes):
+            for g in passes:
+                if g == 0:
+                    take_bank(("m", b, G, c), [P, PACK, P])
+                for t in range(PACK):
+                    mx_pass(bank["m", b, G, c][:, t, :], quantised["k", b, G], g * PASS + t * P, *v_at[b, g, c], P,
+                            start=(g, t) == (0, 0), stop=(g, t) == (1, PACK - 1))
 
-        def kv_quantise(unit, slot, slots):
-            b, halves, first, tiles = unit
-            quantise(("m", unit), slot * HALF, slots * HALF)
-            for at in range(slot, slot + slots):
-                m_codes[b, halves[at // tiles], first + at % tiles] = codes["m", unit] + (at * P,)
+        def kv_out(halves, span, G, c, engine):
+            b, first, tiles = span
+            at = (halves.index(G) * tiles + c - first) * PASS
+            dst = grouped_tile(("m", halves, span), len(halves) * tiles * PASS)[:, at:at + PASS].rearrange("p (n t) -> p n t", t=PACK)
+            empty_bank(("m", b, G, c), dst, bank["m", b, G, c][:].rearrange("p t n -> p n t"), engine)
 
-        def out_passes(b, row, rows, first, tiles, halves):
-            key, width = ("o", b, row, first), tiles * P
+        def kv_banks(halves, span, G, tiles, passes=BOTH, engine=SCALAR):
+            for c in tiles:
+                kv_passes(span[0], G, c, passes)
+                kv_out(halves, span, G, c, engine)
+
+        def kv_quantise(halves, span, now):
+            b, first, tiles = span
+            quantise(("m", halves, span), halves.index(now[0]) * tiles * PASS, len(now) * tiles * PASS)
+            for G in now:
+                kv_at[span, G] = (quantised["m", halves, span], halves.index(G) * tiles * P)
+
+        def out_passes(span, slot, slots, halves=BOTH):
+            b, first, tiles = span
             if halves[0] == 0:
-                take_bank(key, [P, rows, width])
-            order = [(r, G) for r in range(rows) for G in halves]
-            for r, G in order:
-                qc, qs = codes["q", b, (row + r) // 4]
-                mc, ms, at = m_codes[b, G, first]
-                left = ((row + r) // 2 % 2) * HALF + G * 2 * P + ((row + r) % 2) * P
-                m = slice(left, left + P)
-                nc.tensor.matmul_mx(out=bank[key][:, r, :], lhsT=qc[:, m].bitcast(FP8X4), lhsT_scale=qs[:, m],
-                                    rhs=mc[:, at:at + width].bitcast(FP8X4), rhs_scale=ms[:, at:at + width],
-                                    start=((r, G) == (0, 0)), stop=((r, G) == (rows - 1, 1)))
+                take_bank(("o", span, slot), [P, slots, tiles * P])
+            for r in range(slots):
+                for G in halves:
+                    at = ((slot + r) // 2 % 2) * PASS + G * 2 * P + ((slot + r) % 2) * P
+                    mx_pass(bank["o", span, slot][:, r, :], quantised["q", b, (slot + r) // 4], at, *kv_at[span, G], tiles * P,
+                            start=(r, G) == (0, 0), stop=(r, G) == (slots - 1, 1))
 
-        def out_copy(block, row, rows, first, tiles, on_scalar):
-            b, row0, all_rows, first0, all_tiles = block
-            if block not in res:
-                res[block] = work.tile([P, all_rows, all_tiles * P], F32, name="res%d" % (all_rows * all_tiles // 4), bufs=bufs["res%d" % (all_rows * all_tiles // 4)])
-            dst = res[block][:, row - row0:row - row0 + rows, (first - first0) * P:(first - first0 + tiles) * P]
-            evacuate(("o", b, row, first), dst, bank["o", b, row, first][:], on_scalar)
+        def out_copy(span, slot, slots, block_slots, engine):
+            b, first, tiles = span
+            top = slot - slot % block_slots
+            if (span, top) not in res:
+                name = "res%d" % (block_slots * tiles * P // PASS)
+                res[span, top] = work.tile([P, block_slots, tiles * P], F32, name=name, bufs=BUFS[name])
+                res_left[span, top] = block_slots
+            empty_bank(("o", span, slot), res[span, top][:, slot - top:slot - top + slots, :], bank["o", span, slot][:], engine)
+            res_left[span, top] = res_left[span, top] - slots
+            if res_left[span, top] == 0:
+                rows_out = out[b].rearrange("(p r) e -> p r e", r=SLOTS)
+                nc.sync.dma_start(out=rows_out[:, top:top + block_slots, first * P:(first + tiles) * P], in_=res[span, top][:])
 
-        def store(block):
-            b, row0, all_rows, first0, all_tiles = block
-            rows_out = out[b].rearrange("(p r) e -> p r e", r=8)
-            nc.sync.dma_start(out=rows_out[:, row0:row0 + all_rows, first0 * P:(first0 + all_tiles) * P], in_=res[block][:])
+        def out_banks(span, first_slots, slots, block_slots):
+            for slot in first_slots:
+                out_passes(span, slot, slots)
+                out_copy(span, slot, slots, block_slots, SCALAR)
 
-        load_v_rows(0, 0, 0)
-        load_v_rows(0, 0, 2)
-        load_k(0, 0, 0, 1)
-        load_q(0, 0, 1)
+        left, right = (0, 0, 4), (0, 4, 4)
+        wide0, span0, span1, span2, wide1, span3, span4 = (1, 0, 4), (1, 0, 2), (1, 2, 2), (1, 4, 2), (1, 6, 2), (1, 6, 1), (1, 7, 1)
+
+        load_v(0, 0, (0, 1))
+        load_v(0, 0, (2, 3))
+        load_k(0, 0, (0,))
         load_v(0, 1)
-        load_q(0, 1, 1)
-        load_q(0, 2, 1)
-        load_k(0, 1, 0, 1)
-        v_widen((0, (0, 1), 4, 4), 0, (0, 1, 2), True)
-        v_widen((0, (0, 1), 0, 4), 0, (0, 1, 2, 3), False)
-        v_widen((0, (0, 1), 4, 4), 0, (3,), False)
-        v_interleave_half((0, (0,), 0, 4), 1, (0, (0, 1), 0, 4))
-        v_weave((0, (0,), 0, 4), 0, (0, (0, 1), 0, 4))
+        load_q(0, (0,))
+        load_q(0, (1,))
+        load_k(0, 1, (0,))
+        load_q(0, (2,))
+
+        v_widen(right, 0, (0, 1, 2), SCALAR)
+        v_widen(left, 0, ROWS, VECTOR)
+        v_widen(right, 0, (3,), VECTOR)
+        v_interleave_pair(0, left, 1)
+        nc.vector.tensor_scalar(out=folded_scale[:], in0=row_scale[:], scalar1=FACTOR, scalar2=None, op0=MULT)
         k_interleave(0, 0, 0)
-        v_weave((0, (0,), 4, 4), 0, (0, (0, 1), 4, 4))
-        v_weave_out((0, (0,), 0, 4), 0, True)
-        fold_factor()
-        v_interleave_half((0, (0,), 4, 4), 1, (0, (0, 1), 4, 4))
-        q_transpose(0, 0, 0)
-        v_weave_out((0, (0,), 4, 4), 0, True)
-        v_quantise((0, (0,), 0, 4))
-        q_transpose(0, 0, 1)
-        load_q(0, 3, 1)
-        load_k(0, 0, 1, 1)
-        load_q(1, 0, 2)
-        load_k(0, 1, 1, 1)
-        load_k(1, 0, 0, 2)
-        v_widen((0, (0, 1), 0, 4), 1, (0,), True)
+        v_interleave_pair(0, right, 1)
+        for span in (left, right):
+            v_weave(0, span, 0)
+        v_weave_out(0, left, 0)
+        v_widen(left, 1, (0,), SCALAR)
+        v_weave_out(0, right, 0)
+        v_widen(left, 1, (1,), SCALAR)
+        v_widen(right, 1, (0, 1), SCALAR)
+        q_turn(0, 0)
+        load_q(0, (3,))
+        load_k(0, 0, (1,))
+        load_k(0, 1, (1,))
+        load_q(1, (0, 1))
+        load_k(1, 0, BOTH)
+        v_quantise((0,), left)
         k_quantise(0, 0, (0,))
-        q_out(0, 0, 0, True)
-        v_quantise((0, (0,), 4, 4))
-        kv_passes(0, 0, 0, 0)
-        q_out(0, 0, 1, True)
-        v_widen((0, (0, 1), 0, 4), 1, (1, 2, 3), False)
-        kv_passes(0, 0, 1, 0)
-        q_transpose(0, 1, 0)
-        v_widen((0, (0, 1), 4, 4), 1, (0, 1, 2), True)
-        q_transpose(0, 1, 1)
-        v_interleave((0, (1,), 0, 4), (0, (0, 1), 0, 4))
-        kv_passes(0, 0, 2, 0)
-        q_transpose(0, 2, 0)
-        q_out(0, 1, 0, True)
-        q_transpose(0, 2, 1)
+        v_widen(left, 1, (2, 3), VECTOR)
+        v_quantise((0,), right)
+        v_interleave((1,), left, left)
         k_interleave(0, 0, 1)
-        load_k(1, 1, 0, 2)
-        load_q(1, 2, 2)
-        load_v(1, 0)
-        q_out(0, 1, 1, True)
-        kv_passes(0, 0, 3, 0)
-        q_transpose(0, 3, 0)
-        v_widen((0, (0, 1), 4, 4), 1, (3,), True)
-        load_v(1, 1)
-        v_quantise((0, (1,), 0, 4))
-        q_transpose(0, 3, 1)
-        q_out(0, 2, 0, True)
+        v_quantise((1,), left)
         k_quantise(0, 0, (1,))
-        q_out(0, 2, 1, True)
-        v_interleave((0, (1,), 4, 4), (0, (0, 1), 4, 4))
-        q_out(0, 3, 0, True)
-        kv_passes(0, 0, 0, 1)
-        kv_passes(0, 0, 1, 1)
-        q_out(0, 3, 1, True)
-        kv_passes(0, 0, 2, 1)
+        v_widen(right, 1, (2, 3), SCALAR)
+        load_k(1, 1, BOTH)
+        load_v(1, 0)
+        load_q(1, (2, 3))
+        load_v(1, 1)
+
+        for tiles, i in (((0, 1), 1), ((2,), 2), ((3,), 3)):
+            for c in tiles:
+                kv_passes(0, 0, c, (0,))
+            q_turn(0, i)
+        kv_banks((0,), left, 0, range(4), (1,))
+        v_interleave((1,), right, right)
         k_interleave(0, 1, 0)
-        kv_passes(0, 0, 3, 1)
-        kv_out((0, (0,), 0, 4), 0, 0, True)
-        kv_passes(0, 0, 4, 0)
-        kv_out((0, (0,), 0, 4), 0, 1, True)
-        kv_passes(0, 0, 5, 0)
-        kv_passes(0, 0, 6, 0)
-        v_quantise((0, (1,), 4, 4))
-        kv_out((0, (0,), 0, 4), 0, 2, True)
-        kv_passes(0, 0, 7, 0)
-        kv_out((0, (0,), 0, 4), 0, 3, True)
-        q_quantise(0, 0, 2)
-        kv_passes(0, 0, 4, 1)
-        kv_passes(0, 0, 5, 1)
-        kv_passes(0, 0, 6, 1)
-        kv_out((0, (0,), 4, 4), 0, 4, True)
+        v_quantise((1,), right)
+        for c in range(4, 8):
+            kv_passes(0, 0, c, (0,))
+        kv_banks((0,), right, 0, range(4, 8), (1,))
+        q_quantise(0, 0)
         k_interleave(0, 1, 1)
-        kv_passes(0, 0, 7, 1)
-        kv_out((0, (0,), 4, 4), 0, 5, True)
-        q_transpose(1, 0, 0)
-        kv_out((0, (0,), 4, 4), 0, 6, True)
-        q_transpose(1, 0, 1)
-        k_quantise(0, 1, (0,))
-        kv_out((0, (0,), 4, 4), 0, 7, True)
-        q_transpose(1, 1, 0)
-        k_quantise(0, 1, (1,))
-        q_out(1, 0, 0, True)
-        kv_passes(0, 1, 0, 0)
-        q_quantise(0, 2, 2)
-        q_out(1, 0, 1, True)
-        kv_passes(0, 1, 0, 1)
-        kv_passes(0, 1, 1, 0)
-        q_out(1, 1, 0, True)
-        kv_quantise((0, (0,), 0, 4), 0, 4)
-        kv_out((0, (1,), 0, 4), 1, 0, True)
-        kv_passes(0, 1, 1, 1)
-        kv_passes(0, 1, 2, 0)
-        k_interleave(1, 0, 0)
-        kv_out((0, (1,), 0, 4), 1, 1, True)
-        kv_passes(0, 1, 2, 1)
-        kv_passes(0, 1, 3, 0)
-        kv_out((0, (1,), 0, 4), 1, 2, True)
-        k_interleave(1, 0, 1)
-        kv_passes(0, 1, 3, 1)
-        kv_passes(0, 1, 4, 0)
-        kv_out((0, (1,), 0, 4), 1, 3, True)
-        kv_passes(0, 1, 4, 1)
-        kv_passes(0, 1, 5, 0)
-        kv_quantise((0, (1,), 0, 4), 0, 4)
-        kv_out((0, (1,), 4, 4), 1, 4, True)
-        kv_passes(0, 1, 5, 1)
-        kv_quantise((0, (0,), 4, 4), 0, 4)
-        kv_passes(0, 1, 6, 0)
-        kv_out((0, (1,), 4, 4), 1, 5, True)
-        k_quantise(1, 0, (0, 1))
-        kv_passes(0, 1, 6, 1)
-        kv_passes(0, 1, 7, 0)
-        kv_out((0, (1,), 4, 4), 1, 6, True)
-        kv_passes(0, 1, 7, 1)
-        q_shuffle(1, 2)
-        out_passes(0, 0, 1, 0, 4, (0, 1))
-        kv_out((0, (1,), 4, 4), 1, 7, True)
-        q_shuffle(1, 3)
-        out_passes(0, 1, 1, 0, 4, (0, 1))
-        out_copy((0, 0, 2, 0, 4), 0, 1, 0, 4, True)
-        v_widen((1, (0, 1), 0, 4), 0, (0, 1, 2, 3), False)
-        out_passes(0, 2, 1, 0, 4, (0, 1))
-        out_copy((0, 0, 2, 0, 4), 1, 1, 0, 4, True)
-        out_passes(0, 3, 1, 0, 4, (0, 1))
-        out_copy((0, 2, 2, 0, 4), 2, 1, 0, 4, True)
-        kv_quantise((0, (1,), 4, 4), 0, 4)
-        out_passes(0, 4, 1, 0, 4, (0, 1))
-        store((0, 0, 2, 0, 4))
-        out_copy((0, 2, 2, 0, 4), 3, 1, 0, 4, True)
-        v_widen((1, (0, 1), 0, 4), 1, (0, 1, 2, 3), False)
-        out_passes(0, 5, 1, 0, 4, (0, 1))
-        out_copy((0, 4, 2, 0, 4), 4, 1, 0, 4, True)
-        out_passes(0, 6, 1, 0, 4, (0, 1))
-        store((0, 2, 2, 0, 4))
-        out_copy((0, 4, 2, 0, 4), 5, 1, 0, 4, True)
+        for g in BOTH:
+            k_quantise(0, 1, (g,))
+        q_quantise(0, 1)
+        kv_quantise((0,), left, (0,))
+
+        q_turn(1, 0)
+        q_turn(1, 1, (0,))
+        kv_banks((1,), left, 1, range(4))
+        kv_banks((1,), right, 1, range(4, 8))
+        for g in BOTH:
+            k_interleave(1, 0, g)
+        kv_quantise((1,), left, (1,))
+        kv_quantise((0,), right, (0,))
+        k_quantise(1, 0, BOTH)
+        v_widen(wide0, 0, (0,), SCALAR)
+        v_widen(wide0, 0, (1, 2, 3), VECTOR)
+        for i in (2, 3):
+            q_split_words(1, i)
+        kv_quantise((1,), right, (1,))
+        v_widen(wide0, 1, ROWS, VECTOR)
+        out_banks(left, range(SLOTS), 1, 2)
+        q_turn(1, 1, (1,))
+        for i in (2, 3):
+            q_turn(1, i)
         k_interleave(1, 1, 0)
-        out_passes(0, 7, 1, 0, 4, (0, 1))
-        out_copy((0, 6, 2, 0, 4), 6, 1, 0, 4, True)
-        q_transpose(1, 1, 1)
-        store((0, 4, 2, 0, 4))
-        out_copy((0, 6, 2, 0, 4), 7, 1, 0, 4, True)
-        v_interleave((1, (0, 1), 0, 2), (1, (0, 1), 0, 4))
-        q_transpose(1, 2, 0)
-        q_out(1, 1, 1, True)
-        q_transpose(1, 2, 1)
-        store((0, 6, 2, 0, 4))
-        q_out(1, 2, 0, True)
-        q_transpose(1, 3, 0)
+        v_interleave(BOTH, span0, wide0)
         k_interleave(1, 1, 1)
-        q_out(1, 2, 1, True)
-        q_transpose(1, 3, 1)
-        q_out(1, 3, 0, True)
-        out_passes(0, 0, 1, 4, 4, (0, 1))
-        v_quantise((1, (0, 1), 0, 2))
-        q_out(1, 3, 1, True)
-        out_passes(0, 1, 1, 4, 4, (0, 1))
+        v_quantise(BOTH, span0)
         k_quantise(1, 1, (0,))
-        out_copy((0, 0, 2, 4, 4), 0, 1, 4, 4, True)
-        out_passes(0, 2, 1, 4, 4, (0, 1))
-        v_interleave((1, (0, 1), 2, 2), (1, (0, 1), 0, 4))
-        out_copy((0, 0, 2, 4, 4), 1, 1, 4, 4, True)
-        out_passes(0, 3, 1, 4, 4, (0, 1))
-        out_copy((0, 2, 2, 4, 4), 2, 1, 4, 4, True)
-        out_passes(0, 4, 1, 4, 4, (0, 1))
-        store((0, 0, 2, 4, 4))
+        v_interleave(BOTH, span1, wide0)
         k_quantise(1, 1, (1,))
-        out_copy((0, 2, 2, 4, 4), 3, 1, 4, 4, True)
-        out_passes(0, 5, 1, 4, 4, (0, 1))
-        v_quantise((1, (0, 1), 2, 2))
-        out_copy((0, 4, 2, 4, 4), 4, 1, 4, 4, True)
-        out_passes(0, 6, 1, 4, 4, (0, 1))
-        store((0, 2, 2, 4, 4))
-        q_quantise(1, 0, 2)
-        out_copy((0, 4, 2, 4, 4), 5, 1, 4, 4, True)
-        out_passes(0, 7, 1, 4, 4, (0, 1))
-        kv_passes(1, 0, 0, 0)
-        store((0, 4, 2, 4, 4))
-        q_quantise(1, 2, 1)
-        kv_passes(1, 0, 0, 1)
-        kv_passes(1, 0, 1, 0)
-        v_widen((1, (0, 1), 4, 2), 0, (0, 1, 2, 3), False)
-        kv_out((1, (0, 1), 0, 2), 0, 0, True)
-        kv_passes(1, 0, 1, 1)
-        kv_passes(1, 1, 0, 0)
-        kv_out((1, (0, 1), 0, 2), 0, 1, True)
-        kv_passes(1, 1, 0, 1)
-        kv_passes(1, 1, 1, 0)
-        kv_out((1, (0, 1), 0, 2), 1, 0, True)
-        kv_passes(1, 1, 1, 1)
-        kv_passes(1, 0, 2, 0)
-        kv_out((1, (0, 1), 0, 2), 1, 1, True)
-        kv_passes(1, 0, 2, 1)
-        kv_passes(1, 0, 3, 0)
-        kv_quantise((1, (0, 1), 0, 2), 0, 4)
-        kv_out((1, (0, 1), 2, 2), 0, 2, True)
-        kv_passes(1, 0, 3, 1)
-        q_quantise(1, 3, 1)
-        kv_passes(1, 1, 2, 0)
-        kv_out((1, (0, 1), 2, 2), 0, 3, True)
-        v_widen((1, (0, 1), 4, 2), 1, (0, 1, 2, 3), False)
-        kv_passes(1, 1, 2, 1)
-        kv_passes(1, 1, 3, 0)
-        kv_out((1, (0, 1), 2, 2), 1, 2, True)
-        kv_passes(1, 1, 3, 1)
-        out_passes(1, 0, 2, 0, 2, (0, 1))
-        kv_out((1, (0, 1), 2, 2), 1, 3, True)
-        out_passes(1, 2, 2, 0, 2, (0, 1))
-        out_copy((0, 6, 2, 4, 4), 6, 1, 4, 4, True)
-        out_passes(1, 4, 2, 0, 2, (0, 1))
-        kv_quantise((1, (0, 1), 2, 2), 0, 4)
-        out_copy((0, 6, 2, 4, 4), 7, 1, 4, 4, True)
-        out_passes(1, 6, 2, 0, 2, (0, 1))
-        v_interleave((1, (0, 1), 4, 2), (1, (0, 1), 4, 2))
-        out_copy((1, 0, 4, 0, 2), 0, 2, 0, 2, True)
-        out_passes(1, 0, 2, 2, 2, (0, 1))
-        store((0, 6, 2, 4, 4))
-        out_copy((1, 0, 4, 0, 2), 2, 2, 0, 2, True)
-        out_passes(1, 2, 2, 2, 2, (0, 1))
-        v_widen((1, (0, 1), 6, 2), 0, (0, 1, 2, 3), False)
-        out_copy((1, 4, 4, 0, 2), 4, 2, 0, 2, True)
-        out_passes(1, 4, 2, 2, 2, (0, 1))
-        store((1, 0, 4, 0, 2))
-        v_quantise((1, (0, 1), 4, 2))
-        out_copy((1, 4, 4, 0, 2), 6, 2, 0, 2, True)
-        out_passes(1, 6, 2, 2, 2, (0, 1))
-        v_widen((1, (0, 1), 6, 2), 1, (0, 1, 2, 3), False)
-        out_copy((1, 0, 4, 2, 2), 0, 2, 2, 2, True)
-        kv_passes(1, 0, 4, 0)
-        store((1, 4, 4, 0, 2))
-        out_copy((1, 0, 4, 2, 2), 2, 2, 2, 2, True)
-        v_interleave((1, (0, 1), 6, 1), (1, (0, 1), 6, 2))
-        kv_passes(1, 0, 4, 1)
-        kv_passes(1, 0, 5, 0)
-        v_interleave((1, (0, 1), 7, 1), (1, (0, 1), 6, 2))
-        store((1, 0, 4, 2, 2))
-        kv_out((1, (0, 1), 4, 2), 0, 4, True)
-        kv_passes(1, 0, 5, 1)
-        v_quantise((1, (0, 1), 6, 1))
-        kv_passes(1, 1, 4, 0)
-        v_quantise((1, (0, 1), 7, 1))
-        kv_out((1, (0, 1), 4, 2), 0, 5, True)
-        kv_passes(1, 1, 4, 1)
-        kv_passes(1, 1, 5, 0)
-        kv_quantise((1, (0, 1), 4, 2), 0, 2)
-        kv_out((1, (0, 1), 4, 2), 1, 4, True)
-        out_copy((1, 4, 4, 2, 2), 6, 2, 2, 2, False)
-        kv_passes(1, 1, 5, 1)
-        kv_passes(1, 0, 6, 0)
-        kv_out((1, (0, 1), 4, 2), 1, 5, True)
-        kv_passes(1, 0, 6, 1)
-        out_copy((1, 4, 4, 2, 2), 4, 2, 2, 2, True)
-        kv_passes(1, 1, 6, 0)
-        kv_quantise((1, (0, 1), 4, 2), 2, 2)
-        kv_out((1, (0, 1), 6, 1), 0, 6, True)
-        kv_passes(1, 1, 6, 1)
-        store((1, 4, 4, 2, 2))
-        out_passes(1, 0, 2, 4, 2, (0,))
-        out_passes(1, 2, 2, 4, 2, (0,))
-        kv_out((1, (0, 1), 6, 1), 1, 6, False)
-        out_passes(1, 0, 2, 4, 2, (1,))
-        out_passes(1, 2, 2, 4, 2, (1,))
-        out_passes(1, 4, 2, 4, 2, (0, 1))
-        out_copy((1, 0, 4, 4, 2), 0, 2, 4, 2, True)
-        out_copy((1, 0, 4, 4, 2), 2, 2, 4, 2, False)
-        out_passes(1, 6, 2, 4, 2, (0, 1))
-        out_copy((1, 4, 4, 4, 2), 4, 2, 4, 2, True)
-        kv_quantise((1, (0, 1), 6, 1), 0, 2)
-        kv_passes(1, 0, 7, 0)
-        store((1, 0, 4, 4, 2))
-        out_copy((1, 4, 4, 4, 2), 6, 2, 4, 2, False)
-        kv_passes(1, 0, 7, 1)
-        kv_passes(1, 1, 7, 0)
-        store((1, 4, 4, 4, 2))
-        kv_out((1, (0, 1), 7, 1), 0, 7, True)
-        kv_passes(1, 1, 7, 1)
-        out_passes(1, 0, 4, 6, 1, (0, 1))
-        kv_quantise((1, (0, 1), 7, 1), 0, 1)
-        kv_out((1, (0, 1), 7, 1), 1, 7, True)
-        out_passes(1, 4, 4, 6, 1, (0, 1))
-        out_copy((1, 0, 4, 6, 1), 0, 4, 6, 1, False)
-        out_passes(1, 0, 4, 7, 1, (0,))
-        out_passes(1, 4, 4, 7, 1, (0,))
-        out_copy((1, 4, 4, 6, 1), 4, 4, 6, 1, True)
-        kv_quantise((1, (0, 1), 7, 1), 1, 1)
-        store((1, 0, 4, 6, 1))
-        out_passes(1, 0, 4, 7, 1, (1,))
-        out_passes(1, 4, 4, 7, 1, (1,))
-        store((1, 4, 4, 6, 1))
-        out_copy((1, 0, 4, 7, 1), 0, 4, 7, 1, True)
-        out_copy((1, 4, 4, 7, 1), 4, 4, 7, 1, False)
-        store((1, 0, 4, 7, 1))
-        store((1, 4, 4, 7, 1))
+        v_quantise(BOTH, span1)
+        out_banks(right, range(6), 1, 2)
+        for slot in (6, 7):
+            out_passes(right, slot, 1)
+        for pair in BOTH:
+            q_quantise(1, pair)
+
+        for G in BOTH:
+            kv_banks(BOTH, span0, G, (0, 1))
+        kv_quantise(BOTH, span0, BOTH)
+        for g in BOTH:
+            v_widen(span2, g, ROWS, VECTOR)
+        for G in BOTH:
+            kv_banks(BOTH, span1, G, (2, 3))
+        v_widen(wide1, 0, (0, 1), VECTOR)
+        kv_quantise(BOTH, span1, BOTH)
+        for slot in (6, 7):
+            out_copy(right, slot, 1, 2, SCALAR)
+        v_interleave(BOTH, span2, span2)
+        v_widen(wide1, 0, (2, 3), VECTOR)
+        v_quantise(BOTH, span2)
+        v_widen(wide1, 1, ROWS, VECTOR)
+        for span in (span3, span4):
+            v_interleave(BOTH, span, wide1)
+        for span in (span3, span4):
+            v_quantise(BOTH, span)
+        out_banks(span0, (0, 2, 4, 6), 2, 4)
+        out_banks(span1, (0, 2), 2, 4)
+        for slot in (4, 6):
+            out_passes(span1, slot, 2)
+
+        kv_banks(BOTH, span2, 0, (4, 5))
+        kv_quantise(BOTH, span2, (0,))
+        kv_banks(BOTH, span2, 1, (4,))
+        out_copy(span1, 6, 2, 4, VECTOR)
+        kv_banks(BOTH, span2, 1, (5,))
+        out_copy(span1, 4, 2, 4, SCALAR)
+        kv_quantise(BOTH, span2, (1,))
+        kv_banks(BOTH, span3, 0, (6,))
+        kv_banks(BOTH, span3, 1, (6,), engine=VECTOR)
+        for G in BOTH:
+            for slot in (0, 2):
+                out_passes(span2, slot, 2, (G,))
+        for slot in (4, 6):
+            out_passes(span2, slot, 2)
+        for slot, engine in ((0, SCALAR), (2, VECTOR), (4, SCALAR)):
+            out_copy(span2, slot, 2, 4, engine)
+        kv_quantise(BOTH, span3, BOTH)
+        out_copy(span2, 6, 2, 4, VECTOR)
+        for G in BOTH:
+            kv_banks(BOTH, span4, G, (7,))
+        kv_quantise(BOTH, span4, (0,))
+        for slot in (0, 2, 4, 6):
+            out_passes(span3, slot, 2)
+        out_copy(span3, 0, 2, 4, VECTOR)
+        kv_quantise(BOTH, span4, (1,))
+        for slot, engine in ((2, SCALAR), (4, SCALAR), (6, VECTOR)):
+            out_copy(span3, slot, 2, 4, engine)
+        for G in BOTH:
+            for slot in (0, 2, 4, 6):
+                out_passes(span4, slot, 2, (G,))
+        for slot, engine in ((0, SCALAR), (2, VECTOR), (4, SCALAR), (6, VECTOR)):
+            out_copy(span4, slot, 2, 4, engine)

@@ -194,8 +194,8 @@ def tile_efficientattention_kernel(tc, q, k, v_bytes, v_scale, out):
             q_transpose(b, i, halves)
             q_out(b, i, halves)
 
-        def q_quantise(b, pair):
-            quantise(("q", b, pair), 0, 2 * UNIT)
+        def q_quantise(b, pieces):
+            quantise(("q", b, pieces[0] // 2), (pieces[0] % 2) * UNIT, len(pieces) * UNIT)
 
         def kv_passes(b, G, c, passes):
             for g in passes:
@@ -277,8 +277,8 @@ def tile_efficientattention_kernel(tc, q, k, v_bytes, v_scale, out):
         v_widen(left, 1, (1,), SCALAR)
         v_widen(right, 1, (0, 1), SCALAR)
         q_turn(0, 0)
-        load_q(0, (3,))
         load_k(0, 0, (1,))
+        load_q(0, (3,))
         load_k(0, 1, (1,))
         load_q(1, (0, 1))
         load_k(1, 0, BOTH)
@@ -296,32 +296,38 @@ def tile_efficientattention_kernel(tc, q, k, v_bytes, v_scale, out):
         load_q(1, (2, 3))
         load_v(1, 1)
 
-        for tiles, i in (((0, 1), 1), ((2,), 2), ((3,), 3)):
-            for c in tiles:
+        for i in (1, 2):
+            for c in (2 * i - 2, 2 * i - 1):
                 kv_passes(0, 0, c, (0,))
             q_turn(0, i)
+        for c in (4, 5):
+            kv_passes(0, 0, c, (0,))
         kv_banks((0,), left, 0, range(4), (1,))
+        q_turn(0, 3)
         v_interleave((1,), right, right)
         k_interleave(0, 1, 0)
         v_quantise((1,), right)
-        for c in range(4, 8):
+        for c in (6, 7):
             kv_passes(0, 0, c, (0,))
         kv_banks((0,), right, 0, range(4, 8), (1,))
-        q_quantise(0, 0)
+        k_quantise(0, 1, (0,))
         k_interleave(0, 1, 1)
-        for g in BOTH:
-            k_quantise(0, 1, (g,))
-        q_quantise(0, 1)
         kv_quantise((0,), left, (0,))
+        k_quantise(0, 1, (1,))
+        for pieces in ((0, 1), (2, 3)):
+            q_quantise(0, pieces)
 
+        for c in (0, 1):
+            kv_passes(0, 1, c, (0,))
         q_turn(1, 0)
-        q_turn(1, 1, (0,))
-        kv_banks((1,), left, 1, range(4))
+        kv_banks((1,), left, 1, (0, 1), (1,))
+        kv_banks((1,), left, 1, (2, 3))
+        q_turn(1, 1)
         kv_banks((1,), right, 1, range(4, 8))
+        kv_quantise((0,), right, (0,))
         for g in BOTH:
             k_interleave(1, 0, g)
         kv_quantise((1,), left, (1,))
-        kv_quantise((0,), right, (0,))
         k_quantise(1, 0, BOTH)
         v_widen(wide0, 0, (0,), SCALAR)
         v_widen(wide0, 0, (1, 2, 3), VECTOR)
@@ -330,7 +336,6 @@ def tile_efficientattention_kernel(tc, q, k, v_bytes, v_scale, out):
         kv_quantise((1,), right, (1,))
         v_widen(wide0, 1, ROWS, VECTOR)
         out_banks(left, range(SLOTS), 1, 2)
-        q_turn(1, 1, (1,))
         for i in (2, 3):
             q_turn(1, i)
         k_interleave(1, 1, 0)
@@ -344,8 +349,8 @@ def tile_efficientattention_kernel(tc, q, k, v_bytes, v_scale, out):
         out_banks(right, range(6), 1, 2)
         for slot in (6, 7):
             out_passes(right, slot, 1)
-        for pair in BOTH:
-            q_quantise(1, pair)
+        for pieces in ((0, 1), (2, 3)):
+            q_quantise(1, pieces)
 
         for G in BOTH:
             kv_banks(BOTH, span0, G, (0, 1))
@@ -402,4 +407,4 @@ def tile_efficientattention_kernel(tc, q, k, v_bytes, v_scale, out):
             for slot in (0, 2, 4, 6):
                 out_passes(span4, slot, 2, (G,))
         for slot, engine in ((0, SCALAR), (2, VECTOR), (4, SCALAR), (6, VECTOR)):
-            out_copy(span4, slot, 2, 4, engine)
+            out_copy(span4, slot, 2, SLOTS, engine)

@@ -329,8 +329,7 @@ def tile_efficientattention_kernel(tc, q, k, v_bytes, v_scale, out):
             k_interleave(1, 0, g)
         kv_quantise((1,), left, (1,))
         k_quantise(1, 0, BOTH)
-        v_widen(wide0, 0, (0,), SCALAR)
-        v_widen(wide0, 0, (1, 2, 3), VECTOR)
+        v_widen(wide0, 0, ROWS, VECTOR)
         for i in (2, 3):
             q_split_words(1, i)
         kv_quantise((1,), right, (1,))
@@ -367,10 +366,10 @@ def tile_efficientattention_kernel(tc, q, k, v_bytes, v_scale, out):
         v_widen(wide1, 0, (2, 3), VECTOR)
         v_quantise(BOTH, span2)
         v_widen(wide1, 1, ROWS, VECTOR)
-        for span in (span3, span4):
-            v_interleave(BOTH, span, wide1)
-        for span in (span3, span4):
-            v_quantise(BOTH, span)
+        for g in BOTH:
+            v_interleave((g,), wide1, wide1)
+        for g in BOTH:
+            v_quantise((g,), wide1)
         out_banks(span0, (0, 2, 4, 6), 2, 4)
         out_banks(span1, (0, 2), 2, 4)
         for slot in (4, 6):

@@ -45,7 +45,7 @@ def tile_efficientattention_kernel(tc, q, k, v_bytes, v_scale, out):
         ident = keep.tile([P, P], F32, name="ident")
         make_identity(nc, ident[:])
         ident_bf = keep.tile([P, P], BF16, name="ident_bf")
-        make_identity(nc, ident_bf[:])
+        nc.scalar.activation(out=ident_bf[:], in_=ident[:], func=COPY)
 
         k_tile, k_raw, v_raw, q_raw, q_split, v_wide = {}, {}, {}, {}, {}, {}
         grouped, quantised, v_at, kv_at = {}, {}, {}, {}

@@ -25,8 +25,8 @@ ROWS = (0, 1, 2, 3)
 FACTOR = 1.0 / S
 SCALAR, VECTOR = True, False
 
-BUFS = {"k_raw": 3, "v_raw": 2, "q_raw1": 3, "q_raw2": 2, "v_wide": 3, "q_split": 2, "res1": 4, "res2": 4,
-        "k_grp": 2, "v_grp": 3, "q_grp": 4, "m_grp": 3, "k_mx": 2, "v_mx": 4, "q_mx": 3, "m_mx": 4}
+BUFS = {"k_raw": 3, "v_raw": 2, "v_rows": 3, "q_raw1": 4, "q_raw2": 1, "v_wide": 3, "q_split": 2, "kv_pairs": 2, "res1": 5, "res2": 4,
+        "k_grp": 2, "v_grp": 3, "q_grp": 3, "m_grp": 3, "k_mx": 2, "v_mx": 4, "q_mx": 3, "m_mx": 4}
 
 
 def tile_efficientattention_kernel(tc, q, k, v_bytes, v_scale, out):
@@ -48,7 +48,7 @@ def tile_efficientattention_kernel(tc, q, k, v_bytes, v_scale, out):
         nc.scalar.activation(out=ident_bf[:], in_=ident[:], func=COPY)
 
         k_tile, k_raw, v_raw, q_raw, q_split, v_wide = {}, {}, {}, {}, {}, {}
-        grouped, quantised, v_at, kv_at = {}, {}, {}, {}
+        grouped, quantised, v_at, kv_at, kv_pairs = {}, {}, {}, {}, {}
         bank, res, res_left = {}, {}, {}
 
         free_banks, held = list(range(8)), {}
@@ -100,7 +100,7 @@ def tile_efficientattention_kernel(tc, q, k, v_bytes, v_scale, out):
             if rows == ROWS:
                 t = raw.tile([P, PACK, E], U8, name="v_raw", bufs=BUFS["v_raw"])
             else:
-                t = raw.tile([P, len(rows), E], U8, name="v_rows%d" % rows[0])
+                t = raw.tile([P, len(rows), E], U8, name="v_rows", bufs=BUFS["v_rows"])
             source = v_bytes[b].rearrange("(g p j) e -> g p j e", p=P, j=PACK)[g]
             nc.sync.dma_start(out=t[:], in_=source[:, rows[0]:rows[-1] + 1, :])
             for n, j in enumerate(rows):
@@ -145,20 +145,20 @@ def tile_efficientattention_kernel(tc, q, k, v_bytes, v_scale, out):
             nc.vector.tensor_copy(out=dst[:].rearrange("p (g c i j) -> p g c j i", g=len(passes), i=4, j=PACK),
                                   in_=v_wide[wide][:, passes[0]:passes[-1] + 1, :, cols].rearrange("p g j (c i) -> p g c j i", i=4))
 
-        def v_interleave_pair(g, span, pair):
-            dst = grouped_tile(("v", (g,), span), UNIT)[:, pair * 2 * PASS:(pair + 1) * 2 * PASS]
+        def v_interleave_rest(span, at):
+            dst = grouped_tile(("v", (0,), span), UNIT)[:, at * PASS:]
             nc.vector.tensor_copy(out=dst.rearrange("p (c i j) -> p c j i", i=4, j=PACK),
-                                  in_=v_wide[span][:, g, :, pair * 2 * P:(pair + 1) * 2 * P].rearrange("p j (c i) -> p c j i", i=4))
+                                  in_=v_wide[span][:, 0, :, at * P:].rearrange("p j (c i) -> p c j i", i=4))
 
-        def v_weave(g, span, pair):
-            x = take_bank(("w", span, pair), [P, 2, P, PACK], BF16)
-            for n in range(2):
-                col = (2 * pair + n) * P
-                nc.tensor.matmul(x[:, n].rearrange("p c j -> p j c"), lhsT=ident_bf[:], rhs=v_wide[span][:, g, :, col:col + P], start=True, stop=True)
+        def v_weave(span, at, tiles):
+            x = take_bank(("w", span, at), [P, tiles, P, PACK], BF16)
+            for n in range(tiles):
+                col = (at + n) * P
+                nc.tensor.matmul(x[:, n].rearrange("p c j -> p j c"), lhsT=ident_bf[:], rhs=v_wide[span][:, 0, :, col:col + P], start=True, stop=True)
 
-        def v_weave_out(g, span, pair):
-            dst = grouped_tile(("v", (g,), span), UNIT)[:, pair * 2 * PASS:(pair + 1) * 2 * PASS]
-            empty_bank(("w", span, pair), dst, bank["w", span, pair][:].rearrange("p n c j -> p (n c j)"), SCALAR)
+        def v_weave_out(span, at, tiles):
+            dst = grouped_tile(("v", (0,), span), UNIT)[:, at * PASS:(at + tiles) * PASS]
+            empty_bank(("w", span, at), dst, bank["w", span, at][:].rearrange("p n c j -> p (n c j)"), SCALAR)
 
         def v_quantise(passes, span):
             b, first, tiles = span
@@ -216,6 +216,23 @@ def tile_efficientattention_kernel(tc, q, k, v_bytes, v_scale, out):
                 kv_passes(span[0], G, c, passes)
                 kv_out(halves, span, G, c, engine)
 
+        def kv_wide_banks(span, G):
+            b, first, tiles = span
+            if span not in kv_pairs:
+                kv_pairs[span] = work.tile([P, 2, 2, PASS], BF16, name="kv_pairs", bufs=BUFS["kv_pairs"])
+            for h in range(2):
+                x = take_bank(("n", span, G, h), [P, 2, tiles * P])
+                for g in BOTH:
+                    for e in range(2):
+                        mx_pass(x[:, e, :], quantised["k", b, G], g * PASS + (2 * h + e) * P, *v_at[b, g, first], tiles * P,
+                                start=(g, e) == (0, 0), stop=(g, e) == (1, 1))
+                empty_bank(("n", span, G, h), kv_pairs[span][:, G, h, :].rearrange("p (n e) -> p n e", e=2), x[:].rearrange("p e n -> p n e"), SCALAR)
+
+        def kv_join(span, G):
+            dst = grouped_tile(("m", BOTH, span), UNIT)[:, G * 2 * PASS:(G + 1) * 2 * PASS].bitcast(F32)
+            nc.vector.tensor_copy(out=dst.rearrange("p (n i h) -> p n h i", i=4, h=2),
+                                  in_=kv_pairs[span][:, G].bitcast(F32).rearrange("p h (n i) -> p n h i", i=4))
+
         def kv_quantise(halves, span, now):
             b, first, tiles = span
             quantise(("m", halves, span), halves.index(now[0]) * tiles * PASS, len(now) * tiles * PASS)
@@ -251,59 +268,69 @@ def tile_efficientattention_kernel(tc, q, k, v_bytes, v_scale, out):
                 out_copy(span, slot, slots, block_slots, SCALAR)
 
         left, right = (0, 0, 4), (0, 4, 4)
-        wide0, span0, span1, span2, wide1, span3, span4 = (1, 0, 4), (1, 0, 2), (1, 2, 2), (1, 4, 2), (1, 6, 2), (1, 6, 1), (1, 7, 1)
+        wide0, span0, span1, span2, span3 = (1, 0, 4), (1, 0, 2), (1, 2, 2), (1, 4, 2), (1, 6, 2)
 
         load_v(0, 0, (0, 1))
         load_v(0, 0, (2, 3))
+        load_v(0, 1, (0, 1))
         load_k(0, 0, (0,))
-        load_v(0, 1)
         load_q(0, (0,))
-        load_q(0, (1,))
-        load_k(0, 1, (0,))
-        load_q(0, (2,))
 
+        nc.vector.tensor_scalar(out=folded_scale[:], in0=row_scale[:], scalar1=FACTOR, scalar2=None, op0=MULT)
         v_widen(right, 0, (0, 1, 2), SCALAR)
         v_widen(left, 0, ROWS, VECTOR)
         v_widen(right, 0, (3,), VECTOR)
-        v_interleave_pair(0, left, 1)
-        nc.vector.tensor_scalar(out=folded_scale[:], in0=row_scale[:], scalar1=FACTOR, scalar2=None, op0=MULT)
-        k_interleave(0, 0, 0)
-        v_interleave_pair(0, right, 1)
-        for span in (left, right):
-            v_weave(0, span, 0)
-        v_weave_out(0, left, 0)
-        v_widen(left, 1, (0,), SCALAR)
-        v_weave_out(0, right, 0)
-        v_widen(left, 1, (1,), SCALAR)
-        v_widen(right, 1, (0, 1), SCALAR)
-        q_turn(0, 0)
+        load_v(0, 1, (2, 3))
+        load_q(0, (1,))
+        load_k(0, 1, (0,))
+        load_q(0, (2,))
         load_k(0, 0, (1,))
         load_q(0, (3,))
+        v_interleave_rest(left, 2)
+        v_interleave_rest(right, 3)
+        v_widen(left, 1, (1,), VECTOR)
+        k_interleave(0, 0, 0)
+        v_widen(left, 1, (0,), SCALAR)
+        v_widen(right, 1, (0,), SCALAR)
+        for span in (left, right):
+            v_weave(span, 0, 2)
+        v_weave_out(left, 0, 2)
+        v_widen(right, 1, (1,), SCALAR)
+        v_weave_out(right, 0, 2)
+        v_widen(left, 1, (2,), SCALAR)
+        v_widen(right, 1, (2,), SCALAR)
+        q_transpose(0, 0, BOTH)
+        v_weave(right, 2, 1)
+        v_weave_out(right, 2, 1)
+        q_out(0, 0, BOTH)
+        v_widen(right, 1, (3,), SCALAR)
+        load_q(1, (0,))
         load_k(0, 1, (1,))
-        load_q(1, (0, 1))
-        load_k(1, 0, BOTH)
         v_quantise((0,), left)
+        v_widen(left, 1, (3,), VECTOR)
         k_quantise(0, 0, (0,))
-        v_widen(left, 1, (2, 3), VECTOR)
-        v_quantise((0,), right)
         v_interleave((1,), left, left)
+        v_quantise((0,), right)
         k_interleave(0, 0, 1)
         v_quantise((1,), left)
         k_quantise(0, 0, (1,))
-        v_widen(right, 1, (2, 3), SCALAR)
-        load_k(1, 1, BOTH)
-        load_v(1, 0)
-        load_q(1, (2, 3))
-        load_v(1, 1)
 
         for i in (1, 2):
             for c in (2 * i - 2, 2 * i - 1):
                 kv_passes(0, 0, c, (0,))
             q_turn(0, i)
+            if i == 1:
+                load_q(1, (1,))
+                load_k(1, 0, BOTH)
+        load_k(1, 1, BOTH)
+        load_v(1, 0)
+        load_q(1, (2, 3))
+        load_v(1, 1)
         for c in (4, 5):
             kv_passes(0, 0, c, (0,))
         kv_banks((0,), left, 0, range(4), (1,))
         q_turn(0, 3)
+        q_turn(1, 0, (0,))
         v_interleave((1,), right, right)
         k_interleave(0, 1, 0)
         v_quantise((1,), right)
@@ -319,10 +346,10 @@ def tile_efficientattention_kernel(tc, q, k, v_bytes, v_scale, out):
 
         for c in (0, 1):
             kv_passes(0, 1, c, (0,))
-        q_turn(1, 0)
+        q_turn(1, 0, (1,))
+        q_turn(1, 1)
         kv_banks((1,), left, 1, (0, 1), (1,))
         kv_banks((1,), left, 1, (2, 3))
-        q_turn(1, 1)
         kv_banks((1,), right, 1, range(4, 8))
         kv_quantise((0,), right, (0,))
         for g in BOTH:
@@ -338,72 +365,55 @@ def tile_efficientattention_kernel(tc, q, k, v_bytes, v_scale, out):
         for i in (2, 3):
             q_turn(1, i)
         k_interleave(1, 1, 0)
-        v_interleave(BOTH, span0, wide0)
+        for span in (span0, span1):
+            v_interleave(BOTH, span, wide0)
+        for span in (span0, span1):
+            v_quantise(BOTH, span)
         k_interleave(1, 1, 1)
-        v_quantise(BOTH, span0)
-        k_quantise(1, 1, (0,))
-        v_interleave(BOTH, span1, wide0)
-        k_quantise(1, 1, (1,))
-        v_quantise(BOTH, span1)
+        for g in BOTH:
+            k_quantise(1, 1, (g,))
         out_banks(right, range(6), 1, 2)
-        for slot in (6, 7):
-            out_passes(right, slot, 1)
-        for pieces in ((0, 1), (2, 3)):
-            q_quantise(1, pieces)
+        out_passes(right, 6, 1)
 
-        for G in BOTH:
-            kv_banks(BOTH, span0, G, (0, 1))
-        kv_quantise(BOTH, span0, BOTH)
+        for span in (span0, span1):
+            kv_banks(BOTH, span, 0, range(span[1], span[1] + 2))
+        kv_banks(BOTH, span0, 1, (0, 1))
+        out_copy(right, 6, 1, 2, SCALAR)
+        kv_banks(BOTH, span1, 1, (2, 3))
+        out_banks(right, (7,), 1, 2)
+        q_quantise(1, (0, 1))
         for g in BOTH:
             v_widen(span2, g, ROWS, VECTOR)
-        for G in BOTH:
-            kv_banks(BOTH, span1, G, (2, 3))
-        v_widen(wide1, 0, (0, 1), VECTOR)
+        kv_quantise(BOTH, span0, BOTH)
+        q_quantise(1, (2, 3))
         kv_quantise(BOTH, span1, BOTH)
-        for slot in (6, 7):
-            out_copy(right, slot, 1, 2, SCALAR)
         v_interleave(BOTH, span2, span2)
-        v_widen(wide1, 0, (2, 3), VECTOR)
+        v_widen(span3, 0, ROWS, VECTOR)
         v_quantise(BOTH, span2)
-        v_widen(wide1, 1, ROWS, VECTOR)
+        v_widen(span3, 1, ROWS, VECTOR)
         for g in BOTH:
-            v_interleave((g,), wide1, wide1)
+            v_interleave((g,), span3, span3)
         for g in BOTH:
-            v_quantise((g,), wide1)
+            v_quantise((g,), span3)
         out_banks(span0, (0, 2, 4, 6), 2, 4)
-        out_banks(span1, (0, 2), 2, 4)
-        for slot in (4, 6):
-            out_passes(span1, slot, 2)
+        out_banks(span1, (0, 2, 4), 2, 4)
+        out_passes(span1, 6, 2)
 
-        kv_banks(BOTH, span2, 0, (4, 5))
-        kv_quantise(BOTH, span2, (0,))
-        kv_banks(BOTH, span2, 1, (4,))
+        kv_wide_banks(span2, 0)
+        kv_join(span2, 0)
         out_copy(span1, 6, 2, 4, VECTOR)
-        kv_banks(BOTH, span2, 1, (5,))
-        out_copy(span1, 4, 2, 4, SCALAR)
+        kv_quantise(BOTH, span2, (0,))
+        kv_wide_banks(span2, 1)
+        kv_join(span2, 1)
         kv_quantise(BOTH, span2, (1,))
-        kv_banks(BOTH, span3, 0, (6,))
-        kv_banks(BOTH, span3, 1, (6,), engine=VECTOR)
         for G in BOTH:
-            for slot in (0, 2):
-                out_passes(span2, slot, 2, (G,))
-        for slot in (4, 6):
-            out_passes(span2, slot, 2)
-        for slot, engine in ((0, SCALAR), (2, VECTOR), (4, SCALAR)):
-            out_copy(span2, slot, 2, 4, engine)
-        kv_quantise(BOTH, span3, BOTH)
-        out_copy(span2, 6, 2, 4, VECTOR)
-        for G in BOTH:
-            kv_banks(BOTH, span4, G, (7,))
-        kv_quantise(BOTH, span4, (0,))
-        for slot in (0, 2, 4, 6):
-            out_passes(span3, slot, 2)
-        out_copy(span3, 0, 2, 4, VECTOR)
-        kv_quantise(BOTH, span4, (1,))
-        for slot, engine in ((2, SCALAR), (4, SCALAR), (6, VECTOR)):
-            out_copy(span3, slot, 2, 4, engine)
-        for G in BOTH:
-            for slot in (0, 2, 4, 6):
-                out_passes(span4, slot, 2, (G,))
-        for slot, engine in ((0, SCALAR), (2, VECTOR), (4, SCALAR), (6, VECTOR)):
-            out_copy(span4, slot, 2, SLOTS, engine)
+            kv_wide_banks(span3, G)
+            kv_join(span3, G)
+            kv_quantise(BOTH, span3, (G,))
+        for span, slot, engine in ((span2, 0, SCALAR), (span2, 2, SCALAR), (span2, 4, VECTOR), (span2, 6, SCALAR),
+                                   (span3, 0, VECTOR), (span3, 2, SCALAR), (span3, 4, VECTOR)):
+            out_passes(span, slot, 2)
+            out_copy(span, slot, 2, 2, engine)
+        for slot, engine in ((6, SCALAR), (7, VECTOR)):
+            out_passes(span3, slot, 1)
+            out_copy(span3, slot, 1, 2, engine)

@@ -372,19 +372,23 @@ def tile_efficientattention_kernel(tc, q, k, v_bytes, v_scale, out):
         k_interleave(1, 1, 1)
         for g in BOTH:
             k_quantise(1, 1, (g,))
-        out_banks(right, range(6), 1, 2)
-        out_passes(right, 6, 1)
+        out_banks(right, range(4), 1, 2)
+        for slot in (4, 5, 6):
+            out_passes(right, slot, 1)
 
-        for span in (span0, span1):
-            kv_banks(BOTH, span, 0, range(span[1], span[1] + 2))
+        kv_banks(BOTH, span0, 0, (0, 1))
+        out_copy(right, 4, 1, 2, SCALAR)
+        kv_banks(BOTH, span1, 0, (2, 3))
         kv_banks(BOTH, span0, 1, (0, 1))
-        out_copy(right, 6, 1, 2, SCALAR)
+        out_copy(right, 5, 1, 2, SCALAR)
         kv_banks(BOTH, span1, 1, (2, 3))
+        out_copy(right, 6, 1, 2, SCALAR)
         out_banks(right, (7,), 1, 2)
         q_quantise(1, (0, 1))
         for g in BOTH:
             v_widen(span2, g, ROWS, VECTOR)
-        kv_quantise(BOTH, span0, BOTH)
+        for G in BOTH:
+            kv_quantise(BOTH, span0, (G,))
         q_quantise(1, (2, 3))
         kv_quantise(BOTH, span1, BOTH)
         v_interleave(BOTH, span2, span2)
@@ -396,10 +400,12 @@ def tile_efficientattention_kernel(tc, q, k, v_bytes, v_scale, out):
         for g in BOTH:
             v_quantise((g,), span3)
         out_banks(span0, (0, 2, 4, 6), 2, 4)
-        out_banks(span1, (0, 2, 4), 2, 4)
-        out_passes(span1, 6, 2)
+        out_banks(span1, (0, 2), 2, 4)
+        for slot in (4, 6):
+            out_passes(span1, slot, 2)
 
         kv_wide_banks(span2, 0)
+        out_copy(span1, 4, 2, 4, VECTOR)
         kv_join(span2, 0)
         out_copy(span1, 6, 2, 4, VECTOR)
         kv_quantise(BOTH, span2, (0,))

@@ -330,7 +330,6 @@ def tile_efficientattention_kernel(tc, q, k, v_bytes, v_scale, out):
             kv_passes(0, 0, c, (0,))
         kv_banks((0,), left, 0, range(4), (1,))
         q_turn(0, 3)
-        q_turn(1, 0, (0,))
         v_interleave((1,), right, right)
         k_interleave(0, 1, 0)
         v_quantise((1,), right)
@@ -346,10 +345,10 @@ def tile_efficientattention_kernel(tc, q, k, v_bytes, v_scale, out):
 
         for c in (0, 1):
             kv_passes(0, 1, c, (0,))
-        q_turn(1, 0, (1,))
-        q_turn(1, 1)
+        q_turn(1, 0)
         kv_banks((1,), left, 1, (0, 1), (1,))
         kv_banks((1,), left, 1, (2, 3))
+        q_turn(1, 1)
         kv_banks((1,), right, 1, range(4, 8))
         kv_quantise((0,), right, (0,))
         for g in BOTH:
@@ -372,12 +371,11 @@ def tile_efficientattention_kernel(tc, q, k, v_bytes, v_scale, out):
         k_interleave(1, 1, 1)
         for g in BOTH:
             k_quantise(1, 1, (g,))
-        out_banks(right, range(4), 1, 2)
-        for slot in (4, 5, 6):
+        out_banks(right, range(5), 1, 2)
+        for slot in (5, 6):
             out_passes(right, slot, 1)
 
         kv_banks(BOTH, span0, 0, (0, 1))
-        out_copy(right, 4, 1, 2, SCALAR)
         kv_banks(BOTH, span1, 0, (2, 3))
         kv_banks(BOTH, span0, 1, (0, 1))
         out_copy(right, 5, 1, 2, SCALAR)
@@ -389,7 +387,8 @@ def tile_efficientattention_kernel(tc, q, k, v_bytes, v_scale, out):
             v_widen(span2, g, ROWS, VECTOR)
         for G in BOTH:
             kv_quantise(BOTH, span0, (G,))
-        q_quantise(1, (2, 3))
+        for i in (2, 3):
+            q_quantise(1, (i,))
         kv_quantise(BOTH, span1, BOTH)
         v_interleave(BOTH, span2, span2)
         v_widen(span3, 0, ROWS, VECTOR)
@@ -408,10 +407,10 @@ def tile_efficientattention_kernel(tc, q, k, v_bytes, v_scale, out):
         out_copy(span1, 4, 2, 4, VECTOR)
         kv_join(span2, 0)
         out_copy(span1, 6, 2, 4, VECTOR)
-        kv_quantise(BOTH, span2, (0,))
         kv_wide_banks(span2, 1)
         kv_join(span2, 1)
-        kv_quantise(BOTH, span2, (1,))
+        for G in BOTH:
+            kv_quantise(BOTH, span2, (G,))
         for G in BOTH:
             kv_wide_banks(span3, G)
             kv_join(span3, G)

@@ -25,7 +25,7 @@ ROWS = (0, 1, 2, 3)
 FACTOR = 1.0 / S
 SCALAR, VECTOR = True, False
 
-BUFS = {"k_raw": 3, "v_raw": 2, "v_rows": 3, "q_raw1": 4, "q_raw2": 1, "v_wide": 3, "q_split": 2, "kv_pairs": 2, "res1": 5, "res2": 4,
+BUFS = {"k_raw": 3, "v_raw": 2, "v_rows": 3, "q_raw1": 4, "q_raw2": 1, "v_wide": 3, "words": 2, "res1": 8, "res2": 4,
         "k_grp": 2, "v_grp": 3, "q_grp": 3, "m_grp": 3, "k_mx": 2, "v_mx": 4, "q_mx": 3, "m_mx": 4}
 
 
@@ -145,10 +145,13 @@ def tile_efficientattention_kernel(tc, q, k, v_bytes, v_scale, out):
             nc.vector.tensor_copy(out=dst[:].rearrange("p (g c i j) -> p g c j i", g=len(passes), i=4, j=PACK),
                                   in_=v_wide[wide][:, passes[0]:passes[-1] + 1, :, cols].rearrange("p g j (c i) -> p g c j i", i=4))
 
-        def v_interleave_rest(span, at):
-            dst = grouped_tile(("v", (0,), span), UNIT)[:, at * PASS:]
-            nc.vector.tensor_copy(out=dst.rearrange("p (c i j) -> p c j i", i=4, j=PACK),
-                                  in_=v_wide[span][:, 0, :, at * P:].rearrange("p j (c i) -> p c j i", i=4))
+        def v_interleave_part(span, g, at, tiles, engine):
+            dst = grouped_tile(("v", (g,), span), UNIT)[:, at * PASS:(at + tiles) * PASS].rearrange("p (c i j) -> p c j i", i=4, j=PACK)
+            src = v_wide[span][:, g, :, at * P:(at + tiles) * P].rearrange("p j (c i) -> p c j i", i=4)
+            if engine == SCALAR:
+                nc.scalar.copy(out=dst, in_=src)
+            else:
+                nc.vector.tensor_copy(out=dst, in_=src)
 
         def v_weave(span, at, tiles):
             x = take_bank(("w", span, at), [P, tiles, P, PACK], BF16)
@@ -168,7 +171,7 @@ def tile_efficientattention_kernel(tc, q, k, v_bytes, v_scale, out):
                     v_at[b, g, first + a] = (quantised["v", passes, span], (n * tiles + a) * P)
 
         def q_split_words(b, i):
-            t = work.tile([P, 4, 2, P], F32, name="q_split", bufs=BUFS["q_split"])
+            t = work.tile([P, 4, 2, P], F32, name="words", bufs=BUFS["words"])
             nc.vector.tensor_copy(out=t[:].rearrange("p a u (n e) -> p a n u e", e=2),
                                   in_=q_raw[b, i].bitcast(F32).rearrange("p r (G n e u) -> p (r G) n u e", G=2, e=2, u=2))
             q_split[b, i] = t
@@ -219,7 +222,7 @@ def tile_efficientattention_kernel(tc, q, k, v_bytes, v_scale, out):
         def kv_wide_banks(span, G):
             b, first, tiles = span
             if span not in kv_pairs:
-                kv_pairs[span] = work.tile([P, 2, 2, PASS], BF16, name="kv_pairs", bufs=BUFS["kv_pairs"])
+                kv_pairs[span] = work.tile([P, 2, 2, PASS], BF16, name="words", bufs=BUFS["words"])
             for h in range(2):
                 x = take_bank(("n", span, G, h), [P, 2, tiles * P])
                 for g in BOTH:
@@ -253,7 +256,7 @@ def tile_efficientattention_kernel(tc, q, k, v_bytes, v_scale, out):
             b, first, tiles = span
             top = slot - slot % block_slots
             if (span, top) not in res:
-                name = "res%d" % (block_slots * tiles * P // PASS)
+                name = "res%d" % max(1, block_slots * tiles * P // PASS)
                 res[span, top] = work.tile([P, block_slots, tiles * P], F32, name=name, bufs=BUFS[name])
                 res_left[span, top] = block_slots
             empty_bank(("o", span, slot), res[span, top][:, slot - top:slot - top + slots, :], bank["o", span, slot][:], engine)
@@ -286,8 +289,8 @@ def tile_efficientattention_kernel(tc, q, k, v_bytes, v_scale, out):
         load_q(0, (2,))
         load_k(0, 0, (1,))
         load_q(0, (3,))
-        v_interleave_rest(left, 2)
-        v_interleave_rest(right, 3)
+        v_interleave_part(left, 0, 2, 2, VECTOR)
+        v_interleave_part(right, 0, 3, 1, VECTOR)
         v_widen(left, 1, (1,), VECTOR)
         k_interleave(0, 0, 0)
         v_widen(left, 1, (0,), SCALAR)
@@ -322,6 +325,7 @@ def tile_efficientattention_kernel(tc, q, k, v_bytes, v_scale, out):
             if i == 1:
                 load_q(1, (1,))
                 load_k(1, 0, BOTH)
+                v_interleave_part(right, 1, 3, 1, SCALAR)
         load_k(1, 1, BOTH)
         load_v(1, 0)
         load_q(1, (2, 3))
@@ -330,7 +334,7 @@ def tile_efficientattention_kernel(tc, q, k, v_bytes, v_scale, out):
             kv_passes(0, 0, c, (0,))
         kv_banks((0,), left, 0, range(4), (1,))
         q_turn(0, 3)
-        v_interleave((1,), right, right)
+        v_interleave_part(right, 1, 0, 3, VECTOR)
         k_interleave(0, 1, 0)
         v_quantise((1,), right)
         for c in (6, 7):
@@ -415,7 +419,8 @@ def tile_efficientattention_kernel(tc, q, k, v_bytes, v_scale, out):
             kv_wide_banks(span3, G)
             kv_join(span3, G)
             kv_quantise(BOTH, span3, (G,))
-        for span, slot, engine in ((span2, 0, SCALAR), (span2, 2, SCALAR), (span2, 4, VECTOR), (span2, 6, SCALAR),
+        out_banks(span2, (0, 1), 1, 1)
+        for span, slot, engine in ((span2, 2, SCALAR), (span2, 4, VECTOR), (span2, 6, SCALAR),
                                    (span3, 0, VECTOR), (span3, 2, SCALAR), (span3, 4, VECTOR)):
             out_passes(span, slot, 2)
             out_copy(span, slot, 2, 2, engine)

@@ -318,20 +318,19 @@ def tile_efficientattention_kernel(tc, q, k, v_bytes, v_scale, out):
         v_quantise((1,), left)
         k_quantise(0, 0, (1,))
 
-        for i in (1, 2):
-            for c in (2 * i - 2, 2 * i - 1):
-                kv_passes(0, 0, c, (0,))
-            q_turn(0, i)
-            if i == 1:
-                load_q(1, (1,))
-                load_k(1, 0, BOTH)
-                v_interleave_part(right, 1, 3, 1, SCALAR)
+        for c in range(4):
+            kv_passes(0, 0, c, (0,))
+        q_turn(0, 1)
+        v_interleave_part(right, 1, 3, 1, SCALAR)
+        load_q(1, (1,))
+        load_k(1, 0, BOTH)
         load_k(1, 1, BOTH)
         load_v(1, 0)
         load_q(1, (2, 3))
         load_v(1, 1)
         for c in (4, 5):
             kv_passes(0, 0, c, (0,))
+        q_turn(0, 2)
         kv_banks((0,), left, 0, range(4), (1,))
         q_turn(0, 3)
         v_interleave_part(right, 1, 0, 3, VECTOR)

from contextlib import ExitStack

import concourse.mybir as mybir
from concourse.masks import make_identity

B, S, D, E = 2, 1024, 1024, 1024
FLOPS = 2 * B * (D * S * E + S * D * E)

F32 = mybir.dt.float32
BF16 = mybir.dt.bfloat16
U32 = mybir.dt.uint32
U8 = mybir.dt.uint8
FP8 = mybir.dt.float8_e4m3fn
FP8X4 = mybir.dt.float8_e4m3fn_x4
COPY = mybir.ActivationFunctionType.Copy
MULT = mybir.AluOpType.mult

P = 128
PACK = 4
PASS = P * PACK
UNIT = PACK * PASS
SLOTS = S // P
BOTH = (0, 1)
ROWS = (0, 1, 2, 3)
FACTOR = 1.0 / S
SCALAR, VECTOR = True, False

BUFS = {"k_raw": 3, "v_raw": 2, "v_rows": 3, "q_raw1": 4, "q_raw2": 1, "v_wide": 3, "words": 2, "res1": 8, "res2": 4,
        "k_grp": 2, "v_grp": 3, "q_grp": 3, "m_grp": 3, "k_mx": 2, "v_mx": 4, "q_mx": 3, "m_mx": 4}


def tile_efficientattention_kernel(tc, q, k, v_bytes, v_scale, out):
    nc = tc.nc
    with ExitStack() as ctx:
        keep = ctx.enter_context(tc.tile_pool(name="keep", bufs=1))
        raw = ctx.enter_context(tc.tile_pool(name="raw", bufs=1))
        work = ctx.enter_context(tc.tile_pool(name="work", bufs=1))
        mx = ctx.enter_context(tc.tile_pool(name="mx", bufs=1))
        psum = ctx.enter_context(tc.psum_pool(name="psum", bufs=1))
        ctx.enter_context(tc.manual_schedule())

        row_scale = keep.tile([P, 2, PACK], F32, name="row_scale")
        nc.scalar.dma_start(out=row_scale[:], in_=v_scale.rearrange("o (g p j) x -> p (o g) (j x)", p=P, j=PACK))
        folded_scale = keep.tile([P, 2, PACK], F32, name="folded_scale")
        ident = keep.tile([P, P], F32, name="ident")
        make_identity(nc, ident[:])
        ident_bf = keep.tile([P, P], BF16, name="ident_bf")
        nc.scalar.activation(out=ident_bf[:], in_=ident[:], func=COPY)

        k_tile, k_raw, v_raw, q_raw, q_split, v_wide = {}, {}, {}, {}, {}, {}
        grouped, quantised, v_at, kv_at, kv_pairs = {}, {}, {}, {}, {}
        bank, res, res_left = {}, {}, {}

        free_banks, held = list(range(8)), {}

        def take_bank(key, shape, dtype=F32):
            held[key] = free_banks.pop(0)
            bank[key] = psum.tile(shape, dtype, name="bank%d" % held[key])
            return bank[key]

        def empty_bank(key, dst, src, engine):
            if engine == SCALAR:
                nc.scalar.copy(out=dst, in_=src)
            else:
                nc.vector.tensor_copy(out=dst, in_=src)
            free_banks.append(held[key])

        def grouped_tile(key, width):
            if key not in grouped:
                grouped[key] = work.tile([P, width], BF16, name=key[0] + "_grp", align_bytes=64, bufs=BUFS[key[0] + "_grp"])
            return grouped[key]

        def quantise(key, first, width):
            words = grouped[key].shape[1] // PACK
            if key not in quantised:
                codes = mx.tile([P, words], U32, name=key[0] + "_codes", align_bytes=64, bufs=BUFS[key[0] + "_mx"])
                scales = mx.tile([P, words], U8, name=key[0] + "_scales", align_bytes=64, bufs=BUFS[key[0] + "_mx"])
                quantised[key] = (codes, scales)
            codes, scales = quantised[key]
            part = slice(first // PACK, (first + width) // PACK)
            nc.vector.quantize_mx(out=codes[:, part].bitcast(FP8X4), scales=scales[:, part], in_=grouped[key][:, first:first + width])

        def mx_pass(dst, still, still_at, moving, moving_at, width, start, stop):
            m, n = slice(still_at, still_at + P), slice(moving_at, moving_at + width)
            nc.tensor.matmul_mx(out=dst, lhsT=still[0][:, m].bitcast(FP8X4), lhsT_scale=still[1][:, m],
                                rhs=moving[0][:, n].bitcast(FP8X4), rhs_scale=moving[1][:, n], start=start, stop=stop)

        def load_k(b, g, halves):
            key = (b, "pass", g) if halves == BOTH else (b, "half", halves[0])
            if key not in k_tile:
                k_tile[key] = raw.tile([P, 2 * UNIT], BF16, name="k_raw", bufs=BUFS["k_raw"])
            part = k_tile[key][:] if halves == BOTH else k_tile[key][:, g * UNIT:(g + 1) * UNIT]
            t = part.rearrange("p (j d) -> p j d", j=PACK)
            rows = k[b].rearrange("(g p j) d -> g p j d", p=P, j=PACK)[g]
            nc.sync.dma_start(out=t, in_=rows[:, :, halves[0] * PASS:(halves[-1] + 1) * PASS])
            for n, G in enumerate(halves):
                k_raw[b, G, g] = t[:, :, n * PASS:(n + 1) * PASS]

        def load_v(b, g, rows=ROWS):
            if rows == ROWS:
                t = raw.tile([P, PACK, E], U8, name="v_raw", bufs=BUFS["v_raw"])
            else:
                t = raw.tile([P, len(rows), E], U8, name="v_rows", bufs=BUFS["v_rows"])
            source = v_bytes[b].rearrange("(g p j) e -> g p j e", p=P, j=PACK)[g]
            nc.sync.dma_start(out=t[:], in_=source[:, rows[0]:rows[-1] + 1, :])
            for n, j in enumerate(rows):
                v_raw[b, g, j] = t[:, n, :]

        def load_q(b, pieces):
            name = "q_raw%d" % len(pieces)
            t = raw.tile([P, 2 * len(pieces), D], BF16, name=name, bufs=BUFS[name])
            nc.sync.dma_start(out=t[:], in_=q[b].rearrange("(p r) d -> p r d", r=SLOTS)[:, 2 * pieces[0]:2 * pieces[-1] + 2, :])
            for n, i in enumerate(pieces):
                q_raw[b, i] = t[:, 2 * n:2 * n + 2, :]

        def k_interleave(b, G, g):
            dst = grouped_tile(("k", b, G), 2 * UNIT)[:, g * UNIT:(g + 1) * UNIT]
            if (b, g) == (0, 0):
                nc.vector.tensor_scalar(out=dst.rearrange("p (t m j) -> p m j t", t=PACK, j=PACK),
                                        in0=k_raw[b, G, g].rearrange("p j (m t) -> p m j t", t=PACK),
                                        scalar1=FACTOR, scalar2=None, op0=MULT)
            else:
                nc.vector.tensor_copy(out=dst.rearrange("p (t m u e) -> p m u t e", t=PACK, u=2, e=2),
                                      in_=k_raw[b, G, g].rearrange("p (u e) (m t) -> p m u t e", t=PACK, e=2))

        def k_quantise(b, G, passes):
            quantise(("k", b, G), passes[0] * UNIT, len(passes) * UNIT)

        def v_widen(span, g, rows, engine):
            b, first, tiles = span
            if span not in v_wide:
                v_wide[span] = work.tile([P, 2, PACK, tiles * P], BF16, name="v_wide", bufs=BUFS["v_wide"])
            scales = row_scale if (b, g) == (0, 0) else folded_scale
            for j in rows:
                dst, src = v_wide[span][:, g, j, :], v_raw[b, g, j][:, first * P:(first + tiles) * P].bitcast(FP8)
                if engine == SCALAR:
                    nc.scalar.activation(out=dst, in_=src, func=COPY, scale=scales[:, g, j:j + 1])
                else:
                    nc.vector.tensor_scalar(out=dst, in0=src, scalar1=scales[:, g, j:j + 1], scalar2=None, op0=MULT)

        def v_interleave(passes, span, wide):
            b, first, tiles = span
            dst = grouped_tile(("v", passes, span), len(passes) * tiles * PASS)
            cols = slice((first - wide[1]) * P, (first - wide[1] + tiles) * P)
            nc.vector.tensor_copy(out=dst[:].rearrange("p (g c i j) -> p g c j i", g=len(passes), i=4, j=PACK),
                                  in_=v_wide[wide][:, passes[0]:passes[-1] + 1, :, cols].rearrange("p g j (c i) -> p g c j i", i=4))

        def v_interleave_part(span, g, at, tiles, engine):
            dst = grouped_tile(("v", (g,), span), UNIT)[:, at * PASS:(at + tiles) * PASS].rearrange("p (c i j) -> p c j i", i=4, j=PACK)
            src = v_wide[span][:, g, :, at * P:(at + tiles) * P].rearrange("p j (c i) -> p c j i", i=4)
            if engine == SCALAR:
                nc.scalar.copy(out=dst, in_=src)
            else:
                nc.vector.tensor_copy(out=dst, in_=src)

        def v_weave(span, at, tiles):
            x = take_bank(("w", span, at), [P, tiles, P, PACK], BF16)
            for n in range(tiles):
                col = (at + n) * P
                nc.tensor.matmul(x[:, n].rearrange("p c j -> p j c"), lhsT=ident_bf[:], rhs=v_wide[span][:, 0, :, col:col + P], start=True, stop=True)

        def v_weave_out(span, at, tiles):
            dst = grouped_tile(("v", (0,), span), UNIT)[:, at * PASS:(at + tiles) * PASS]
            empty_bank(("w", span, at), dst, bank["w", span, at][:].rearrange("p n c j -> p (n c j)"), SCALAR)

        def v_quantise(passes, span):
            b, first, tiles = span
            quantise(("v", passes, span), 0, len(passes) * tiles * PASS)
            for n, g in enumerate(passes):
                for a in range(tiles):
                    v_at[b, g, first + a] = (quantised["v", passes, span], (n * tiles + a) * P)

        def q_split_words(b, i):
            t = work.tile([P, 4, 2, P], F32, name="words", bufs=BUFS["words"])
            nc.vector.tensor_copy(out=t[:].rearrange("p a u (n e) -> p a n u e", e=2),
                                  in_=q_raw[b, i].bitcast(F32).rearrange("p r (G n e u) -> p (r G) n u e", G=2, e=2, u=2))
            q_split[b, i] = t

        def q_transpose(b, i, halves):
            for G in halves:
                x = take_bank(("q", b, i, G), [P, 2, 2, P])
                for r in range(2):
                    for u in range(2):
                        if (b, i) in q_split:
                            src = q_split[b, i][:, 2 * r + G, u]
                        else:
                            src = q_raw[b, i][:, r, :].bitcast(F32)[:, 256 * G + u:256 * (G + 1):2]
                        nc.tensor.transpose(x[:, r, u, :], src, ident[:])

        def q_out(b, i, halves):
            for G in halves:
                at = (i % 2) * UNIT + G * 2 * PASS
                dst = grouped_tile(("q", b, i // 2), 2 * UNIT)[:, at:at + 2 * PASS].bitcast(F32).rearrange("p (r n u) -> p r n u", r=2, u=2)
                empty_bank(("q", b, i, G), dst, bank["q", b, i, G][:].rearrange("p r u n -> p r n u"), SCALAR)

        def q_turn(b, i, halves=BOTH):
            q_transpose(b, i, halves)
            q_out(b, i, halves)

        def q_quantise(b, pieces):
            quantise(("q", b, pieces[0] // 2), (pieces[0] % 2) * UNIT, len(pieces) * UNIT)

        def kv_passes(b, G, c, passes):
            for g in passes:
                if g == 0:
                    take_bank(("m", b, G, c), [P, PACK, P])
                for t in range(PACK):
                    mx_pass(bank["m", b, G, c][:, t, :], quantised["k", b, G], g * PASS + t * P, *v_at[b, g, c], P,
                            start=(g, t) == (0, 0), stop=(g, t) == (1, PACK - 1))

        def kv_out(halves, span, G, c, engine):
            b, first, tiles = span
            at = (halves.index(G) * tiles + c - first) * PASS
            dst = grouped_tile(("m", halves, span), len(halves) * tiles * PASS)[:, at:at + PASS].rearrange("p (n t) -> p n t", t=PACK)
            empty_bank(("m", b, G, c), dst, bank["m", b, G, c][:].rearrange("p t n -> p n t"), engine)

        def kv_banks(halves, span, G, tiles, passes=BOTH, engine=SCALAR):
            for c in tiles:
                kv_passes(span[0], G, c, passes)
                kv_out(halves, span, G, c, engine)

        def kv_wide_banks(span, G):
            b, first, tiles = span
            if span not in kv_pairs:
                kv_pairs[span] = work.tile([P, 2, 2, PASS], BF16, name="words", bufs=BUFS["words"])
            for h in range(2):
                x = take_bank(("n", span, G, h), [P, 2, tiles * P])
                for g in BOTH:
                    for e in range(2):
                        mx_pass(x[:, e, :], quantised["k", b, G], g * PASS + (2 * h + e) * P, *v_at[b, g, first], tiles * P,
                                start=(g, e) == (0, 0), stop=(g, e) == (1, 1))
                empty_bank(("n", span, G, h), kv_pairs[span][:, G, h, :].rearrange("p (n e) -> p n e", e=2), x[:].rearrange("p e n -> p n e"), SCALAR)

        def kv_join(span, G):
            dst = grouped_tile(("m", BOTH, span), UNIT)[:, G * 2 * PASS:(G + 1) * 2 * PASS].bitcast(F32)
            nc.vector.tensor_copy(out=dst.rearrange("p (n i h) -> p n h i", i=4, h=2),
                                  in_=kv_pairs[span][:, G].bitcast(F32).rearrange("p h (n i) -> p n h i", i=4))

        def kv_quantise(halves, span, now):
            b, first, tiles = span
            quantise(("m", halves, span), halves.index(now[0]) * tiles * PASS, len(now) * tiles * PASS)
            for G in now:
                kv_at[span, G] = (quantised["m", halves, span], halves.index(G) * tiles * P)

        def out_passes(span, slot, slots, halves=BOTH):
            b, first, tiles = span
            if halves[0] == 0:
                take_bank(("o", span, slot), [P, slots, tiles * P])
            for r in range(slots):
                for G in halves:
                    at = ((slot + r) // 2 % 2) * PASS + G * 2 * P + ((slot + r) % 2) * P
                    mx_pass(bank["o", span, slot][:, r, :], quantised["q", b, (slot + r) // 4], at, *kv_at[span, G], tiles * P,
                            start=(r, G) == (0, 0), stop=(r, G) == (slots - 1, 1))

        def out_copy(span, slot, slots, block_slots, engine):
            b, first, tiles = span
            top = slot - slot % block_slots
            if (span, top) not in res:
                name = "res%d" % max(1, block_slots * tiles * P // PASS)
                res[span, top] = work.tile([P, block_slots, tiles * P], F32, name=name, bufs=BUFS[name])
                res_left[span, top] = block_slots
            empty_bank(("o", span, slot), res[span, top][:, slot - top:slot - top + slots, :], bank["o", span, slot][:], engine)
            res_left[span, top] = res_left[span, top] - slots
            if res_left[span, top] == 0:
                rows_out = out[b].rearrange("(p r) e -> p r e", r=SLOTS)
                nc.sync.dma_start(out=rows_out[:, top:top + block_slots, first * P:(first + tiles) * P], in_=res[span, top][:])

        def out_banks(span, first_slots, slots, block_slots):
            for slot in first_slots:
                out_passes(span, slot, slots)
                out_copy(span, slot, slots, block_slots, SCALAR)

        left, right = (0, 0, 4), (0, 4, 4)
        wide0, span0, span1, span2, span3 = (1, 0, 4), (1, 0, 2), (1, 2, 2), (1, 4, 2), (1, 6, 2)

        load_v(0, 0, (0, 1))
        load_v(0, 0, (2, 3))
        load_v(0, 1, (0, 1))
        load_k(0, 0, (0,))
        load_q(0, (0,))

        nc.vector.tensor_scalar(out=folded_scale[:], in0=row_scale[:], scalar1=FACTOR, scalar2=None, op0=MULT)
        v_widen(right, 0, (0, 1, 2), SCALAR)
        v_widen(left, 0, ROWS, VECTOR)
        v_widen(right, 0, (3,), VECTOR)
        load_v(0, 1, (2, 3))
        load_q(0, (1,))
        load_k(0, 1, (0,))
        load_q(0, (2,))
        load_k(0, 0, (1,))
        load_q(0, (3,))
        v_interleave_part(left, 0, 2, 2, VECTOR)
        v_interleave_part(right, 0, 3, 1, VECTOR)
        v_widen(left, 1, (1,), VECTOR)
        k_interleave(0, 0, 0)
        v_widen(left, 1, (0,), SCALAR)
        v_widen(right, 1, (0,), SCALAR)
        for span in (left, right):
            v_weave(span, 0, 2)
        v_weave_out(left, 0, 2)
        v_widen(right, 1, (1,), SCALAR)
        v_weave_out(right, 0, 2)
        v_widen(left, 1, (2,), SCALAR)
        v_widen(right, 1, (2,), SCALAR)
        q_transpose(0, 0, BOTH)
        v_weave(right, 2, 1)
        v_weave_out(right, 2, 1)
        q_out(0, 0, BOTH)
        v_widen(right, 1, (3,), SCALAR)
        load_q(1, (0,))
        load_k(0, 1, (1,))
        v_quantise((0,), left)
        v_widen(left, 1, (3,), VECTOR)
        k_quantise(0, 0, (0,))
        v_interleave((1,), left, left)
        v_quantise((0,), right)
        k_interleave(0, 0, 1)
        v_quantise((1,), left)
        k_quantise(0, 0, (1,))

        for c in range(4):
            kv_passes(0, 0, c, (0,))
        q_turn(0, 1)
        v_interleave_part(right, 1, 3, 1, SCALAR)
        load_q(1, (1,))
        load_k(1, 0, BOTH)
        load_k(1, 1, BOTH)
        load_v(1, 0)
        load_q(1, (2, 3))
        load_v(1, 1)
        for c in (4, 5):
            kv_passes(0, 0, c, (0,))
        q_turn(0, 2)
        kv_banks((0,), left, 0, range(4), (1,))
        q_turn(0, 3)
        v_interleave_part(right, 1, 0, 3, VECTOR)
        k_interleave(0, 1, 0)
        v_quantise((1,), right)
        for c in (6, 7):
            kv_passes(0, 0, c, (0,))
        kv_banks((0,), right, 0, range(4, 8), (1,))
        k_quantise(0, 1, (0,))
        k_interleave(0, 1, 1)
        kv_quantise((0,), left, (0,))
        k_quantise(0, 1, (1,))
        for pieces in ((0, 1), (2, 3)):
            q_quantise(0, pieces)

        for c in (0, 1):
            kv_passes(0, 1, c, (0,))
        q_turn(1, 0)
        kv_banks((1,), left, 1, (0, 1), (1,))
        kv_banks((1,), left, 1, (2, 3))
        q_turn(1, 1)
        kv_banks((1,), right, 1, range(4, 8))
        kv_quantise((0,), right, (0,))
        for g in BOTH:
            k_interleave(1, 0, g)
        kv_quantise((1,), left, (1,))
        k_quantise(1, 0, BOTH)
        v_widen(wide0, 0, ROWS, VECTOR)
        for i in (2, 3):
            q_split_words(1, i)
        kv_quantise((1,), right, (1,))
        v_widen(wide0, 1, ROWS, VECTOR)
        out_banks(left, range(SLOTS), 1, 2)
        for i in (2, 3):
            q_turn(1, i)
        k_interleave(1, 1, 0)
        for span in (span0, span1):
            v_interleave(BOTH, span, wide0)
        for span in (span0, span1):
            v_quantise(BOTH, span)
        k_interleave(1, 1, 1)
        for g in BOTH:
            k_quantise(1, 1, (g,))
        out_banks(right, range(5), 1, 2)
        for slot in (5, 6):
            out_passes(right, slot, 1)

        kv_banks(BOTH, span0, 0, (0, 1))
        kv_banks(BOTH, span1, 0, (2, 3))
        kv_banks(BOTH, span0, 1, (0, 1))
        out_copy(right, 5, 1, 2, SCALAR)
        kv_banks(BOTH, span1, 1, (2, 3))
        out_copy(right, 6, 1, 2, SCALAR)
        out_banks(right, (7,), 1, 2)
        q_quantise(1, (0, 1))
        for g in BOTH:
            v_widen(span2, g, ROWS, VECTOR)
        for G in BOTH:
            kv_quantise(BOTH, span0, (G,))
        for i in (2, 3):
            q_quantise(1, (i,))
        kv_quantise(BOTH, span1, BOTH)
        v_interleave(BOTH, span2, span2)
        v_widen(span3, 0, ROWS, VECTOR)
        v_quantise(BOTH, span2)
        v_widen(span3, 1, ROWS, VECTOR)
        for g in BOTH:
            v_interleave((g,), span3, span3)
        for g in BOTH:
            v_quantise((g,), span3)
        out_banks(span0, (0, 2, 4, 6), 2, 4)
        out_banks(span1, (0, 2), 2, 4)
        for slot in (4, 6):
            out_passes(span1, slot, 2)

        kv_wide_banks(span2, 0)
        out_copy(span1, 4, 2, 4, VECTOR)
        kv_join(span2, 0)
        out_copy(span1, 6, 2, 4, VECTOR)
        kv_wide_banks(span2, 1)
        kv_join(span2, 1)
        for G in BOTH:
            kv_quantise(BOTH, span2, (G,))
        for G in BOTH:
            kv_wide_banks(span3, G)
            kv_join(span3, G)
            kv_quantise(BOTH, span3, (G,))
        out_banks(span2, (0, 1), 1, 1)
        for span, slot, engine in ((span2, 2, SCALAR), (span2, 4, VECTOR), (span2, 6, SCALAR),
                                   (span3, 0, VECTOR), (span3, 2, SCALAR), (span3, 4, VECTOR)):
            out_passes(span, slot, 2)
            out_copy(span, slot, 2, 2, engine)
        for slot, engine in ((6, SCALAR), (7, VECTOR)):
            out_passes(span3, slot, 1)
            out_copy(span3, slot, 1, 2, engine)
